import numpy as np
import ml_dtypes


def mxq(x, axis, fmt="e4m3"):
    dtype, down = {"e4m3": (ml_dtypes.float8_e4m3fn, 7), "e5m2": (ml_dtypes.float8_e5m2, 14)}[fmt]
    v = np.moveaxis(np.asarray(x, np.float32).astype(ml_dtypes.bfloat16).astype(np.float64), axis, -1)
    blocks = v.reshape(v.shape[:-1] + (-1, 32))
    amax = np.abs(blocks).max(-1, keepdims=True)
    byte = np.maximum(np.where(amax > 0, np.frexp(amax)[1] - 1 + 127, 0) - down, 1)
    scale = np.exp2(byte - 127.0)
    codes = (blocks / scale).astype(np.float32).astype(dtype).astype(np.float64)
    return np.moveaxis((codes * scale).reshape(v.shape), -1, axis)


WIDE = False


def mx_kscale(k):
    if not WIDE:
        return np.ones(k)
    levels = np.array([18, -18])
    if k % 512:
        return np.exp2(np.random.permutation(np.resize(levels, k // 32))).repeat(32)
    a = np.empty((k // 512, 16))
    for p in range(k // 512):
        a[p, :8] = np.random.permutation(np.resize(levels, 8))
        for g in range(8):
            far = levels[np.abs(levels - a[p, g]) >= 10]
            a[p, g + 8] = far[np.random.randint(len(far))]
    return np.exp2(a.ravel()).repeat(32)


BF16 = ml_dtypes.bfloat16


def bf(x):
    return np.asarray(x, np.float32).astype(BF16)


def f64(x):
    return np.asarray(x).astype(np.float64)


N, NK, D_IN, D_H, D_V = 1024, 1024, 512, 512, 512


def softmax_rows(sc):
    e = np.exp(sc - sc.max(-1, keepdims=True))
    return e / e.sum(-1, keepdims=True)


def setup_inputs():
    u = mx_kscale(N)
    v = mx_kscale(D_V)
    s = mx_kscale(NK)
    uu = u / np.min(u)
    ss = s / np.min(s)
    vv = v / np.max(v)
    c = np.min(s)
    q = bf(np.random.standard_normal((N, D_H)) * 1.4)
    k = bf(np.random.standard_normal((N, D_H)) * 1.4)
    h0 = bf(np.random.standard_normal((N, D_H)) * 1.1)
    cooccur0 = bf(np.random.standard_normal((N, N)) * 0.5 / np.sqrt(N))
    wv0 = bf(np.random.standard_normal((D_H, D_H)) * 2.7 / np.sqrt(D_H))
    bv = bf(np.random.standard_normal(D_H) * 0.3)
    p = softmax_rows(f64(q) @ f64(k).T / np.sqrt(D_H))
    y = (p + f64(cooccur0)) @ (f64(h0) @ f64(wv0).T + f64(bv))
    g = bf(np.random.standard_normal((N, D_V)) * np.exp2(np.random.randint(-6, 1, (N, 1))) / uu[:, None] * vv[None, :] * c)
    return {
        "q": q,
        "k": k,
        "h": bf(f64(h0) / ss[:, None]),
        "cooccur": bf(f64(cooccur0) * uu[:, None] * ss[None, :]),
        "wv": bf(f64(wv0) / vv[:, None]),
        "bv": bv,
        "p": np.asarray(p, np.float32),
        "y": np.asarray(y, np.float32),
        "grad_out": g,
    }


def reference(q, k, h, cooccur, wv, bv, p, y, grad_out):
    g = f64(grad_out)
    dz2 = g * (f64(y) > 0.0)
    att = f64(p) + f64(cooccur)
    dz1 = mxq(att, 0, "e4m3").T @ mxq(dz2, 0, "e5m2")
    dh = (mxq(dz1, 1, "e5m2") @ mxq(f64(wv), 0, "e4m3")) + g
    dwv = mxq(dz1, 0, "e5m2").T @ mxq(f64(h), 0, "e4m3")
    return dh, dwv

@@ -1,0 +1,292 @@
+from contextlib import ExitStack
+
+import concourse.mybir as mybir
+from concourse.masks import make_identity
+
+N = 1024
+D = 512
+P = 128
+J = 4
+G = 512
+
+F32 = mybir.dt.float32
+BF16 = mybir.dt.bfloat16
+U32 = mybir.dt.uint32
+U8 = mybir.dt.uint8
+E4M3 = mybir.dt.float8_e4m3fn_x4
+E5M2 = mybir.dt.float8_e5m2_x4
+ALU = mybir.AluOpType
+
+FLOPS = 2 * N * N * D + 2 * 2 * N * D * D
+BYTES = N * D * 2 * 2 + N * N * 2 + D * D * 2 + N * N * 4 + N * D * 4 + N * D * 4 + D * D * 4
+
+
+def tile_semanticgraph_pb_v_kernel(tc, q, k, h, cooccur, wv, bv, p, y, grad_out, out_0, out_1):
+    nc = tc.nc
+    with ExitStack() as ctx:
+        keep = ctx.enter_context(tc.tile_pool(name="keep", bufs=1))
+        psum = ctx.enter_context(tc.psum_pool(name="psum", bufs=1))
+
+        def sb(shape, dtype, name):
+            return keep.tile(shape, dtype, name=name, align_bytes=64)
+
+        def bank(shape, name):
+            return psum.tile(shape, F32, name=name)
+
+        ctx.enter_context(tc.manual_schedule())
+
+        def load(ap, shape, dtype, name):
+            t = sb(shape, dtype, name)
+            nc.sync.dma_start(out=t[:], in_=ap)
+            return t
+
+        def rows(ap, i, c0, c1):
+            return ap[G * i : G * (i + 1), c0:c1].rearrange("(p j) w -> p j w", j=J)
+
+        def load_p(i, hf):
+            return load(rows(p, i, G * hf, G * (hf + 1)), [P, J, G], F32, f"p_{i}{hf}")
+
+        def load_c(i, hf):
+            return load(rows(cooccur, i, G * hf, G * (hf + 1)), [P, J, G], BF16, f"c_{i}{hf}")[:]
+
+        g_raw, y_raw, p_raw, c_raw = {}, {}, {}, {}
+        h_raw = {}
+        y_raw[0] = load(rows(y, 0, 0, D), [P, J, D], F32, "y_0")
+        g_raw[0] = load(rows(grad_out, 0, 0, D), [P, J, D], BF16, "g_0")
+        c_raw[0, 0] = load_c(0, 0)
+        p_raw[0, 0] = load_p(0, 0)
+        y_raw[1] = load(rows(y, 1, 0, D), [P, J, D], F32, "y_1")
+        g_raw[1] = load(rows(grad_out, 1, 0, D), [P, J, D], BF16, "g_1")
+        c_raw[1, 0] = load_c(1, 0)
+        p_raw[1, 0] = load_p(1, 0)
+        wv_raw = load(rows(wv, 0, 0, D), [P, J, D], BF16, "wv_raw")
+        c_raw[0, 1] = load_c(0, 1)
+        p_raw[0, 1] = load_p(0, 1)
+        c_raw[1, 1] = load_c(1, 1)
+        p_raw[1, 1] = load_p(1, 1)
+        h_raw[0] = load(rows(h, 0, 0, D), [P, J, D], BF16, "h_raw0")
+        h_raw[1] = load(rows(h, 1, 0, D), [P, J, D], BF16, "h_raw1")
+
+        ident = sb([P, P], F32, "ident")
+        make_identity(nc, ident[:])
+
+        def operand(width, name):
+            return (sb([P, width], U32, name + "_codes"), sb([P, width], U8, name + "_scales"))
+
+        def quantize(op, fmt, grouped, c0, c1):
+            codes, scales = op
+            nc.vector.quantize_mx(
+                out=codes[:, c0:c1].bitcast(fmt), scales=scales[:, c0:c1], in_=grouped[:, J * c0 : J * c1]
+            )
+
+        dz2 = [sb([P, J, D], BF16, f"dz2_{i}") for i in range(2)]
+        dz2_g = [sb([P, D * J], BF16, f"dz2_g{i}") for i in range(2)]
+        dz2_q = [operand(D, f"dz2_q{i}") for i in range(2)]
+        att_g = {(i, hf): sb([P, G * J], BF16, f"att_g{i}{hf}") for i in range(2) for hf in range(2)}
+        att_q = {(i, hf): operand(G, f"att_q{i}{hf}") for i in range(2) for hf in range(2)}
+        wv_g = sb([P, D * J], BF16, "wv_g")
+        wv_q = operand(D, "wv_q")
+        h_g = [sb([P, D * J], BF16, f"h_g{i}") for i in range(2)]
+        h_q = [operand(D, f"h_q{i}") for i in range(2)]
+        dz1 = [sb([P, J, D], BF16, f"dz1_{hf}") for hf in range(2)]
+        dk_g = [sb([P, G * J], BF16, f"dk_g{hf}") for hf in range(2)]
+        dk_q = [operand(G, f"dk_q{hf}") for hf in range(2)]
+        dv_g = [sb([P, D * J], BF16, f"dv_g{hf}") for hf in range(2)]
+        dv_q = [operand(D, f"dv_q{hf}") for hf in range(2)]
+        o0 = [sb([P, J, D], F32, f"o0_{hf}") for hf in range(2)]
+        o1 = sb([P, J, D], F32, "o1")
+
+        def relu_grad(i, yt, c0, c1):
+            nc.vector.scalar_tensor_tensor(
+                out=dz2[i][:, :, c0:c1],
+                in0=yt,
+                scalar=0.0,
+                in1=g_raw[i][:, :, c0:c1],
+                op0=ALU.is_gt,
+                op1=ALU.mult,
+            )
+
+
+        def add_att(i, hf, m0, m1):
+            nc.vector.tensor_tensor(
+                out=att_g[i, hf][:].rearrange("p (t m j) -> p m j t", t=4, j=J)[:, m0:m1],
+                in0=p_raw[i, hf][:].rearrange("p j (m t) -> p m j t", t=4)[:, m0:m1],
+                in1=c_raw[i, hf].rearrange("p j (m t) -> p m j t", t=4)[:, m0:m1],
+                op=ALU.add,
+            )
+
+        def interleave(engine_copy, dst, src, c0, c1):
+            engine_copy(
+                out=dst[:, J * c0 : J * c1].rearrange("p (c i j) -> p c j i", i=4, j=J),
+                in_=src[:, :, c0:c1].rearrange("p j (c i) -> p c j i", i=4),
+            )
+
+        def mm(out, a, a_fmt, a0, b, b_fmt, start, stop):
+            nc.tensor.matmul_mx(
+                out=out,
+                lhsT=a[0][:, a0 : a0 + P].bitcast(a_fmt),
+                lhsT_scale=a[1][:, a0 : a0 + P],
+                rhs=b[0][:].bitcast(b_fmt),
+                rhs_scale=b[1][:],
+                start=start,
+                stop=stop,
+            )
+
+        acc = {}
+
+        def stage1(hf, i, ts):
+            for t in ts:
+                if i == 0:
+                    acc[hf, t] = bank([P, D], f"acc{t}")
+                mm(acc[hf, t][:], att_q[i, hf], E4M3, P * t, dz2_q[i], E5M2, i == 0, i == 1)
+
+        def evac1(copy, hf, t):
+            copy(out=dz1[hf][:, t, :], in_=acc[hf, t][:])
+
+        tb = {}
+
+        def turn(hf, b):
+            tb[hf, b] = bank([P, 2, 2, P], f"turn{b}")
+            for a in range(2):
+                words = dz1[hf][:, 2 * b + a, :].bitcast(F32)
+                for u in range(2):
+                    nc.tensor.transpose(tb[hf, b][:, a, u, :], words[:, u::2], ident[:])
+
+        def turn_out(hf, b):
+            nc.scalar.copy(
+                out=dk_g[hf][:, 2 * P * J * b : 2 * P * J * (b + 1)].bitcast(F32).rearrange("p (a r u) -> p a r u", a=2, u=2),
+                in_=tb[hf, b][:].rearrange("p a u r -> p a r u"),
+            )
+
+        ob = {}
+
+        def stage2a(hf, t):
+            ob[hf, t] = bank([P, D], f"turn{t - 2}" if (hf, t // 2) == (1, 1) else f"ob{t % 2}")
+            mm(ob[hf, t][:], dk_q[hf], E5M2, P * t, wv_q, E4M3, True, True)
+
+        def evac2a(hf, t):
+            nc.vector.tensor_tensor(out=o0[hf][:, t, :], in0=ob[hf, t][:], in1=g_raw[hf][:, t, :], op=ALU.add)
+
+        def store_out0(hf, t0, t1):
+            nc.sync.dma_start(out=rows(out_0, hf, 0, D)[:, t0:t1, :], in_=o0[hf][:, t0:t1, :])
+
+        vcopy, scopy = nc.vector.tensor_copy, nc.scalar.copy
+        wb = {}
+
+        def stage2b(c, i):
+            if i == 0:
+                wb[c] = bank([P, D], f"acc{c}")
+            mm(wb[c][:], dv_q[i], E5M2, P * c, h_q[i], E4M3, i == 0, i == 1)
+
+        def evac2b(copy, c):
+            copy(out=o1[:, c, :], in_=wb[c][:])
+
+        def store_out1(c):
+            nc.sync.dma_start(out=out_1[P * c : P * (c + 1), :], in_=o1[:, c, :])
+
+        relu_grad(0, y_raw[0][:, :, 0:256], 0, 256)
+        interleave(scopy, dz2_g[0], dz2[0], 0, 256)
+        relu_grad(0, y_raw[0][:, :, 256:512], 256, 512)
+        interleave(scopy, dz2_g[0], dz2[0], 256, 512)
+        add_att(0, 0, 0, P)
+        quantize(dz2_q[0], E5M2, dz2_g[0], 0, D)
+        quantize(att_q[0, 0], E4M3, att_g[0, 0], 0, G)
+        stage1(0, 0, [0])
+        stage1(0, 0, [1])
+        stage1(0, 0, [2])
+        stage1(0, 0, [3])
+        relu_grad(1, y_raw[1][:, :, 0:256], 0, 256)
+        interleave(scopy, dz2_g[1], dz2[1], 0, 256)
+        relu_grad(1, y_raw[1][:, :, 256:512], 256, 512)
+        interleave(scopy, dz2_g[1], dz2[1], 256, 512)
+        add_att(1, 0, 0, P)
+        quantize(dz2_q[1], E5M2, dz2_g[1], 0, D)
+        quantize(att_q[1, 0], E4M3, att_g[1, 0], 0, G)
+        stage1(0, 1, [0])
+        stage1(0, 1, [1])
+        stage1(0, 1, [2])
+        stage1(0, 1, [3])
+        interleave(scopy, wv_g, wv_raw, 0, D)
+        quantize(wv_q, E4M3, wv_g, 0, D)
+        evac1(scopy, 0, 0)
+        evac1(scopy, 0, 1)
+        turn(0, 0)
+        evac1(scopy, 0, 2)
+        evac1(scopy, 0, 3)
+        turn(0, 1)
+        turn_out(0, 0)
+        add_att(0, 1, 0, P)
+        interleave(scopy, dv_g[0], dz1[0], 0, D)
+        turn_out(0, 1)
+        quantize(att_q[0, 1], E4M3, att_g[0, 1], 0, G)
+        stage1(1, 0, [0])
+        stage1(1, 0, [1])
+        stage1(1, 0, [2])
+        stage1(1, 0, [3])
+        quantize(dk_q[0], E5M2, dk_g[0], 0, 256)
+        stage2a(0, 0)
+        stage2a(0, 1)
+        interleave(scopy, h_g[1], h_raw[1], 0, D)
+        add_att(1, 1, 0, P)
+        quantize(dk_q[0], E5M2, dk_g[0], 256, 512)
+        quantize(att_q[1, 1], E4M3, att_g[1, 1], 0, 256)
+        stage1(1, 1, [0])
+        stage1(1, 1, [1])
+        quantize(att_q[1, 1], E4M3, att_g[1, 1], 256, 512)
+        stage1(1, 1, [2])
+        stage1(1, 1, [3])
+        evac1(scopy, 1, 0)
+        evac1(scopy, 1, 1)
+        evac1(scopy, 1, 2)
+        evac1(scopy, 1, 3)
+        interleave(vcopy, h_g[0], h_raw[0], 0, D)
+        quantize(dv_q[0], E5M2, dv_g[0], 0, D)
+        quantize(h_q[0], E4M3, h_g[0], 0, D)
+        turn(1, 0)
+        evac2a(0, 0)
+        evac2a(0, 1)
+        store_out0(0, 0, 2)
+        stage2a(0, 2)
+        stage2a(0, 3)
+        turn_out(1, 0)
+        turn(1, 1)
+        stage2b(0, 0)
+        stage2b(1, 0)
+        quantize(h_q[1], E4M3, h_g[1], 0, D)
+        evac2a(0, 2)
+        store_out0(0, 2, 3)
+        quantize(dk_q[1], E5M2, dk_g[1], 0, 256)
+        interleave(scopy, dv_g[1], dz1[1], 0, 256)
+        stage2a(1, 0)
+        evac2a(0, 3)
+        store_out0(0, 3, 4)
+        stage2a(1, 1)
+        turn_out(1, 1)
+        quantize(dv_q[1], E5M2, dv_g[1], 0, 256)
+        evac2a(1, 0)
+        store_out0(1, 0, 1)
+        stage2b(0, 1)
+        stage2b(1, 1)
+        stage2b(2, 0)
+        stage2b(3, 0)
+        interleave(scopy, dv_g[1], dz1[1], 256, 512)
+        evac2a(1, 1)
+        store_out0(1, 1, 2)
+        quantize(dv_q[1], E5M2, dv_g[1], 256, 512)
+        evac2b(scopy, 0)
+        store_out1(0)
+        quantize(dk_q[1], E5M2, dk_g[1], 256, 512)
+        evac2b(scopy, 1)
+        store_out1(1)
+        stage2b(2, 1)
+        stage2a(1, 2)
+        stage2b(3, 1)
+        evac2b(scopy, 2)
+        store_out1(2)
+        evac2a(1, 2)
+        store_out0(1, 2, 3)
+        stage2a(1, 3)
+        evac2a(1, 3)
+        store_out0(1, 3, 4)
+        evac2b(scopy, 3)
+        store_out1(3)

@@ -30,9 +30,6 @@ def tile_semanticgraph_pb_v_kernel(tc, q, k, h, cooccur, wv, bv, p, y, grad_out,
         def sb(shape, dtype, name):
             return keep.tile(shape, dtype, name=name, align_bytes=64)
 
-        def bank(shape, name):
-            return psum.tile(shape, F32, name=name)
-
         ctx.enter_context(tc.manual_schedule())
 
         def load(ap, shape, dtype, name):
@@ -43,32 +40,42 @@ def tile_semanticgraph_pb_v_kernel(tc, q, k, h, cooccur, wv, bv, p, y, grad_out,
         def rows(ap, i, c0, c1):
             return ap[G * i : G * (i + 1), c0:c1].rearrange("(p j) w -> p j w", j=J)
 
-        def load_p(i, hf):
-            return load(rows(p, i, G * hf, G * (hf + 1)), [P, J, G], F32, f"p_{i}{hf}")
+        g_raw, y_raw, p_raw, c_raw, h_raw = {}, {}, {}, {}, {}
+
+        def load_yg(i):
+            y_raw[i] = load(rows(y, i, 0, D), [P, J, D], F32, f"y_{i}")
+            g_raw[i] = load(rows(grad_out, i, 0, D), [P, J, D], BF16, f"g_{i}")
 
         def load_c(i, hf):
-            return load(rows(cooccur, i, G * hf, G * (hf + 1)), [P, J, G], BF16, f"c_{i}{hf}")[:]
+            c_raw[i, hf] = load(rows(cooccur, i, G * hf, G * (hf + 1)), [P, J, G], BF16, f"c_{i}{hf}")
 
-        g_raw, y_raw, p_raw, c_raw = {}, {}, {}, {}
-        h_raw = {}
-        y_raw[0] = load(rows(y, 0, 0, D), [P, J, D], F32, "y_0")
-        g_raw[0] = load(rows(grad_out, 0, 0, D), [P, J, D], BF16, "g_0")
-        c_raw[0, 0] = load_c(0, 0)
-        p_raw[0, 0] = load_p(0, 0)
-        y_raw[1] = load(rows(y, 1, 0, D), [P, J, D], F32, "y_1")
-        g_raw[1] = load(rows(grad_out, 1, 0, D), [P, J, D], BF16, "g_1")
-        c_raw[1, 0] = load_c(1, 0)
-        p_raw[1, 0] = load_p(1, 0)
+        def load_p(i, hf, k0, k1):
+            p_raw[i, hf, k0] = load(rows(p, i, G * hf + k0, G * hf + k1), [P, J, k1 - k0], F32, f"p_{i}{hf}_{k0}")
+
+        def load_h(i):
+            h_raw[i] = load(rows(h, i, 0, D), [P, J, D], BF16, f"h_raw{i}")
+
+        load_yg(0)
+        load_c(0, 0)
+        load_p(0, 0, 0, 512)
+        load_yg(1)
+        load_c(1, 0)
+        load_p(1, 0, 0, 256)
+        load_p(1, 0, 256, 512)
         wv_raw = load(rows(wv, 0, 0, D), [P, J, D], BF16, "wv_raw")
-        c_raw[0, 1] = load_c(0, 1)
-        p_raw[0, 1] = load_p(0, 1)
-        c_raw[1, 1] = load_c(1, 1)
-        p_raw[1, 1] = load_p(1, 1)
-        h_raw[0] = load(rows(h, 0, 0, D), [P, J, D], BF16, "h_raw0")
-        h_raw[1] = load(rows(h, 1, 0, D), [P, J, D], BF16, "h_raw1")
+        load_c(0, 1)
+        load_p(0, 1, 0, 256)
+        load_p(0, 1, 256, 512)
+        load_h(0)
+        load_c(1, 1)
+        load_p(1, 1, 0, 256)
+        load_p(1, 1, 256, 512)
+        load_h(1)
 
         ident = sb([P, P], F32, "ident")
         make_identity(nc, ident[:])
+        ident_bf = sb([P, P], BF16, "ident_bf")
+        make_identity(nc, ident_bf[:])
 
         def operand(width, name):
             return (sb([P, width], U32, name + "_codes"), sb([P, width], U8, name + "_scales"))
@@ -88,35 +95,41 @@ def tile_semanticgraph_pb_v_kernel(tc, q, k, h, cooccur, wv, bv, p, y, grad_out,
         wv_q = operand(D, "wv_q")
         h_g = [sb([P, D * J], BF16, f"h_g{i}") for i in range(2)]
         h_q = [operand(D, f"h_q{i}") for i in range(2)]
-        dz1 = [sb([P, J, D], BF16, f"dz1_{hf}") for hf in range(2)]
+        dz1 = [sb([P, J, G], BF16, f"dz1_{hf}") for hf in range(2)]
         dk_g = [sb([P, G * J], BF16, f"dk_g{hf}") for hf in range(2)]
         dk_q = [operand(G, f"dk_q{hf}") for hf in range(2)]
         dv_g = [sb([P, D * J], BF16, f"dv_g{hf}") for hf in range(2)]
         dv_q = [operand(D, f"dv_q{hf}") for hf in range(2)]
         o0 = [sb([P, J, D], F32, f"o0_{hf}") for hf in range(2)]
         o1 = sb([P, J, D], F32, "o1")
+        vcopy, scopy = nc.vector.tensor_copy, nc.scalar.copy
 
-        def relu_grad(i, yt, c0, c1):
+        def relu_grad(i, c0, c1):
             nc.vector.scalar_tensor_tensor(
                 out=dz2[i][:, :, c0:c1],
-                in0=yt,
+                in0=y_raw[i][:, :, c0:c1],
                 scalar=0.0,
                 in1=g_raw[i][:, :, c0:c1],
                 op0=ALU.is_gt,
                 op1=ALU.mult,
             )
 
+        def sort_dz2(i, c0, c1):
+            scopy(
+                out=dz2_g[i][:].rearrange("p (s m j) -> p m j s", s=4, j=J)[:, c0 // 4 : c1 // 4],
+                in_=dz2[i][:, :, c0:c1].rearrange("p j (m s) -> p m j s", s=4),
+            )
 
-        def add_att(i, hf, m0, m1):
+        def add_att(i, hf, k0, k1, piece):
             nc.vector.tensor_tensor(
-                out=att_g[i, hf][:].rearrange("p (t m j) -> p m j t", t=4, j=J)[:, m0:m1],
-                in0=p_raw[i, hf][:].rearrange("p j (m t) -> p m j t", t=4)[:, m0:m1],
-                in1=c_raw[i, hf].rearrange("p j (m t) -> p m j t", t=4)[:, m0:m1],
+                out=att_g[i, hf][:, J * k0 : J * k1].rearrange("p (c i j) -> p c j i", i=4, j=J),
+                in0=p_raw[i, hf, piece][:, :, k0 - piece : k1 - piece].rearrange("p j (c i) -> p c j i", i=4),
+                in1=c_raw[i, hf][:, :, k0:k1].rearrange("p j (c i) -> p c j i", i=4),
                 op=ALU.add,
             )
 
-        def interleave(engine_copy, dst, src, c0, c1):
-            engine_copy(
+        def interleave(copy, dst, src, c0, c1):
+            copy(
                 out=dst[:, J * c0 : J * c1].rearrange("p (c i j) -> p c j i", i=4, j=J),
                 in_=src[:, :, c0:c1].rearrange("p j (c i) -> p c j i", i=4),
             )
@@ -132,36 +145,73 @@ def tile_semanticgraph_pb_v_kernel(tc, q, k, h, cooccur, wv, bv, p, y, grad_out,
                 stop=stop,
             )
 
-        acc = {}
+        acc, turned, side, ob, wb, sums = {}, {}, {}, {}, {}, {}
 
-        def stage1(hf, i, ts):
-            for t in ts:
+        def stage1(hf, i, ss):
+            for s in ss:
                 if i == 0:
-                    acc[hf, t] = bank([P, D], f"acc{t}")
-                mm(acc[hf, t][:], att_q[i, hf], E4M3, P * t, dz2_q[i], E5M2, i == 0, i == 1)
+                    acc[hf, s] = psum.tile([P, G], F32, name=f"acc{s}")
+                mm(acc[hf, s][:], dz2_q[i], E5M2, P * s, att_q[i, hf], E4M3, i == 0, i == 1)
 
-        def evac1(copy, hf, t):
-            copy(out=dz1[hf][:, t, :], in_=acc[hf, t][:])
-
-        tb = {}
-
-        def turn(hf, b):
-            tb[hf, b] = bank([P, 2, 2, P], f"turn{b}")
-            for a in range(2):
-                words = dz1[hf][:, 2 * b + a, :].bitcast(F32)
-                for u in range(2):
-                    nc.tensor.transpose(tb[hf, b][:, a, u, :], words[:, u::2], ident[:])
-
-        def turn_out(hf, b):
-            nc.scalar.copy(
-                out=dk_g[hf][:, 2 * P * J * b : 2 * P * J * (b + 1)].bitcast(F32).rearrange("p (a r u) -> p a r u", a=2, u=2),
-                in_=tb[hf, b][:].rearrange("p a u r -> p a r u"),
+        def evac1(copy, hf, s):
+            copy(
+                out=dz1[hf][:, s, :].rearrange("p (u w e) -> p u w e", u=2, e=2),
+                in_=acc[hf, s][:].rearrange("p (w u e) -> p u w e", u=2, e=2),
             )
 
-        ob = {}
+        def turn(hf, s0, s1, tag):
+            turned[hf, s0] = psum.tile([P, s1 - s0, 2, P], F32, name=tag)
+            for s in range(s0, s1):
+                words = dz1[hf][:, s, :].bitcast(F32)
+                for u in range(2):
+                    nc.tensor.transpose(turned[hf, s0][:, s - s0, u, :], words[:, P * u : P * (u + 1)], ident[:])
 
-        def stage2a(hf, t):
-            ob[hf, t] = bank([P, D], f"turn{t - 2}" if (hf, t // 2) == (1, 1) else f"ob{t % 2}")
+        def turn_out(copy, hf, s0, s1):
+            copy(
+                out=dv_g[hf][:, G * s0 : G * s1].bitcast(F32).rearrange("p (s m u) -> p s m u", m=P, u=2),
+                in_=turned[hf, s0][:].rearrange("p s u m -> p s m u"),
+            )
+
+        def pe_side(key, half, tag, views):
+            side[key, half] = psum.tile([P, 2 * G], BF16, name=tag)
+            for a in range(2):
+                nc.tensor.matmul(
+                    out=side[key, half][:, G * a : G * (a + 1)], lhsT=ident_bf[:], rhs=views[a], start=True, stop=True
+                )
+
+        def pe_side_h(i, half, tag):
+            src = h_raw[i][:].rearrange("p j (b a c) -> p b a c j", b=2, a=2)
+            pe_side(("h", i), half, tag, [src[:, half, a] for a in range(2)])
+
+        def pe_side_dk(hf, u, tag):
+            src = dz1[hf][:].rearrange("p s (u w e) -> p u e w s", u=2, e=2)
+            pe_side(("dk", hf), u, tag, [src[:, u, e] for e in range(2)])
+
+        def side_out(copy, key, dst, half):
+            copy(out=dst[:, 2 * G * half : 2 * G * (half + 1)], in_=side[key, half][:])
+
+        def interleave_dk(copy, hf, u):
+            copy(
+                out=dk_g[hf][:, 2 * G * u : 2 * G * (u + 1)].rearrange("p (e a b s) -> p a s b e", e=2, b=2, s=4),
+                in_=dz1[hf][:, :, 2 * P * u : 2 * P * (u + 1)].rearrange("p s (a b e) -> p a s b e", b=2, e=2),
+            )
+
+        def pe_add(i, hf, k0, piece, tag):
+            sums[i, hf, k0] = psum.tile([P, J, P], F32, name=tag)
+            out = sums[i, hf, k0][:].rearrange("p j c -> p (j c)")
+            nc.tensor.matmul(out=out, lhsT=ident_bf[:], rhs=c_raw[i, hf][:, :, k0 : k0 + P], start=True, stop=False)
+            nc.tensor.matmul(
+                out=out, lhsT=ident[:], rhs=p_raw[i, hf, piece][:, :, k0 - piece : k0 - piece + P], start=False, stop=True
+            )
+
+        def add_out(copy, i, hf, k0):
+            copy(
+                out=att_g[i, hf][:, J * k0 : J * (k0 + P)].rearrange("p (c j) -> p c j", j=J),
+                in_=sums[i, hf, k0][:].rearrange("p j c -> p c j"),
+            )
+
+        def stage2a(hf, t, tag):
+            ob[hf, t] = psum.tile([P, D], F32, name=tag)
             mm(ob[hf, t][:], dk_q[hf], E5M2, P * t, wv_q, E4M3, True, True)
 
         def evac2a(hf, t):
@@ -170,123 +220,125 @@ def tile_semanticgraph_pb_v_kernel(tc, q, k, h, cooccur, wv, bv, p, y, grad_out,
         def store_out0(hf, t0, t1):
             nc.sync.dma_start(out=rows(out_0, hf, 0, D)[:, t0:t1, :], in_=o0[hf][:, t0:t1, :])
 
-        vcopy, scopy = nc.vector.tensor_copy, nc.scalar.copy
-        wb = {}
+        def stage2b(s, hf, tag=None):
+            if hf == 0:
+                wb[s] = psum.tile([P, D], F32, name=tag)
+            mm(wb[s][:], dv_q[hf], E5M2, P * s, h_q[hf], E4M3, hf == 0, hf == 1)
 
-        def stage2b(c, i):
-            if i == 0:
-                wb[c] = bank([P, D], f"acc{c}")
-            mm(wb[c][:], dv_q[i], E5M2, P * c, h_q[i], E4M3, i == 0, i == 1)
+        def evac2b(copy, s):
+            copy(out=o1[:, s, :], in_=wb[s][:])
 
-        def evac2b(copy, c):
-            copy(out=o1[:, c, :], in_=wb[c][:])
+        def store_out1(s0, s1):
+            nc.sync.dma_start(out=rows(out_1, 0, 0, D)[:, s0:s1, :], in_=o1[:, s0:s1, :])
 
-        def store_out1(c):
-            nc.sync.dma_start(out=out_1[P * c : P * (c + 1), :], in_=o1[:, c, :])
-
-        relu_grad(0, y_raw[0][:, :, 0:256], 0, 256)
-        interleave(scopy, dz2_g[0], dz2[0], 0, 256)
-        relu_grad(0, y_raw[0][:, :, 256:512], 256, 512)
-        interleave(scopy, dz2_g[0], dz2[0], 256, 512)
-        add_att(0, 0, 0, P)
+        for c0 in (0, 256):
+            relu_grad(0, c0, c0 + 256)
+            sort_dz2(0, c0, c0 + 256)
+        add_att(0, 0, 0, 256, 0)
+        add_att(0, 0, 256, 512, 0)
+        quantize(att_q[0, 0], E4M3, att_g[0, 0], 0, 256)
+        quantize(att_q[0, 0], E4M3, att_g[0, 0], 256, 512)
+        for c0 in range(0, D, P):
+            relu_grad(1, c0, c0 + P)
+            sort_dz2(1, c0, c0 + P)
         quantize(dz2_q[0], E5M2, dz2_g[0], 0, D)
-        quantize(att_q[0, 0], E4M3, att_g[0, 0], 0, G)
-        stage1(0, 0, [0])
-        stage1(0, 0, [1])
-        stage1(0, 0, [2])
-        stage1(0, 0, [3])
-        relu_grad(1, y_raw[1][:, :, 0:256], 0, 256)
-        interleave(scopy, dz2_g[1], dz2[1], 0, 256)
-        relu_grad(1, y_raw[1][:, :, 256:512], 256, 512)
-        interleave(scopy, dz2_g[1], dz2[1], 256, 512)
-        add_att(1, 0, 0, P)
+        stage1(0, 0, range(4))
+        add_att(1, 0, 0, 256, 0)
         quantize(dz2_q[1], E5M2, dz2_g[1], 0, D)
-        quantize(att_q[1, 0], E4M3, att_g[1, 0], 0, G)
-        stage1(0, 1, [0])
-        stage1(0, 1, [1])
-        stage1(0, 1, [2])
-        stage1(0, 1, [3])
+        add_att(1, 0, 256, 512, 256)
+        quantize(att_q[1, 0], E4M3, att_g[1, 0], 0, 256)
+        quantize(att_q[1, 0], E4M3, att_g[1, 0], 256, 512)
+        stage1(0, 1, range(4))
+
         interleave(scopy, wv_g, wv_raw, 0, D)
-        quantize(wv_q, E4M3, wv_g, 0, D)
-        evac1(scopy, 0, 0)
-        evac1(scopy, 0, 1)
-        turn(0, 0)
+        pe_add(0, 1, 0, 0, "turn0")
+        evac1(vcopy, 0, 0)
+        evac1(vcopy, 0, 1)
         evac1(scopy, 0, 2)
         evac1(scopy, 0, 3)
-        turn(0, 1)
-        turn_out(0, 0)
-        add_att(0, 1, 0, P)
-        interleave(scopy, dv_g[0], dz1[0], 0, D)
-        turn_out(0, 1)
-        quantize(att_q[0, 1], E4M3, att_g[0, 1], 0, G)
-        stage1(1, 0, [0])
-        stage1(1, 0, [1])
-        stage1(1, 0, [2])
-        stage1(1, 0, [3])
+        add_att(0, 1, 128, 256, 0)
+        pe_side_dk(0, 0, "ob0")
+        pe_side_dk(0, 1, "ob1")
+        add_out(scopy, 0, 1, 0)
+        turn(0, 0, 2, "turn1")
+        turn(0, 2, 4, "turn0")
+        side_out(scopy, ("dk", 0), dk_g[0], 0)
+        side_out(scopy, ("dk", 0), dk_g[0], 1)
+        turn_out(scopy, 0, 0, 2)
+        turn_out(scopy, 0, 2, 4)
+        interleave(scopy, h_g[0], h_raw[0], 0, D)
+        quantize(wv_q, E4M3, wv_g, 0, D)
+        add_att(0, 1, 256, 512, 256)
+        quantize(att_q[0, 1], E4M3, att_g[0, 1], 0, 256)
         quantize(dk_q[0], E5M2, dk_g[0], 0, 256)
-        stage2a(0, 0)
-        stage2a(0, 1)
-        interleave(scopy, h_g[1], h_raw[1], 0, D)
-        add_att(1, 1, 0, P)
+        stage2a(0, 0, "ob0")
+        stage2a(0, 1, "ob1")
+        quantize(att_q[0, 1], E4M3, att_g[0, 1], 256, 512)
         quantize(dk_q[0], E5M2, dk_g[0], 256, 512)
-        quantize(att_q[1, 1], E4M3, att_g[1, 1], 0, 256)
-        stage1(1, 1, [0])
-        stage1(1, 1, [1])
-        quantize(att_q[1, 1], E4M3, att_g[1, 1], 256, 512)
-        stage1(1, 1, [2])
-        stage1(1, 1, [3])
-        evac1(scopy, 1, 0)
-        evac1(scopy, 1, 1)
-        evac1(scopy, 1, 2)
-        evac1(scopy, 1, 3)
-        interleave(vcopy, h_g[0], h_raw[0], 0, D)
-        quantize(dv_q[0], E5M2, dv_g[0], 0, D)
-        quantize(h_q[0], E4M3, h_g[0], 0, D)
-        turn(1, 0)
+        stage2a(0, 2, "turn1")
+        stage2a(0, 3, "turn0")
+        stage1(1, 0, [0])
         evac2a(0, 0)
         evac2a(0, 1)
-        store_out0(0, 0, 2)
-        stage2a(0, 2)
-        stage2a(0, 3)
-        turn_out(1, 0)
-        turn(1, 1)
-        stage2b(0, 0)
-        stage2b(1, 0)
-        quantize(h_q[1], E4M3, h_g[1], 0, D)
+        pe_add(1, 1, 0, 0, "ob0")
+        stage1(1, 0, [1, 2, 3])
+        add_out(scopy, 1, 1, 0)
+        add_att(1, 1, 128, 256, 0)
         evac2a(0, 2)
-        store_out0(0, 2, 3)
-        quantize(dk_q[1], E5M2, dk_g[1], 0, 256)
-        interleave(scopy, dv_g[1], dz1[1], 0, 256)
-        stage2a(1, 0)
+        quantize(dv_q[0], E5M2, dv_g[0], 0, 256)
+        add_att(1, 1, 256, 512, 256)
+        quantize(att_q[1, 1], E4M3, att_g[1, 1], 0, 256)
+        quantize(att_q[1, 1], E4M3, att_g[1, 1], 256, 512)
+        pe_side_h(1, 1, "ob1")
+        stage1(1, 1, range(4))
+        store_out0(0, 0, 3)
+
+        interleave(scopy, h_g[1], h_raw[1], 0, 256)
+        quantize(h_q[0], E4M3, h_g[0], 0, D)
         evac2a(0, 3)
         store_out0(0, 3, 4)
-        stage2a(1, 1)
-        turn_out(1, 1)
-        quantize(dv_q[1], E5M2, dv_g[1], 0, 256)
+        evac1(scopy, 1, 0)
+        side_out(scopy, ("h", 1), h_g[1], 1)
+        evac1(vcopy, 1, 1)
+        evac1(vcopy, 1, 2)
+        evac1(scopy, 1, 3)
+        stage2b(0, 0, "ob0")
+        turn(1, 0, 1, "turn1")
+        turn(1, 1, 2, "turn0")
+        stage2b(1, 0, "acc0")
+        turn(1, 2, 4, "ob1")
+        turn_out(scopy, 1, 0, 1)
+        turn_out(scopy, 1, 1, 2)
+        turn_out(scopy, 1, 2, 4)
+        quantize(h_q[1], E4M3, h_g[1], 0, D)
+        quantize(dv_q[0], E5M2, dv_g[0], 256, 512)
+        quantize(dv_q[1], E5M2, dv_g[1], 0, 128)
+        stage2b(0, 1)
+        quantize(dv_q[1], E5M2, dv_g[1], 128, 256)
+        stage2b(1, 1)
+        stage2b(2, 0, "acc1")
+        stage2b(3, 0, "acc3")
+        interleave_dk(vcopy, 1, 0)
+        evac2b(scopy, 0)
+        store_out1(0, 1)
+        quantize(dv_q[1], E5M2, dv_g[1], 256, 512)
+        stage2b(2, 1)
+        stage2b(3, 1)
+        quantize(dk_q[1], E5M2, dk_g[1], 0, 256)
+        stage2a(1, 0, "turn1")
+        stage2a(1, 1, "turn0")
+        evac2b(scopy, 1)
+        store_out1(1, 2)
+        interleave_dk(vcopy, 1, 1)
+        evac2b(scopy, 2)
+        store_out1(2, 3)
         evac2a(1, 0)
         store_out0(1, 0, 1)
-        stage2b(0, 1)
-        stage2b(1, 1)
-        stage2b(2, 0)
-        stage2b(3, 0)
-        interleave(scopy, dv_g[1], dz1[1], 256, 512)
-        evac2a(1, 1)
-        store_out0(1, 1, 2)
-        quantize(dv_q[1], E5M2, dv_g[1], 256, 512)
-        evac2b(scopy, 0)
-        store_out1(0)
         quantize(dk_q[1], E5M2, dk_g[1], 256, 512)
-        evac2b(scopy, 1)
-        store_out1(1)
-        stage2b(2, 1)
-        stage2a(1, 2)
-        stage2b(3, 1)
-        evac2b(scopy, 2)
-        store_out1(2)
-        evac2a(1, 2)
-        store_out0(1, 2, 3)
-        stage2a(1, 3)
-        evac2a(1, 3)
-        store_out0(1, 3, 4)
+        stage2a(1, 2, "acc2")
+        stage2a(1, 3, "ob1")
         evac2b(scopy, 3)
-        store_out1(3)
+        store_out1(3, 4)
+        for t in range(1, 4):
+            evac2a(1, t)
+            store_out0(1, t, t + 1)

@@ -251,81 +251,75 @@ def tile_semanticgraph_pb_v_kernel(tc, q, k, h, cooccur, wv, bv, p, y, grad_out,
         stage1(0, 1, range(4))
 
         interleave(scopy, wv_g, wv_raw, 0, D)
-        pe_add(0, 1, 0, 0, "turn0")
+        pe_add(0, 1, 0, 0, "ob1")
         evac1(vcopy, 0, 0)
         evac1(vcopy, 0, 1)
         evac1(scopy, 0, 2)
         evac1(scopy, 0, 3)
         add_att(0, 1, 128, 256, 0)
-        pe_side_dk(0, 0, "ob0")
-        pe_side_dk(0, 1, "ob1")
+        quantize(wv_q, E4M3, wv_g, 0, D)
+        interleave_dk(scopy, 0, 0)
         add_out(scopy, 0, 1, 0)
+        interleave_dk(scopy, 0, 1)
         turn(0, 0, 2, "turn1")
         turn(0, 2, 4, "turn0")
-        side_out(scopy, ("dk", 0), dk_g[0], 0)
-        side_out(scopy, ("dk", 0), dk_g[0], 1)
-        turn_out(scopy, 0, 0, 2)
-        turn_out(scopy, 0, 2, 4)
-        interleave(scopy, h_g[0], h_raw[0], 0, D)
-        quantize(wv_q, E4M3, wv_g, 0, D)
         add_att(0, 1, 256, 512, 256)
-        quantize(att_q[0, 1], E4M3, att_g[0, 1], 0, 256)
         quantize(dk_q[0], E5M2, dk_g[0], 0, 256)
         stage2a(0, 0, "ob0")
         stage2a(0, 1, "ob1")
         quantize(att_q[0, 1], E4M3, att_g[0, 1], 256, 512)
+        quantize(att_q[0, 1], E4M3, att_g[0, 1], 0, 256)
+        turn_out(scopy, 0, 0, 2)
+        turn_out(scopy, 0, 2, 4)
+        interleave(scopy, h_g[0], h_raw[0], 0, D)
+        stage1(1, 0, range(4))
+        evac2a(0, 0)
+        evac2a(0, 1)
+        quantize(dv_q[0], E5M2, dv_g[0], 0, 256)
+        add_att(1, 1, 0, 256, 0)
         quantize(dk_q[0], E5M2, dk_g[0], 256, 512)
         stage2a(0, 2, "turn1")
         stage2a(0, 3, "turn0")
-        stage1(1, 0, [0])
-        evac2a(0, 0)
-        evac2a(0, 1)
-        pe_add(1, 1, 0, 0, "ob0")
-        stage1(1, 0, [1, 2, 3])
-        add_out(scopy, 1, 1, 0)
-        add_att(1, 1, 128, 256, 0)
-        evac2a(0, 2)
-        quantize(dv_q[0], E5M2, dv_g[0], 0, 256)
         add_att(1, 1, 256, 512, 256)
         quantize(att_q[1, 1], E4M3, att_g[1, 1], 0, 256)
         quantize(att_q[1, 1], E4M3, att_g[1, 1], 256, 512)
-        pe_side_h(1, 1, "ob1")
         stage1(1, 1, range(4))
-        store_out0(0, 0, 3)
+        store_out0(0, 0, 2)
 
-        interleave(scopy, h_g[1], h_raw[1], 0, 256)
+        interleave(scopy, h_g[1], h_raw[1], 0, D)
         quantize(h_q[0], E4M3, h_g[0], 0, D)
-        evac2a(0, 3)
-        store_out0(0, 3, 4)
-        evac1(scopy, 1, 0)
-        side_out(scopy, ("h", 1), h_g[1], 1)
+        quantize(dv_q[0], E5M2, dv_g[0], 256, 512)
+        evac1(vcopy, 1, 0)
         evac1(vcopy, 1, 1)
-        evac1(vcopy, 1, 2)
-        evac1(scopy, 1, 3)
+        evac1(scopy, 1, 2)
         stage2b(0, 0, "ob0")
-        turn(1, 0, 1, "turn1")
-        turn(1, 1, 2, "turn0")
-        stage2b(1, 0, "acc0")
-        turn(1, 2, 4, "ob1")
+        turn(1, 0, 1, "ob1")
+        turn(1, 1, 2, "acc0")
         turn_out(scopy, 1, 0, 1)
+        evac1(scopy, 1, 3)
+        stage2b(1, 0, "acc1")
+        quantize(h_q[1], E4M3, h_g[1], 0, D)
+        evac2a(0, 2)
+        store_out0(0, 2, 3)
+        turn(1, 2, 4, "acc2")
         turn_out(scopy, 1, 1, 2)
         turn_out(scopy, 1, 2, 4)
-        quantize(h_q[1], E4M3, h_g[1], 0, D)
-        quantize(dv_q[0], E5M2, dv_g[0], 256, 512)
         quantize(dv_q[1], E5M2, dv_g[1], 0, 128)
         stage2b(0, 1)
+        stage2b(2, 0, "acc3")
+        evac2a(0, 3)
+        store_out0(0, 3, 4)
         quantize(dv_q[1], E5M2, dv_g[1], 128, 256)
         stage2b(1, 1)
-        stage2b(2, 0, "acc1")
-        stage2b(3, 0, "acc3")
+        stage2b(3, 0, "turn1")
         interleave_dk(vcopy, 1, 0)
         evac2b(scopy, 0)
         store_out1(0, 1)
         quantize(dv_q[1], E5M2, dv_g[1], 256, 512)
         stage2b(2, 1)
-        stage2b(3, 1)
         quantize(dk_q[1], E5M2, dk_g[1], 0, 256)
-        stage2a(1, 0, "turn1")
+        stage2a(1, 0, "ob1")
+        stage2b(3, 1)
         stage2a(1, 1, "turn0")
         evac2b(scopy, 1)
         store_out1(1, 2)
@@ -335,8 +329,8 @@ def tile_semanticgraph_pb_v_kernel(tc, q, k, h, cooccur, wv, bv, p, y, grad_out,
         evac2a(1, 0)
         store_out0(1, 0, 1)
         quantize(dk_q[1], E5M2, dk_g[1], 256, 512)
-        stage2a(1, 2, "acc2")
-        stage2a(1, 3, "ob1")
+        stage2a(1, 2, "acc0")
+        stage2a(1, 3, "acc2")
         evac2b(scopy, 3)
         store_out1(3, 4)
         for t in range(1, 4):

@@ -74,8 +74,6 @@ def tile_semanticgraph_pb_v_kernel(tc, q, k, h, cooccur, wv, bv, p, y, grad_out,
 
         ident = sb([P, P], F32, "ident")
         make_identity(nc, ident[:])
-        ident_bf = sb([P, P], BF16, "ident_bf")
-        make_identity(nc, ident_bf[:])
 
         def operand(width, name):
             return (sb([P, width], U32, name + "_codes"), sb([P, width], U8, name + "_scales"))
@@ -114,8 +112,8 @@ def tile_semanticgraph_pb_v_kernel(tc, q, k, h, cooccur, wv, bv, p, y, grad_out,
                 op1=ALU.mult,
             )
 
-        def sort_dz2(i, c0, c1):
-            scopy(
+        def sort_dz2(i, c0, c1, copy=nc.scalar.copy):
+            copy(
                 out=dz2_g[i][:].rearrange("p (s m j) -> p m j s", s=4, j=J)[:, c0 // 4 : c1 // 4],
                 in_=dz2[i][:, :, c0:c1].rearrange("p j (m s) -> p m j s", s=4),
             )
@@ -145,7 +143,7 @@ def tile_semanticgraph_pb_v_kernel(tc, q, k, h, cooccur, wv, bv, p, y, grad_out,
                 stop=stop,
             )
 
-        acc, turned, side, ob, wb, sums = {}, {}, {}, {}, {}, {}
+        acc, turned, ob, wb = {}, {}, {}, {}
 
         def stage1(hf, i, ss):
             for s in ss:
@@ -172,42 +170,10 @@ def tile_semanticgraph_pb_v_kernel(tc, q, k, h, cooccur, wv, bv, p, y, grad_out,
                 in_=turned[hf, s0][:].rearrange("p s u m -> p s m u"),
             )
 
-        def pe_side(key, half, tag, views):
-            side[key, half] = psum.tile([P, 2 * G], BF16, name=tag)
-            for a in range(2):
-                nc.tensor.matmul(
-                    out=side[key, half][:, G * a : G * (a + 1)], lhsT=ident_bf[:], rhs=views[a], start=True, stop=True
-                )
-
-        def pe_side_h(i, half, tag):
-            src = h_raw[i][:].rearrange("p j (b a c) -> p b a c j", b=2, a=2)
-            pe_side(("h", i), half, tag, [src[:, half, a] for a in range(2)])
-
-        def pe_side_dk(hf, u, tag):
-            src = dz1[hf][:].rearrange("p s (u w e) -> p u e w s", u=2, e=2)
-            pe_side(("dk", hf), u, tag, [src[:, u, e] for e in range(2)])
-
-        def side_out(copy, key, dst, half):
-            copy(out=dst[:, 2 * G * half : 2 * G * (half + 1)], in_=side[key, half][:])
-
         def interleave_dk(copy, hf, u):
             copy(
                 out=dk_g[hf][:, 2 * G * u : 2 * G * (u + 1)].rearrange("p (e a b s) -> p a s b e", e=2, b=2, s=4),
                 in_=dz1[hf][:, :, 2 * P * u : 2 * P * (u + 1)].rearrange("p s (a b e) -> p a s b e", b=2, e=2),
-            )
-
-        def pe_add(i, hf, k0, piece, tag):
-            sums[i, hf, k0] = psum.tile([P, J, P], F32, name=tag)
-            out = sums[i, hf, k0][:].rearrange("p j c -> p (j c)")
-            nc.tensor.matmul(out=out, lhsT=ident_bf[:], rhs=c_raw[i, hf][:, :, k0 : k0 + P], start=True, stop=False)
-            nc.tensor.matmul(
-                out=out, lhsT=ident[:], rhs=p_raw[i, hf, piece][:, :, k0 - piece : k0 - piece + P], start=False, stop=True
-            )
-
-        def add_out(copy, i, hf, k0):
-            copy(
-                out=att_g[i, hf][:, J * k0 : J * (k0 + P)].rearrange("p (c j) -> p c j", j=J),
-                in_=sums[i, hf, k0][:].rearrange("p j c -> p c j"),
             )
 
         def stage2a(hf, t, tag):
@@ -250,32 +216,29 @@ def tile_semanticgraph_pb_v_kernel(tc, q, k, h, cooccur, wv, bv, p, y, grad_out,
         quantize(att_q[1, 0], E4M3, att_g[1, 0], 256, 512)
         stage1(0, 1, range(4))
 
-        interleave(scopy, wv_g, wv_raw, 0, D)
-        pe_add(0, 1, 0, 0, "ob1")
-        evac1(vcopy, 0, 0)
+        interleave(scopy, wv_g, wv_raw, 0, 320)
+        interleave(vcopy, wv_g, wv_raw, 320, 512)
+        quantize(wv_q, E4M3, wv_g, 0, D)
+        evac1(scopy, 0, 0)
         evac1(vcopy, 0, 1)
         evac1(scopy, 0, 2)
         evac1(scopy, 0, 3)
-        add_att(0, 1, 128, 256, 0)
-        quantize(wv_q, E4M3, wv_g, 0, D)
-        interleave_dk(scopy, 0, 0)
-        add_out(scopy, 0, 1, 0)
-        interleave_dk(scopy, 0, 1)
+        add_att(0, 1, 0, 256, 0)
         turn(0, 0, 2, "turn1")
         turn(0, 2, 4, "turn0")
+        interleave_dk(scopy, 0, 0)
+        turn_out(scopy, 0, 0, 2)
+        turn_out(scopy, 0, 2, 4)
+        interleave_dk(scopy, 0, 1)
+        interleave(scopy, h_g[0], h_raw[0], 0, D)
         add_att(0, 1, 256, 512, 256)
         quantize(dk_q[0], E5M2, dk_g[0], 0, 256)
         stage2a(0, 0, "ob0")
         stage2a(0, 1, "ob1")
-        quantize(att_q[0, 1], E4M3, att_g[0, 1], 256, 512)
-        quantize(att_q[0, 1], E4M3, att_g[0, 1], 0, 256)
-        turn_out(scopy, 0, 0, 2)
-        turn_out(scopy, 0, 2, 4)
-        interleave(scopy, h_g[0], h_raw[0], 0, D)
+        quantize(att_q[0, 1], E4M3, att_g[0, 1], 0, G)
         stage1(1, 0, range(4))
+        quantize(dv_q[0], E5M2, dv_g[0], 0, D)
         evac2a(0, 0)
-        evac2a(0, 1)
-        quantize(dv_q[0], E5M2, dv_g[0], 0, 256)
         add_att(1, 1, 0, 256, 0)
         quantize(dk_q[0], E5M2, dk_g[0], 256, 512)
         stage2a(0, 2, "turn1")
@@ -284,43 +247,46 @@ def tile_semanticgraph_pb_v_kernel(tc, q, k, h, cooccur, wv, bv, p, y, grad_out,
         quantize(att_q[1, 1], E4M3, att_g[1, 1], 0, 256)
         quantize(att_q[1, 1], E4M3, att_g[1, 1], 256, 512)
         stage1(1, 1, range(4))
-        store_out0(0, 0, 2)
+        store_out0(0, 0, 1)
 
-        interleave(scopy, h_g[1], h_raw[1], 0, D)
+        interleave(scopy, h_g[1], h_raw[1], 0, 384)
         quantize(h_q[0], E4M3, h_g[0], 0, D)
-        quantize(dv_q[0], E5M2, dv_g[0], 256, 512)
+        interleave(vcopy, h_g[1], h_raw[1], 384, 512)
         evac1(vcopy, 1, 0)
-        evac1(vcopy, 1, 1)
+        evac1(scopy, 1, 1)
         evac1(scopy, 1, 2)
         stage2b(0, 0, "ob0")
-        turn(1, 0, 1, "ob1")
-        turn(1, 1, 2, "acc0")
+        turn(1, 0, 1, "acc0")
+        turn(1, 1, 2, "acc1")
         turn_out(scopy, 1, 0, 1)
         evac1(scopy, 1, 3)
-        stage2b(1, 0, "acc1")
+        turn(1, 2, 3, "acc2")
+        stage2b(1, 0, "acc0")
         quantize(h_q[1], E4M3, h_g[1], 0, D)
+        evac2a(0, 1)
+        store_out0(0, 1, 2)
+        stage2b(2, 0, "ob1")
         evac2a(0, 2)
         store_out0(0, 2, 3)
-        turn(1, 2, 4, "acc2")
-        turn_out(scopy, 1, 1, 2)
-        turn_out(scopy, 1, 2, 4)
+        turn(1, 3, 4, "acc3")
+        for s in range(1, 4):
+            turn_out(scopy, 1, s, s + 1)
         quantize(dv_q[1], E5M2, dv_g[1], 0, 128)
         stage2b(0, 1)
-        stage2b(2, 0, "acc3")
+        stage2b(3, 0, "turn1")
         evac2a(0, 3)
         store_out0(0, 3, 4)
         quantize(dv_q[1], E5M2, dv_g[1], 128, 256)
         stage2b(1, 1)
-        stage2b(3, 0, "turn1")
         interleave_dk(vcopy, 1, 0)
         evac2b(scopy, 0)
         store_out1(0, 1)
         quantize(dv_q[1], E5M2, dv_g[1], 256, 512)
         stage2b(2, 1)
         quantize(dk_q[1], E5M2, dk_g[1], 0, 256)
-        stage2a(1, 0, "ob1")
+        stage2a(1, 0, "acc1")
         stage2b(3, 1)
-        stage2a(1, 1, "turn0")
+        stage2a(1, 1, "acc2")
         evac2b(scopy, 1)
         store_out1(1, 2)
         interleave_dk(vcopy, 1, 1)
@@ -329,8 +295,8 @@ def tile_semanticgraph_pb_v_kernel(tc, q, k, h, cooccur, wv, bv, p, y, grad_out,
         evac2a(1, 0)
         store_out0(1, 0, 1)
         quantize(dk_q[1], E5M2, dk_g[1], 256, 512)
-        stage2a(1, 2, "acc0")
-        stage2a(1, 3, "acc2")
+        stage2a(1, 2, "turn0")
+        stage2a(1, 3, "acc3")
         evac2b(scopy, 3)
         store_out1(3, 4)
         for t in range(1, 4):

@@ -66,9 +66,9 @@ def tile_semanticgraph_pb_v_kernel(tc, q, k, h, cooccur, wv, bv, p, y, grad_out,
         load_c(0, 1)
         load_p(0, 1, 0, 256)
         load_p(0, 1, 256, 512)
-        load_h(0)
         load_c(1, 1)
         load_p(1, 1, 0, 256)
+        load_h(0)
         load_p(1, 1, 256, 512)
         load_h(1)
 
@@ -237,9 +237,10 @@ def tile_semanticgraph_pb_v_kernel(tc, q, k, h, cooccur, wv, bv, p, y, grad_out,
         stage2a(0, 1, "ob1")
         quantize(att_q[0, 1], E4M3, att_g[0, 1], 0, G)
         stage1(1, 0, range(4))
-        quantize(dv_q[0], E5M2, dv_g[0], 0, D)
-        evac2a(0, 0)
+        quantize(dv_q[0], E5M2, dv_g[0], 0, 256)
         add_att(1, 1, 0, 256, 0)
+        evac2a(0, 0)
+        evac2a(0, 1)
         quantize(dk_q[0], E5M2, dk_g[0], 256, 512)
         stage2a(0, 2, "turn1")
         stage2a(0, 3, "turn0")
@@ -247,7 +248,7 @@ def tile_semanticgraph_pb_v_kernel(tc, q, k, h, cooccur, wv, bv, p, y, grad_out,
         quantize(att_q[1, 1], E4M3, att_g[1, 1], 0, 256)
         quantize(att_q[1, 1], E4M3, att_g[1, 1], 256, 512)
         stage1(1, 1, range(4))
-        store_out0(0, 0, 1)
+        store_out0(0, 0, 2)
 
         interleave(scopy, h_g[1], h_raw[1], 0, 384)
         quantize(h_q[0], E4M3, h_g[0], 0, D)
@@ -258,33 +259,34 @@ def tile_semanticgraph_pb_v_kernel(tc, q, k, h, cooccur, wv, bv, p, y, grad_out,
         stage2b(0, 0, "ob0")
         turn(1, 0, 1, "acc0")
         turn(1, 1, 2, "acc1")
+        stage2b(1, 0, "ob1")
         turn_out(scopy, 1, 0, 1)
         evac1(scopy, 1, 3)
         turn(1, 2, 3, "acc2")
-        stage2b(1, 0, "acc0")
         quantize(h_q[1], E4M3, h_g[1], 0, D)
-        evac2a(0, 1)
-        store_out0(0, 1, 2)
-        stage2b(2, 0, "ob1")
+        quantize(dv_q[0], E5M2, dv_g[0], 256, 512)
+        stage2b(2, 0, "acc0")
         evac2a(0, 2)
         store_out0(0, 2, 3)
-        turn(1, 3, 4, "acc3")
-        for s in range(1, 4):
-            turn_out(scopy, 1, s, s + 1)
+        turn_out(scopy, 1, 1, 2)
+        turn_out(scopy, 1, 2, 3)
         quantize(dv_q[1], E5M2, dv_g[1], 0, 128)
         stage2b(0, 1)
+        turn(1, 3, 4, "acc3")
         stage2b(3, 0, "turn1")
         evac2a(0, 3)
         store_out0(0, 3, 4)
         quantize(dv_q[1], E5M2, dv_g[1], 128, 256)
         stage2b(1, 1)
-        interleave_dk(vcopy, 1, 0)
         evac2b(scopy, 0)
         store_out1(0, 1)
-        quantize(dv_q[1], E5M2, dv_g[1], 256, 512)
+        turn_out(scopy, 1, 3, 4)
+        interleave_dk(vcopy, 1, 0)
+        quantize(dv_q[1], E5M2, dv_g[1], 256, 384)
         stage2b(2, 1)
         quantize(dk_q[1], E5M2, dk_g[1], 0, 256)
         stage2a(1, 0, "acc1")
+        quantize(dv_q[1], E5M2, dv_g[1], 384, 512)
         stage2b(3, 1)
         stage2a(1, 1, "acc2")
         evac2b(scopy, 1)

@@ -203,11 +203,11 @@ def tile_semanticgraph_pb_v_kernel(tc, q, k, h, cooccur, wv, bv, p, y, grad_out,
         add_att(0, 0, 0, 256, 0)
         add_att(0, 0, 256, 512, 0)
         quantize(att_q[0, 0], E4M3, att_g[0, 0], 0, 256)
-        quantize(att_q[0, 0], E4M3, att_g[0, 0], 256, 512)
+        quantize(dz2_q[0], E5M2, dz2_g[0], 0, D)
         for c0 in range(0, D, P):
             relu_grad(1, c0, c0 + P)
             sort_dz2(1, c0, c0 + P)
-        quantize(dz2_q[0], E5M2, dz2_g[0], 0, D)
+        quantize(att_q[0, 0], E4M3, att_g[0, 0], 256, 512)
         stage1(0, 0, range(4))
         add_att(1, 0, 0, 256, 0)
         quantize(dz2_q[1], E5M2, dz2_g[1], 0, D)
@@ -232,10 +232,11 @@ def tile_semanticgraph_pb_v_kernel(tc, q, k, h, cooccur, wv, bv, p, y, grad_out,
         interleave_dk(scopy, 0, 1)
         interleave(scopy, h_g[0], h_raw[0], 0, D)
         add_att(0, 1, 256, 512, 256)
+        quantize(att_q[0, 1], E4M3, att_g[0, 1], 0, 256)
         quantize(dk_q[0], E5M2, dk_g[0], 0, 256)
         stage2a(0, 0, "ob0")
         stage2a(0, 1, "ob1")
-        quantize(att_q[0, 1], E4M3, att_g[0, 1], 0, G)
+        quantize(att_q[0, 1], E4M3, att_g[0, 1], 256, 512)
         stage1(1, 0, range(4))
         quantize(dv_q[0], E5M2, dv_g[0], 0, 256)
         add_att(1, 1, 0, 256, 0)

@@ -7,7 +7,10 @@ N = 1024
 D = 512
 P = 128
 J = 4
-G = 512
+G = P * J
+PIECE = G // 2
+WV_SCALAR = 320
+H_SCALAR = 384
 
 F32 = mybir.dt.float32
 BF16 = mybir.dt.bfloat16
@@ -52,24 +55,24 @@ def tile_semanticgraph_pb_v_kernel(tc, q, k, h, cooccur, wv, bv, p, y, grad_out,
         def load_p(i, hf, k0, k1):
             p_raw[i, hf, k0] = load(rows(p, i, G * hf + k0, G * hf + k1), [P, J, k1 - k0], F32, f"p_{i}{hf}_{k0}")
 
-        def load_h(i):
-            h_raw[i] = load(rows(h, i, 0, D), [P, J, D], BF16, f"h_raw{i}")
+        def load_h(hf):
+            h_raw[hf] = load(rows(h, hf, 0, D), [P, J, D], BF16, f"h_raw{hf}")
 
         load_yg(0)
         load_c(0, 0)
-        load_p(0, 0, 0, 512)
+        load_p(0, 0, 0, G)
         load_yg(1)
         load_c(1, 0)
-        load_p(1, 0, 0, 256)
-        load_p(1, 0, 256, 512)
+        load_p(1, 0, 0, PIECE)
+        load_p(1, 0, PIECE, G)
         wv_raw = load(rows(wv, 0, 0, D), [P, J, D], BF16, "wv_raw")
         load_c(0, 1)
-        load_p(0, 1, 0, 256)
-        load_p(0, 1, 256, 512)
+        load_p(0, 1, 0, PIECE)
+        load_p(0, 1, PIECE, G)
         load_c(1, 1)
-        load_p(1, 1, 0, 256)
+        load_p(1, 1, 0, PIECE)
         load_h(0)
-        load_p(1, 1, 256, 512)
+        load_p(1, 1, PIECE, G)
         load_h(1)
 
         ident = sb([P, P], F32, "ident")
@@ -91,8 +94,8 @@ def tile_semanticgraph_pb_v_kernel(tc, q, k, h, cooccur, wv, bv, p, y, grad_out,
         att_q = {(i, hf): operand(G, f"att_q{i}{hf}") for i in range(2) for hf in range(2)}
         wv_g = sb([P, D * J], BF16, "wv_g")
         wv_q = operand(D, "wv_q")
-        h_g = [sb([P, D * J], BF16, f"h_g{i}") for i in range(2)]
-        h_q = [operand(D, f"h_q{i}") for i in range(2)]
+        h_g = [sb([P, D * J], BF16, f"h_g{hf}") for hf in range(2)]
+        h_q = [operand(D, f"h_q{hf}") for hf in range(2)]
         dz1 = [sb([P, J, G], BF16, f"dz1_{hf}") for hf in range(2)]
         dk_g = [sb([P, G * J], BF16, f"dk_g{hf}") for hf in range(2)]
         dk_q = [operand(G, f"dk_q{hf}") for hf in range(2)]
@@ -102,7 +105,7 @@ def tile_semanticgraph_pb_v_kernel(tc, q, k, h, cooccur, wv, bv, p, y, grad_out,
         o1 = sb([P, J, D], F32, "o1")
         vcopy, scopy = nc.vector.tensor_copy, nc.scalar.copy
 
-        def relu_grad(i, c0, c1):
+        def mask_and_sort(i, c0, c1):
             nc.vector.scalar_tensor_tensor(
                 out=dz2[i][:, :, c0:c1],
                 in0=y_raw[i][:, :, c0:c1],
@@ -111,197 +114,195 @@ def tile_semanticgraph_pb_v_kernel(tc, q, k, h, cooccur, wv, bv, p, y, grad_out,
                 op0=ALU.is_gt,
                 op1=ALU.mult,
             )
-
-        def sort_dz2(i, c0, c1, copy=nc.scalar.copy):
-            copy(
-                out=dz2_g[i][:].rearrange("p (s m j) -> p m j s", s=4, j=J)[:, c0 // 4 : c1 // 4],
-                in_=dz2[i][:, :, c0:c1].rearrange("p j (m s) -> p m j s", s=4),
+            scopy(
+                out=dz2_g[i][:].rearrange("p (s m j) -> p m j s", s=J, j=J)[:, c0 // J : c1 // J],
+                in_=dz2[i][:, :, c0:c1].rearrange("p j (m s) -> p m j s", s=J),
             )
 
         def add_att(i, hf, k0, k1, piece):
             nc.vector.tensor_tensor(
-                out=att_g[i, hf][:, J * k0 : J * k1].rearrange("p (c i j) -> p c j i", i=4, j=J),
-                in0=p_raw[i, hf, piece][:, :, k0 - piece : k1 - piece].rearrange("p j (c i) -> p c j i", i=4),
-                in1=c_raw[i, hf][:, :, k0:k1].rearrange("p j (c i) -> p c j i", i=4),
+                out=att_g[i, hf][:, J * k0 : J * k1].rearrange("p (c a j) -> p c j a", a=4, j=J),
+                in0=p_raw[i, hf, piece][:, :, k0 - piece : k1 - piece].rearrange("p j (c a) -> p c j a", a=4),
+                in1=c_raw[i, hf][:, :, k0:k1].rearrange("p j (c a) -> p c j a", a=4),
                 op=ALU.add,
             )
 
         def interleave(copy, dst, src, c0, c1):
             copy(
-                out=dst[:, J * c0 : J * c1].rearrange("p (c i j) -> p c j i", i=4, j=J),
-                in_=src[:, :, c0:c1].rearrange("p j (c i) -> p c j i", i=4),
+                out=dst[:, J * c0 : J * c1].rearrange("p (c a j) -> p c j a", a=4, j=J),
+                in_=src[:, :, c0:c1].rearrange("p j (c a) -> p c j a", a=4),
             )
 
-        def mm(out, a, a_fmt, a0, b, b_fmt, start, stop):
+        def quantize_att(i, hf, k0, k1):
+            quantize(att_q[i, hf], E4M3, att_g[i, hf], k0, k1)
+
+        def mm(out, stationary, tile, moving, start, stop):
             nc.tensor.matmul_mx(
                 out=out,
-                lhsT=a[0][:, a0 : a0 + P].bitcast(a_fmt),
-                lhsT_scale=a[1][:, a0 : a0 + P],
-                rhs=b[0][:].bitcast(b_fmt),
-                rhs_scale=b[1][:],
+                lhsT=stationary[0][:, P * tile : P * (tile + 1)].bitcast(E5M2),
+                lhsT_scale=stationary[1][:, P * tile : P * (tile + 1)],
+                rhs=moving[0][:].bitcast(E4M3),
+                rhs_scale=moving[1][:],
                 start=start,
                 stop=stop,
             )
 
-        acc, turned, ob, wb = {}, {}, {}, {}
+        acc, turned, bank0, bank1 = {}, {}, {}, {}
 
-        def stage1(hf, i, ss):
-            for s in ss:
+        def stage1(hf, i):
+            for s in range(J):
                 if i == 0:
                     acc[hf, s] = psum.tile([P, G], F32, name=f"acc{s}")
-                mm(acc[hf, s][:], dz2_q[i], E5M2, P * s, att_q[i, hf], E4M3, i == 0, i == 1)
+                mm(acc[hf, s][:], dz2_q[i], s, att_q[i, hf], i == 0, i == 1)
 
-        def evac1(copy, hf, s):
+        def round_dz1(copy, hf, s):
             copy(
                 out=dz1[hf][:, s, :].rearrange("p (u w e) -> p u w e", u=2, e=2),
                 in_=acc[hf, s][:].rearrange("p (w u e) -> p u w e", u=2, e=2),
             )
 
-        def turn(hf, s0, s1, tag):
-            turned[hf, s0] = psum.tile([P, s1 - s0, 2, P], F32, name=tag)
+        def turn(hf, s0, s1, bank):
+            turned[hf, s0] = psum.tile([P, s1 - s0, 2, P], F32, name=bank)
             for s in range(s0, s1):
                 words = dz1[hf][:, s, :].bitcast(F32)
                 for u in range(2):
                     nc.tensor.transpose(turned[hf, s0][:, s - s0, u, :], words[:, P * u : P * (u + 1)], ident[:])
 
-        def turn_out(copy, hf, s0, s1):
-            copy(
+        def group_dv(hf, s0, s1):
+            scopy(
                 out=dv_g[hf][:, G * s0 : G * s1].bitcast(F32).rearrange("p (s m u) -> p s m u", m=P, u=2),
                 in_=turned[hf, s0][:].rearrange("p s u m -> p s m u"),
             )
 
-        def interleave_dk(copy, hf, u):
+        def group_dk(copy, hf, u):
             copy(
-                out=dk_g[hf][:, 2 * G * u : 2 * G * (u + 1)].rearrange("p (e a b s) -> p a s b e", e=2, b=2, s=4),
+                out=dk_g[hf][:, 2 * G * u : 2 * G * (u + 1)].rearrange("p (e a b s) -> p a s b e", e=2, b=2, s=J),
                 in_=dz1[hf][:, :, 2 * P * u : 2 * P * (u + 1)].rearrange("p s (a b e) -> p a s b e", b=2, e=2),
             )
 
-        def stage2a(hf, t, tag):
-            ob[hf, t] = psum.tile([P, D], F32, name=tag)
-            mm(ob[hf, t][:], dk_q[hf], E5M2, P * t, wv_q, E4M3, True, True)
+        def quantize_dk(hf, u):
+            quantize(dk_q[hf], E5M2, dk_g[hf], 2 * P * u, 2 * P * (u + 1))
 
-        def evac2a(hf, t):
-            nc.vector.tensor_tensor(out=o0[hf][:, t, :], in0=ob[hf, t][:], in1=g_raw[hf][:, t, :], op=ALU.add)
+        def quantize_dv(hf, s0, s1):
+            quantize(dv_q[hf], E5M2, dv_g[hf], P * s0, P * s1)
 
-        def store_out0(hf, t0, t1):
+        def product0(hf, t, bank):
+            bank0[hf, t] = psum.tile([P, D], F32, name=bank)
+            mm(bank0[hf, t][:], dk_q[hf], t, wv_q, True, True)
+
+        def residual(hf, t):
+            nc.vector.tensor_tensor(out=o0[hf][:, t, :], in0=bank0[hf, t][:], in1=g_raw[hf][:, t, :], op=ALU.add)
+
+        def store0(hf, t0, t1):
             nc.sync.dma_start(out=rows(out_0, hf, 0, D)[:, t0:t1, :], in_=o0[hf][:, t0:t1, :])
 
-        def stage2b(s, hf, tag=None):
-            if hf == 0:
-                wb[s] = psum.tile([P, D], F32, name=tag)
-            mm(wb[s][:], dv_q[hf], E5M2, P * s, h_q[hf], E4M3, hf == 0, hf == 1)
+        def finish0(hf, t):
+            residual(hf, t)
+            store0(hf, t, t + 1)
 
-        def evac2b(copy, s):
-            copy(out=o1[:, s, :], in_=wb[s][:])
+        def open1(s, bank):
+            bank1[s] = psum.tile([P, D], F32, name=bank)
+            mm(bank1[s][:], dv_q[0], s, h_q[0], True, False)
 
-        def store_out1(s0, s1):
-            nc.sync.dma_start(out=rows(out_1, 0, 0, D)[:, s0:s1, :], in_=o1[:, s0:s1, :])
+        def close1(s):
+            mm(bank1[s][:], dv_q[1], s, h_q[1], False, True)
 
-        for c0 in (0, 256):
-            relu_grad(0, c0, c0 + 256)
-            sort_dz2(0, c0, c0 + 256)
-        add_att(0, 0, 0, 256, 0)
-        add_att(0, 0, 256, 512, 0)
-        quantize(att_q[0, 0], E4M3, att_g[0, 0], 0, 256)
+        def finish1(s, queue):
+            scopy(out=o1[:, s, :], in_=bank1[s][:])
+            queue.dma_start(out=rows(out_1, 0, 0, D)[:, s : s + 1, :], in_=o1[:, s : s + 1, :])
+
+        for c0 in range(0, D, 2 * P):
+            mask_and_sort(0, c0, c0 + 2 * P)
+        add_att(0, 0, 0, PIECE, 0)
+        add_att(0, 0, PIECE, G, 0)
+        quantize_att(0, 0, 0, PIECE)
         quantize(dz2_q[0], E5M2, dz2_g[0], 0, D)
         for c0 in range(0, D, P):
-            relu_grad(1, c0, c0 + P)
-            sort_dz2(1, c0, c0 + P)
-        quantize(att_q[0, 0], E4M3, att_g[0, 0], 256, 512)
-        stage1(0, 0, range(4))
-        add_att(1, 0, 0, 256, 0)
+            mask_and_sort(1, c0, c0 + P)
+        quantize_att(0, 0, PIECE, G)
+        stage1(0, 0)
+        add_att(1, 0, 0, PIECE, 0)
         quantize(dz2_q[1], E5M2, dz2_g[1], 0, D)
-        add_att(1, 0, 256, 512, 256)
-        quantize(att_q[1, 0], E4M3, att_g[1, 0], 0, 256)
-        quantize(att_q[1, 0], E4M3, att_g[1, 0], 256, 512)
-        stage1(0, 1, range(4))
+        add_att(1, 0, PIECE, G, PIECE)
+        quantize_att(1, 0, 0, PIECE)
+        quantize_att(1, 0, PIECE, G)
+        stage1(0, 1)
 
-        interleave(scopy, wv_g, wv_raw, 0, 320)
-        interleave(vcopy, wv_g, wv_raw, 320, 512)
+        interleave(scopy, wv_g, wv_raw, 0, WV_SCALAR)
+        interleave(vcopy, wv_g, wv_raw, WV_SCALAR, D)
         quantize(wv_q, E4M3, wv_g, 0, D)
-        evac1(scopy, 0, 0)
-        evac1(vcopy, 0, 1)
-        evac1(scopy, 0, 2)
-        evac1(scopy, 0, 3)
-        add_att(0, 1, 0, 256, 0)
+        for s, copy in enumerate((scopy, vcopy, scopy, scopy)):
+            round_dz1(copy, 0, s)
+        add_att(0, 1, 0, PIECE, 0)
         turn(0, 0, 2, "turn1")
         turn(0, 2, 4, "turn0")
-        interleave_dk(scopy, 0, 0)
-        turn_out(scopy, 0, 0, 2)
-        turn_out(scopy, 0, 2, 4)
-        interleave_dk(scopy, 0, 1)
+        group_dk(scopy, 0, 0)
+        group_dv(0, 0, 2)
+        group_dv(0, 2, 4)
+        group_dk(scopy, 0, 1)
         interleave(scopy, h_g[0], h_raw[0], 0, D)
-        add_att(0, 1, 256, 512, 256)
-        quantize(att_q[0, 1], E4M3, att_g[0, 1], 0, 256)
-        quantize(dk_q[0], E5M2, dk_g[0], 0, 256)
-        stage2a(0, 0, "ob0")
-        stage2a(0, 1, "ob1")
-        quantize(att_q[0, 1], E4M3, att_g[0, 1], 256, 512)
-        stage1(1, 0, range(4))
-        quantize(dv_q[0], E5M2, dv_g[0], 0, 256)
-        add_att(1, 1, 0, 256, 0)
-        evac2a(0, 0)
-        evac2a(0, 1)
-        quantize(dk_q[0], E5M2, dk_g[0], 256, 512)
-        stage2a(0, 2, "turn1")
-        stage2a(0, 3, "turn0")
-        add_att(1, 1, 256, 512, 256)
-        quantize(att_q[1, 1], E4M3, att_g[1, 1], 0, 256)
-        quantize(att_q[1, 1], E4M3, att_g[1, 1], 256, 512)
-        stage1(1, 1, range(4))
-        store_out0(0, 0, 2)
+        add_att(0, 1, PIECE, G, PIECE)
+        quantize_att(0, 1, 0, PIECE)
+        quantize_dk(0, 0)
+        product0(0, 0, "ob0")
+        product0(0, 1, "ob1")
+        quantize_att(0, 1, PIECE, G)
+        stage1(1, 0)
+        quantize_dv(0, 0, 2)
+        add_att(1, 1, 0, PIECE, 0)
+        residual(0, 0)
+        residual(0, 1)
+        quantize_dk(0, 1)
+        product0(0, 2, "turn1")
+        product0(0, 3, "turn0")
+        add_att(1, 1, PIECE, G, PIECE)
+        quantize_att(1, 1, 0, PIECE)
+        quantize_att(1, 1, PIECE, G)
+        stage1(1, 1)
+        store0(0, 0, 2)
 
-        interleave(scopy, h_g[1], h_raw[1], 0, 384)
+        interleave(scopy, h_g[1], h_raw[1], 0, H_SCALAR)
         quantize(h_q[0], E4M3, h_g[0], 0, D)
-        interleave(vcopy, h_g[1], h_raw[1], 384, 512)
-        evac1(vcopy, 1, 0)
-        evac1(scopy, 1, 1)
-        evac1(scopy, 1, 2)
-        stage2b(0, 0, "ob0")
+        interleave(vcopy, h_g[1], h_raw[1], H_SCALAR, D)
+        for s, copy in enumerate((vcopy, scopy, scopy)):
+            round_dz1(copy, 1, s)
+        open1(0, "ob0")
         turn(1, 0, 1, "acc0")
         turn(1, 1, 2, "acc1")
-        stage2b(1, 0, "ob1")
-        turn_out(scopy, 1, 0, 1)
-        evac1(scopy, 1, 3)
+        open1(1, "ob1")
+        group_dv(1, 0, 1)
+        round_dz1(scopy, 1, 3)
         turn(1, 2, 3, "acc2")
         quantize(h_q[1], E4M3, h_g[1], 0, D)
-        quantize(dv_q[0], E5M2, dv_g[0], 256, 512)
-        stage2b(2, 0, "acc0")
-        evac2a(0, 2)
-        store_out0(0, 2, 3)
-        turn_out(scopy, 1, 1, 2)
-        turn_out(scopy, 1, 2, 3)
-        quantize(dv_q[1], E5M2, dv_g[1], 0, 128)
-        stage2b(0, 1)
+        quantize_dv(0, 2, 4)
+        open1(2, "acc0")
+        finish0(0, 2)
+        group_dv(1, 1, 2)
+        group_dv(1, 2, 3)
+        quantize_dv(1, 0, 1)
+        close1(0)
         turn(1, 3, 4, "acc3")
-        stage2b(3, 0, "turn1")
-        evac2a(0, 3)
-        store_out0(0, 3, 4)
-        quantize(dv_q[1], E5M2, dv_g[1], 128, 256)
-        stage2b(1, 1)
-        evac2b(scopy, 0)
-        store_out1(0, 1)
-        turn_out(scopy, 1, 3, 4)
-        interleave_dk(vcopy, 1, 0)
-        quantize(dv_q[1], E5M2, dv_g[1], 256, 384)
-        stage2b(2, 1)
-        quantize(dk_q[1], E5M2, dk_g[1], 0, 256)
-        stage2a(1, 0, "acc1")
-        quantize(dv_q[1], E5M2, dv_g[1], 384, 512)
-        stage2b(3, 1)
-        stage2a(1, 1, "acc2")
-        evac2b(scopy, 1)
-        store_out1(1, 2)
-        interleave_dk(vcopy, 1, 1)
-        evac2b(scopy, 2)
-        store_out1(2, 3)
-        evac2a(1, 0)
-        store_out0(1, 0, 1)
-        quantize(dk_q[1], E5M2, dk_g[1], 256, 512)
-        stage2a(1, 2, "turn0")
-        stage2a(1, 3, "acc3")
-        evac2b(scopy, 3)
-        store_out1(3, 4)
-        for t in range(1, 4):
-            evac2a(1, t)
-            store_out0(1, t, t + 1)
+        open1(3, "turn1")
+        finish0(0, 3)
+        quantize_dv(1, 1, 2)
+        close1(1)
+        finish1(0, nc.sync)
+        group_dv(1, 3, 4)
+        group_dk(vcopy, 1, 0)
+        quantize_dv(1, 2, 3)
+        close1(2)
+        quantize_dk(1, 0)
+        product0(1, 0, "acc1")
+        quantize_dv(1, 3, 4)
+        close1(3)
+        product0(1, 1, "acc2")
+        finish1(1, nc.sync)
+        group_dk(vcopy, 1, 1)
+        finish1(2, nc.sync)
+        finish0(1, 0)
+        quantize_dk(1, 1)
+        product0(1, 2, "turn0")
+        product0(1, 3, "acc3")
+        finish1(3, nc.scalar)
+        for t in range(1, J):
+            finish0(1, t)

@@ -121,9 +121,9 @@ def tile_semanticgraph_pb_v_kernel(tc, q, k, h, cooccur, wv, bv, p, y, grad_out,
 
         def add_att(i, hf, k0, k1, piece):
             nc.vector.tensor_tensor(
-                out=att_g[i, hf][:, J * k0 : J * k1].rearrange("p (c a j) -> p c j a", a=4, j=J),
-                in0=p_raw[i, hf, piece][:, :, k0 - piece : k1 - piece].rearrange("p j (c a) -> p c j a", a=4),
-                in1=c_raw[i, hf][:, :, k0:k1].rearrange("p j (c a) -> p c j a", a=4),
+                out=att_g[i, hf][:, J * k0 : J * k1].rearrange("p (c a j) -> p c j a", a=2, j=J),
+                in0=p_raw[i, hf, piece][:, :, k0 - piece : k1 - piece].rearrange("p j (c a) -> p c j a", a=2),
+                in1=c_raw[i, hf][:, :, k0:k1].rearrange("p j (c a) -> p c j a", a=2),
                 op=ALU.add,
             )
 

@@ -129,8 +129,8 @@ def tile_semanticgraph_pb_v_kernel(tc, q, k, h, cooccur, wv, bv, p, y, grad_out,
 
         def interleave(copy, dst, src, c0, c1):
             copy(
-                out=dst[:, J * c0 : J * c1].rearrange("p (c a j) -> p c j a", a=4, j=J),
-                in_=src[:, :, c0:c1].rearrange("p j (c a) -> p c j a", a=4),
+                out=dst[:, J * c0 : J * c1].rearrange("p (c a j) -> p c j a", a=2, j=J),
+                in_=src[:, :, c0:c1].rearrange("p j (c a) -> p c j a", a=2),
             )
 
         def quantize_att(i, hf, k0, k1):
@@ -176,8 +176,8 @@ def tile_semanticgraph_pb_v_kernel(tc, q, k, h, cooccur, wv, bv, p, y, grad_out,
 
         def group_dk(copy, hf, u):
             copy(
-                out=dk_g[hf][:, 2 * G * u : 2 * G * (u + 1)].rearrange("p (e a b s) -> p a s b e", e=2, b=2, s=J),
-                in_=dz1[hf][:, :, 2 * P * u : 2 * P * (u + 1)].rearrange("p s (a b e) -> p a s b e", b=2, e=2),
+                out=dk_g[hf][:, 2 * G * u : 2 * G * (u + 1)].rearrange("p (e a b s) -> p e a s b", e=2, b=2, s=J),
+                in_=dz1[hf][:, :, 2 * P * u : 2 * P * (u + 1)].rearrange("p s (a b e) -> p e a s b", b=2, e=2),
             )
 
         def quantize_dk(hf, u):

@@ -228,9 +228,11 @@ def tile_semanticgraph_pb_v_kernel(tc, q, k, h, cooccur, wv, bv, p, y, grad_out,
         quantize_att(1, 0, PIECE, G)
         stage1(0, 1)
 
-        interleave(scopy, wv_g, wv_raw, 0, WV_SCALAR)
+        interleave(scopy, wv_g, wv_raw, 0, D // 2)
+        interleave(scopy, wv_g, wv_raw, D // 2, WV_SCALAR)
         interleave(vcopy, wv_g, wv_raw, WV_SCALAR, D)
-        quantize(wv_q, E4M3, wv_g, 0, D)
+        quantize(wv_q, E4M3, wv_g, 0, D // 2)
+        quantize(wv_q, E4M3, wv_g, D // 2, D)
         for s, copy in enumerate((scopy, vcopy, scopy, scopy)):
             round_dz1(copy, 0, s)
         add_att(0, 1, 0, PIECE, 0)
@@ -282,10 +284,10 @@ def tile_semanticgraph_pb_v_kernel(tc, q, k, h, cooccur, wv, bv, p, y, grad_out,
         quantize_dv(1, 0, 1)
         close1(0)
         turn(1, 3, 4, "acc3")
-        open1(3, "turn1")
         finish0(0, 3)
         quantize_dv(1, 1, 2)
         close1(1)
+        open1(3, "turn1")
         finish1(0, nc.sync)
         group_dv(1, 3, 4)
         group_dk(vcopy, 1, 0)

@@ -8,9 +8,8 @@ D = 512
 P = 128
 J = 4
 G = P * J
-PIECE = G // 2
+Q = G // 2
 WV_SCALAR = 320
-H_SCALAR = 384
 
 F32 = mybir.dt.float32
 BF16 = mybir.dt.bfloat16
@@ -43,6 +42,9 @@ def tile_semanticgraph_pb_v_kernel(tc, q, k, h, cooccur, wv, bv, p, y, grad_out,
         def rows(ap, i, c0, c1):
             return ap[G * i : G * (i + 1), c0:c1].rearrange("(p j) w -> p j w", j=J)
 
+        def pairs(ap, x):
+            return ap[G + Q * x : G + Q * (x + 1), :].rearrange("(p u) w -> p u w", u=2)
+
         g_raw, y_raw, p_raw, c_raw, h_raw = {}, {}, {}, {}, {}
 
         def load_yg(i):
@@ -63,20 +65,23 @@ def tile_semanticgraph_pb_v_kernel(tc, q, k, h, cooccur, wv, bv, p, y, grad_out,
         load_p(0, 0, 0, G)
         load_yg(1)
         load_c(1, 0)
-        load_p(1, 0, 0, PIECE)
-        load_p(1, 0, PIECE, G)
+        load_p(1, 0, 0, Q)
+        load_p(1, 0, Q, G)
         wv_raw = load(rows(wv, 0, 0, D), [P, J, D], BF16, "wv_raw")
         load_c(0, 1)
-        load_p(0, 1, 0, PIECE)
-        load_p(0, 1, PIECE, G)
+        load_p(0, 1, 0, Q)
         load_c(1, 1)
-        load_p(1, 1, 0, PIECE)
+        load_p(1, 1, 0, Q)
         load_h(0)
-        load_p(1, 1, PIECE, G)
+        load_p(0, 1, Q, G)
+        load_p(1, 1, Q, G)
         load_h(1)
+        g_pairs = [load(pairs(grad_out, x), [P, 2, D], BF16, f"g_pairs{x}") for x in range(2)]
 
         ident = sb([P, P], F32, "ident")
         make_identity(nc, ident[:])
+        ident_bf = sb([P, P], BF16, "ident_bf")
+        make_identity(nc, ident_bf[:])
 
         def operand(width, name):
             return (sb([P, width], U32, name + "_codes"), sb([P, width], U8, name + "_scales"))
@@ -133,79 +138,119 @@ def tile_semanticgraph_pb_v_kernel(tc, q, k, h, cooccur, wv, bv, p, y, grad_out,
                 in_=src[:, :, c0:c1].rearrange("p j (c a) -> p c j a", a=2),
             )
 
+        def interleave_h1(copy, c0, c1):
+            copy(
+                out=h_g[1][:, J * c0 : J * c1].rearrange("p (c a u e) -> p c u e a", a=2, u=2, e=2),
+                in_=h_raw[1][:, :, c0:c1].rearrange("p (e u) (c a) -> p c u e a", a=2, u=2),
+            )
+
+        def group_on_tensor(row_pairs, bank):
+            t = psum.tile([P, Q * J], BF16, name=bank)
+            for n, two_rows in enumerate(row_pairs):
+                out = t[:].rearrange("p (c n e) -> p n c e", n=2, e=2)[:, n]
+                nc.tensor.matmul(out, ident_bf[:], two_rows, start=True, stop=True)
+            return t
+
+        def h_rows(hf, c0):
+            first, second = ((0, 2, 1), (2, 4, 1)) if hf == 0 else ((0, 4, 2), (1, 4, 2))
+            return [h_raw[hf][:, a:b:c, c0 : c0 + Q].rearrange("p e c -> p c e") for a, b, c in (first, second)]
+
+        def unload(dst, c0, t):
+            scopy(out=dst[:, J * c0 : J * (c0 + Q)], in_=t[:])
+
         def quantize_att(i, hf, k0, k1):
             quantize(att_q[i, hf], E4M3, att_g[i, hf], k0, k1)
 
-        def mm(out, stationary, tile, moving, start, stop):
+        def mm(out, stationary, tile, moving, c0, c1, start, stop):
             nc.tensor.matmul_mx(
                 out=out,
                 lhsT=stationary[0][:, P * tile : P * (tile + 1)].bitcast(E5M2),
                 lhsT_scale=stationary[1][:, P * tile : P * (tile + 1)],
-                rhs=moving[0][:].bitcast(E4M3),
-                rhs_scale=moving[1][:],
+                rhs=moving[0][:, c0:c1].bitcast(E4M3),
+                rhs_scale=moving[1][:, c0:c1],
                 start=start,
                 stop=stop,
             )
 
-        acc, turned, bank0, bank1 = {}, {}, {}, {}
+        acc, acc_q, turned, bank0, bank1 = {}, {}, {}, {}, {}
 
-        def stage1(hf, i):
+        def stage1(i):
             for s in range(J):
                 if i == 0:
-                    acc[hf, s] = psum.tile([P, G], F32, name=f"acc{s}")
-                mm(acc[hf, s][:], dz2_q[i], s, att_q[i, hf], i == 0, i == 1)
+                    acc[s] = psum.tile([P, G], F32, name=f"acc{s}")
+                mm(acc[s][:], dz2_q[i], s, att_q[i, 0], 0, G, i == 0, i == 1)
 
-        def round_dz1(copy, hf, s):
+        def stage1_quarter(x, i):
+            for s in range(J):
+                n, a = divmod(s, 2)
+                if i == 0 and a == 0:
+                    acc_q[x, n] = psum.tile([P, 2, Q], F32, name=f"acc{n}")
+                mm(acc_q[x, n][:, a, :], dz2_q[i], s, att_q[i, 1], Q * x, Q * (x + 1), i + a == 0, i + a == 2)
+
+        def round_dz1(copy, s):
             copy(
-                out=dz1[hf][:, s, :].rearrange("p (u w e) -> p u w e", u=2, e=2),
-                in_=acc[hf, s][:].rearrange("p (w u e) -> p u w e", u=2, e=2),
+                out=dz1[0][:, s, :].rearrange("p (u w e) -> p u w e", u=2, e=2),
+                in_=acc[s][:].rearrange("p (w u e) -> p u w e", u=2, e=2),
             )
 
-        def turn(hf, s0, s1, bank):
-            turned[hf, s0] = psum.tile([P, s1 - s0, 2, P], F32, name=bank)
-            for s in range(s0, s1):
-                words = dz1[hf][:, s, :].bitcast(F32)
-                for u in range(2):
-                    nc.tensor.transpose(turned[hf, s0][:, s - s0, u, :], words[:, P * u : P * (u + 1)], ident[:])
+        def round_quarter(copy, x, n):
+            copy(
+                out=dz1[1][:, 2 * n : 2 * n + 2, :].rearrange("p s (u x m) -> p x s u m", u=2, x=2)[:, x],
+                in_=acc_q[x, n][:].rearrange("p s (m u) -> p s u m", u=2),
+            )
 
-        def group_dv(hf, s0, s1):
+        def turn(hf, s0, bank):
+            turned[hf, s0] = psum.tile([P, 2, 2, P], F32, name=bank)
+            for a in range(2):
+                words = dz1[hf][:, s0 + a, :].bitcast(F32)
+                for u in range(2):
+                    nc.tensor.transpose(turned[hf, s0][:, a, u, :], words[:, P * u : P * (u + 1)], ident[:])
+
+        def group_dv(hf, s0):
             scopy(
-                out=dv_g[hf][:, G * s0 : G * s1].bitcast(F32).rearrange("p (s m u) -> p s m u", m=P, u=2),
+                out=dv_g[hf][:, G * s0 : G * (s0 + 2)].bitcast(F32).rearrange("p (s m u) -> p s m u", m=P, u=2),
                 in_=turned[hf, s0][:].rearrange("p s u m -> p s m u"),
             )
 
-        def group_dk(copy, hf, u):
+        def group_dk(copy, u):
             copy(
-                out=dk_g[hf][:, 2 * G * u : 2 * G * (u + 1)].rearrange("p (e a b s) -> p e a s b", e=2, b=2, s=J),
-                in_=dz1[hf][:, :, 2 * P * u : 2 * P * (u + 1)].rearrange("p s (a b e) -> p e a s b", b=2, e=2),
+                out=dk_g[0][:, 2 * G * u : 2 * G * (u + 1)].rearrange("p (e a b s) -> p e a s b", e=2, b=2, s=J),
+                in_=dz1[0][:, :, 2 * P * u : 2 * P * (u + 1)].rearrange("p s (a b e) -> p e a s b", b=2, e=2),
             )
 
-        def quantize_dk(hf, u):
-            quantize(dk_q[hf], E5M2, dk_g[hf], 2 * P * u, 2 * P * (u + 1))
+        def dk_rows(x):
+            return [
+                dz1[1][:, 2 * n : 2 * n + 2, :].rearrange("p s (u x m) -> p x u m s", u=2, x=2)[:, x] for n in range(2)
+            ]
 
-        def quantize_dv(hf, s0, s1):
-            quantize(dv_q[hf], E5M2, dv_g[hf], P * s0, P * s1)
+        def quantize_dk(hf, n):
+            quantize(dk_q[hf], E5M2, dk_g[hf], Q * n, Q * (n + 1))
+
+        def quantize_dv(hf, s0):
+            quantize(dv_q[hf], E5M2, dv_g[hf], P * s0, P * (s0 + 2))
 
         def product0(hf, t, bank):
             bank0[hf, t] = psum.tile([P, D], F32, name=bank)
-            mm(bank0[hf, t][:], dk_q[hf], t, wv_q, True, True)
+            mm(bank0[hf, t][:], dk_q[hf], t, wv_q, 0, D, True, True)
 
         def residual(hf, t):
-            nc.vector.tensor_tensor(out=o0[hf][:, t, :], in0=bank0[hf, t][:], in1=g_raw[hf][:, t, :], op=ALU.add)
+            g_tile = g_raw[0][:, t, :] if hf == 0 else g_pairs[t // 2][:, t % 2, :]
+            nc.vector.tensor_tensor(out=o0[hf][:, t, :], in0=bank0[hf, t][:], in1=g_tile, op=ALU.add)
 
-        def store0(hf, t0, t1):
-            nc.sync.dma_start(out=rows(out_0, hf, 0, D)[:, t0:t1, :], in_=o0[hf][:, t0:t1, :])
+        def store0(hf, t):
+            dst = rows(out_0, 0, 0, D)[:, t : t + 1, :] if hf == 0 else pairs(out_0, t // 2)[:, t % 2 : t % 2 + 1, :]
+            nc.sync.dma_start(out=dst, in_=o0[hf][:, t : t + 1, :])
 
         def finish0(hf, t):
             residual(hf, t)
-            store0(hf, t, t + 1)
+            store0(hf, t)
 
         def open1(s, bank):
             bank1[s] = psum.tile([P, D], F32, name=bank)
-            mm(bank1[s][:], dv_q[0], s, h_q[0], True, False)
+            mm(bank1[s][:], dv_q[0], s, h_q[0], 0, D, True, False)
 
         def close1(s):
-            mm(bank1[s][:], dv_q[1], s, h_q[1], False, True)
+            mm(bank1[s][:], dv_q[1], s, h_q[1], 0, D, False, True)
 
         def finish1(s, queue):
             scopy(out=o1[:, s, :], in_=bank1[s][:])
@@ -213,20 +258,20 @@ def tile_semanticgraph_pb_v_kernel(tc, q, k, h, cooccur, wv, bv, p, y, grad_out,
 
         for c0 in range(0, D, 2 * P):
             mask_and_sort(0, c0, c0 + 2 * P)
-        add_att(0, 0, 0, PIECE, 0)
-        add_att(0, 0, PIECE, G, 0)
-        quantize_att(0, 0, 0, PIECE)
+        add_att(0, 0, 0, Q, 0)
+        add_att(0, 0, Q, G, 0)
+        quantize_att(0, 0, 0, Q)
         quantize(dz2_q[0], E5M2, dz2_g[0], 0, D)
         for c0 in range(0, D, P):
             mask_and_sort(1, c0, c0 + P)
-        quantize_att(0, 0, PIECE, G)
-        stage1(0, 0)
-        add_att(1, 0, 0, PIECE, 0)
+        quantize_att(0, 0, Q, G)
+        stage1(0)
+        add_att(1, 0, 0, Q, 0)
         quantize(dz2_q[1], E5M2, dz2_g[1], 0, D)
-        add_att(1, 0, PIECE, G, PIECE)
-        quantize_att(1, 0, 0, PIECE)
-        quantize_att(1, 0, PIECE, G)
-        stage1(0, 1)
+        add_att(1, 0, Q, G, Q)
+        quantize_att(1, 0, 0, Q)
+        quantize_att(1, 0, Q, G)
+        stage1(1)
 
         interleave(scopy, wv_g, wv_raw, 0, D // 2)
         interleave(scopy, wv_g, wv_raw, D // 2, WV_SCALAR)
@@ -234,77 +279,79 @@ def tile_semanticgraph_pb_v_kernel(tc, q, k, h, cooccur, wv, bv, p, y, grad_out,
         quantize(wv_q, E4M3, wv_g, 0, D // 2)
         quantize(wv_q, E4M3, wv_g, D // 2, D)
         for s, copy in enumerate((scopy, vcopy, scopy, scopy)):
-            round_dz1(copy, 0, s)
-        add_att(0, 1, 0, PIECE, 0)
-        turn(0, 0, 2, "turn1")
-        turn(0, 2, 4, "turn0")
-        group_dk(scopy, 0, 0)
-        group_dv(0, 0, 2)
-        group_dv(0, 2, 4)
-        group_dk(scopy, 0, 1)
-        interleave(scopy, h_g[0], h_raw[0], 0, D)
-        add_att(0, 1, PIECE, G, PIECE)
-        quantize_att(0, 1, 0, PIECE)
-        quantize_dk(0, 0)
-        product0(0, 0, "ob0")
-        product0(0, 1, "ob1")
-        quantize_att(0, 1, PIECE, G)
-        stage1(1, 0)
-        quantize_dv(0, 0, 2)
-        add_att(1, 1, 0, PIECE, 0)
-        residual(0, 0)
-        residual(0, 1)
+            round_dz1(copy, s)
+        add_att(0, 1, 0, Q, 0)
+        turn(0, 0, "turn1")
+        turn(0, 2, "turn0")
+        group_dk(scopy, 0)
+        group_dk(vcopy, 1)
+        quantize_att(0, 1, 0, Q)
         quantize_dk(0, 1)
-        product0(0, 2, "turn1")
-        product0(0, 3, "turn0")
-        add_att(1, 1, PIECE, G, PIECE)
-        quantize_att(1, 1, 0, PIECE)
-        quantize_att(1, 1, PIECE, G)
-        stage1(1, 1)
-        store0(0, 0, 2)
+        product0(0, 2, "ob0")
+        product0(0, 3, "ob1")
+        stage1_quarter(0, 0)
+        group_dv(0, 0)
+        group_dv(0, 2)
+        interleave(scopy, h_g[0], h_raw[0], 0, Q)
+        add_att(1, 1, 0, Q, 0)
+        quantize_dk(0, 0)
+        quantize_att(1, 1, 0, Q)
+        stage1_quarter(0, 1)
+        h0_bank = group_on_tensor(h_rows(0, Q), "acc3")
+        product0(0, 0, "turn1")
+        product0(0, 1, "turn0")
+        residual(0, 2)
+        add_att(0, 1, Q, G, Q)
+        round_quarter(scopy, 0, 0)
+        round_quarter(scopy, 0, 1)
+        unload(h_g[0], Q, h0_bank)
+        unload(dk_g[1], 0, group_on_tensor(dk_rows(0), "acc2"))
+        add_att(1, 1, Q, G, Q)
+        h1_bank = group_on_tensor(h_rows(1, 0), "ob0")
+        interleave_h1(scopy, Q, D)
+        quantize_att(0, 1, Q, G)
+        stage1_quarter(1, 0)
+        quantize_att(1, 1, Q, G)
+        stage1_quarter(1, 1)
+        store0(0, 2)
 
-        interleave(scopy, h_g[1], h_raw[1], 0, H_SCALAR)
-        quantize(h_q[0], E4M3, h_g[0], 0, D)
-        interleave(vcopy, h_g[1], h_raw[1], H_SCALAR, D)
-        for s, copy in enumerate((vcopy, scopy, scopy)):
-            round_dz1(copy, 1, s)
-        open1(0, "ob0")
-        turn(1, 0, 1, "acc0")
-        turn(1, 1, 2, "acc1")
-        open1(1, "ob1")
-        group_dv(1, 0, 1)
-        round_dz1(scopy, 1, 3)
-        turn(1, 2, 3, "acc2")
-        quantize(h_q[1], E4M3, h_g[1], 0, D)
-        quantize_dv(0, 2, 4)
-        open1(2, "acc0")
-        finish0(0, 2)
-        group_dv(1, 1, 2)
-        group_dv(1, 2, 3)
-        quantize_dv(1, 0, 1)
-        close1(0)
-        turn(1, 3, 4, "acc3")
         finish0(0, 3)
-        quantize_dv(1, 1, 2)
-        close1(1)
-        open1(3, "turn1")
-        finish1(0, nc.sync)
-        group_dv(1, 3, 4)
-        group_dk(vcopy, 1, 0)
-        quantize_dv(1, 2, 3)
-        close1(2)
+        unload(h_g[1], 0, h1_bank)
         quantize_dk(1, 0)
-        product0(1, 0, "acc1")
-        quantize_dv(1, 3, 4)
-        close1(3)
-        product0(1, 1, "acc2")
-        finish1(1, nc.sync)
-        group_dk(vcopy, 1, 1)
-        finish1(2, nc.sync)
+        product0(1, 0, "acc2")
+        product0(1, 1, "acc3")
+        round_quarter(scopy, 1, 0)
+        finish0(0, 0)
+        round_quarter(scopy, 1, 1)
+        quantize(h_q[0], E4M3, h_g[0], 0, D)
+        turn(1, 0, "ob1")
+        turn(1, 2, "ob0")
+        dk_bank = group_on_tensor(dk_rows(1), "acc1")
+        finish0(0, 1)
+        quantize_dv(0, 0)
+        open1(0, "acc0")
+        open1(1, "turn1")
+        group_dv(1, 0)
         finish0(1, 0)
+        quantize(h_q[1], E4M3, h_g[1], 0, D)
+        group_dv(1, 2)
+        quantize_dv(1, 0)
+        close1(0)
+        close1(1)
+        unload(dk_g[1], Q, dk_bank)
+        finish0(1, 1)
+        quantize_dv(0, 2)
+        open1(2, "turn0")
+        finish1(0, nc.sync)
         quantize_dk(1, 1)
-        product0(1, 2, "turn0")
-        product0(1, 3, "acc3")
+        product0(1, 2, "ob1")
+        quantize_dv(1, 2)
+        close1(2)
+        product0(1, 3, "acc2")
+        open1(3, "ob0")
+        close1(3)
+        finish1(1, nc.sync)
+        finish0(1, 2)
+        finish1(2, nc.sync)
+        finish0(1, 3)
         finish1(3, nc.scalar)
-        for t in range(1, J):
-            finish0(1, t)

@@ -80,8 +80,6 @@ def tile_semanticgraph_pb_v_kernel(tc, q, k, h, cooccur, wv, bv, p, y, grad_out,
 
         ident = sb([P, P], F32, "ident")
         make_identity(nc, ident[:])
-        ident_bf = sb([P, P], BF16, "ident_bf")
-        make_identity(nc, ident_bf[:])
 
         def operand(width, name):
             return (sb([P, width], U32, name + "_codes"), sb([P, width], U8, name + "_scales"))
@@ -144,19 +142,15 @@ def tile_semanticgraph_pb_v_kernel(tc, q, k, h, cooccur, wv, bv, p, y, grad_out,
                 in_=h_raw[1][:, :, c0:c1].rearrange("p (e u) (c a) -> p c u e a", a=2, u=2),
             )
 
-        def group_on_tensor(row_pairs, bank):
-            t = psum.tile([P, Q * J], BF16, name=bank)
-            for n, two_rows in enumerate(row_pairs):
-                out = t[:].rearrange("p (c n e) -> p n c e", n=2, e=2)[:, n]
-                nc.tensor.matmul(out, ident_bf[:], two_rows, start=True, stop=True)
-            return t
-
-        def h_rows(hf, c0):
-            first, second = ((0, 2, 1), (2, 4, 1)) if hf == 0 else ((0, 4, 2), (1, 4, 2))
-            return [h_raw[hf][:, a:b:c, c0 : c0 + Q].rearrange("p e c -> p c e") for a, b, c in (first, second)]
-
-        def unload(dst, c0, t):
-            scopy(out=dst[:, J * c0 : J * (c0 + Q)], in_=t[:])
+        def interleave_h1_gpsimd(dst, c0, c1):
+            nc.gpsimd.tensor_scalar(
+                out=dst[:, J * c0 : J * c1].rearrange("p (c u e) -> p c u e", u=2, e=2),
+                in0=h_raw[1][:, :, c0:c1].rearrange("p (e u) c -> p c u e", u=2),
+                scalar1=1.0,
+                scalar2=0.0,
+                op0=ALU.mult,
+                op1=ALU.add,
+            )
 
         def quantize_att(i, hf, k0, k1):
             quantize(att_q[i, hf], E4M3, att_g[i, hf], k0, k1)
@@ -180,11 +174,11 @@ def tile_semanticgraph_pb_v_kernel(tc, q, k, h, cooccur, wv, bv, p, y, grad_out,
                     acc[s] = psum.tile([P, G], F32, name=f"acc{s}")
                 mm(acc[s][:], dz2_q[i], s, att_q[i, 0], 0, G, i == 0, i == 1)
 
-        def stage1_quarter(x, i):
+        def stage1_quarter(x, i, first=None):
             for s in range(J):
                 n, a = divmod(s, 2)
                 if i == 0 and a == 0:
-                    acc_q[x, n] = psum.tile([P, 2, Q], F32, name=f"acc{n}")
+                    acc_q[x, n] = psum.tile([P, 2, Q], F32, name=f"acc{first + n}")
                 mm(acc_q[x, n][:, a, :], dz2_q[i], s, att_q[i, 1], Q * x, Q * (x + 1), i + a == 0, i + a == 2)
 
         def round_dz1(copy, s):
@@ -218,10 +212,11 @@ def tile_semanticgraph_pb_v_kernel(tc, q, k, h, cooccur, wv, bv, p, y, grad_out,
                 in_=dz1[0][:, :, 2 * P * u : 2 * P * (u + 1)].rearrange("p s (a b e) -> p e a s b", b=2, e=2),
             )
 
-        def dk_rows(x):
-            return [
-                dz1[1][:, 2 * n : 2 * n + 2, :].rearrange("p s (u x m) -> p x u m s", u=2, x=2)[:, x] for n in range(2)
-            ]
+        def group_dk_quarter(copy, x, u0, u1):
+            copy(
+                out=dk_g[1][:, G * (2 * x + u0) : G * (2 * x + u1)].rearrange("p (u a b s) -> p u a s b", a=P // 2, b=2, s=J),
+                in_=dz1[1][:].rearrange("p s (u x a b) -> p x u a s b", u=2, x=2, b=2)[:, x, u0:u1],
+            )
 
         def quantize_dk(hf, n):
             quantize(dk_q[hf], E5M2, dk_g[hf], Q * n, Q * (n + 1))
@@ -289,69 +284,69 @@ def tile_semanticgraph_pb_v_kernel(tc, q, k, h, cooccur, wv, bv, p, y, grad_out,
         quantize_dk(0, 1)
         product0(0, 2, "ob0")
         product0(0, 3, "ob1")
-        stage1_quarter(0, 0)
+        stage1_quarter(0, 0, 0)
         group_dv(0, 0)
         group_dv(0, 2)
         interleave(scopy, h_g[0], h_raw[0], 0, Q)
         add_att(1, 1, 0, Q, 0)
-        quantize_dk(0, 0)
+        residual(0, 2)
         quantize_att(1, 1, 0, Q)
         stage1_quarter(0, 1)
-        h0_bank = group_on_tensor(h_rows(0, Q), "acc3")
-        product0(0, 0, "turn1")
-        product0(0, 1, "turn0")
-        residual(0, 2)
+        quantize_dv(0, 0)
         add_att(0, 1, Q, G, Q)
         round_quarter(scopy, 0, 0)
         round_quarter(scopy, 0, 1)
-        unload(h_g[0], Q, h0_bank)
-        unload(dk_g[1], 0, group_on_tensor(dk_rows(0), "acc2"))
+        interleave(scopy, h_g[0], h_raw[0], Q, D)
+        quantize_dk(0, 0)
+        product0(0, 0, "turn1")
+        product0(0, 1, "turn0")
         add_att(1, 1, Q, G, Q)
-        h1_bank = group_on_tensor(h_rows(1, 0), "ob0")
-        interleave_h1(scopy, Q, D)
+        group_dk_quarter(scopy, 0, 0, 2)
         quantize_att(0, 1, Q, G)
-        stage1_quarter(1, 0)
+        stage1_quarter(1, 0, 0)
         quantize_att(1, 1, Q, G)
         stage1_quarter(1, 1)
         store0(0, 2)
 
-        finish0(0, 3)
-        unload(h_g[1], 0, h1_bank)
-        quantize_dk(1, 0)
-        product0(1, 0, "acc2")
-        product0(1, 1, "acc3")
-        round_quarter(scopy, 1, 0)
-        finish0(0, 0)
-        round_quarter(scopy, 1, 1)
         quantize(h_q[0], E4M3, h_g[0], 0, D)
-        turn(1, 0, "ob1")
-        turn(1, 2, "ob0")
-        dk_bank = group_on_tensor(dk_rows(1), "acc1")
+        interleave_h1_gpsimd(h_g[0], Q, D)
+        open1(0, "ob0")
+        interleave_h1(scopy, 0, P)
+        finish0(0, 3)
+        finish0(0, 0)
         finish0(0, 1)
-        quantize_dv(0, 0)
-        open1(0, "acc0")
-        open1(1, "turn1")
+        round_quarter(scopy, 1, 0)
+        open1(1, "acc2")
+        round_quarter(scopy, 1, 1)
+        interleave_h1(scopy, P, Q)
+        turn(1, 0, "ob1")
+        turn(1, 2, "acc3")
+        quantize_dk(1, 0)
+        product0(1, 0, "acc0")
+        product0(1, 1, "turn1")
+        quantize(h_q[1], E4M3, h_g[0], Q, D)
+        quantize_dv(0, 2)
+        open1(2, "turn0")
         group_dv(1, 0)
-        finish0(1, 0)
-        quantize(h_q[1], E4M3, h_g[1], 0, D)
-        group_dv(1, 2)
+        quantize(h_q[1], E4M3, h_g[1], 0, Q)
         quantize_dv(1, 0)
         close1(0)
         close1(1)
-        unload(dk_g[1], Q, dk_bank)
+        open1(3, "acc1")
+        finish0(1, 0)
+        group_dv(1, 2)
+        group_dk_quarter(scopy, 1, 0, 1)
         finish0(1, 1)
-        quantize_dv(0, 2)
-        open1(2, "turn0")
         finish1(0, nc.sync)
-        quantize_dk(1, 1)
-        product0(1, 2, "ob1")
         quantize_dv(1, 2)
         close1(2)
-        product0(1, 3, "acc2")
-        open1(3, "ob0")
         close1(3)
+        group_dk_quarter(vcopy, 1, 1, 2)
         finish1(1, nc.sync)
-        finish0(1, 2)
+        quantize_dk(1, 1)
+        product0(1, 2, "ob1")
+        product0(1, 3, "acc3")
         finish1(2, nc.sync)
+        finish1(3, nc.sync)
+        finish0(1, 2)
         finish0(1, 3)
-        finish1(3, nc.scalar)

@@ -10,6 +10,7 @@ J = 4
 G = P * J
 Q = G // 2
 WV_SCALAR = 320
+H0_FIRST = 352
 
 F32 = mybir.dt.float32
 BF16 = mybir.dt.bfloat16
@@ -84,10 +85,11 @@ def tile_semanticgraph_pb_v_kernel(tc, q, k, h, cooccur, wv, bv, p, y, grad_out,
         def operand(width, name):
             return (sb([P, width], U32, name + "_codes"), sb([P, width], U8, name + "_scales"))
 
-        def quantize(op, fmt, grouped, c0, c1):
+        def quantize(op, fmt, grouped, c0, c1, at=None):
             codes, scales = op
+            g0 = c0 if at is None else at
             nc.vector.quantize_mx(
-                out=codes[:, c0:c1].bitcast(fmt), scales=scales[:, c0:c1], in_=grouped[:, J * c0 : J * c1]
+                out=codes[:, c0:c1].bitcast(fmt), scales=scales[:, c0:c1], in_=grouped[:, J * g0 : J * (g0 + c1 - c0)]
             )
 
         dz2 = [sb([P, J, D], BF16, f"dz2_{i}") for i in range(2)]
@@ -144,7 +146,7 @@ def tile_semanticgraph_pb_v_kernel(tc, q, k, h, cooccur, wv, bv, p, y, grad_out,
 
         def interleave_h1_gpsimd(dst, c0, c1):
             nc.gpsimd.tensor_scalar(
-                out=dst[:, J * c0 : J * c1].rearrange("p (c u e) -> p c u e", u=2, e=2),
+                out=dst[:, : J * (c1 - c0)].rearrange("p (c u e) -> p c u e", u=2, e=2),
                 in0=h_raw[1][:, :, c0:c1].rearrange("p (e u) c -> p c u e", u=2),
                 scalar1=1.0,
                 scalar2=0.0,
@@ -200,10 +202,10 @@ def tile_semanticgraph_pb_v_kernel(tc, q, k, h, cooccur, wv, bv, p, y, grad_out,
                 for u in range(2):
                     nc.tensor.transpose(turned[hf, s0][:, a, u, :], words[:, P * u : P * (u + 1)], ident[:])
 
-        def group_dv(hf, s0):
+        def group_dv(hf, s0, s1):
             scopy(
-                out=dv_g[hf][:, G * s0 : G * (s0 + 2)].bitcast(F32).rearrange("p (s m u) -> p s m u", m=P, u=2),
-                in_=turned[hf, s0][:].rearrange("p s u m -> p s m u"),
+                out=dv_g[hf][:, G * s0 : G * s1].bitcast(F32).rearrange("p (s m u) -> p s m u", m=P, u=2),
+                in_=turned[hf, s0 - s0 % 2][:, s0 % 2 : s0 % 2 + s1 - s0].rearrange("p s u m -> p s m u"),
             )
 
         def group_dk(copy, u):
@@ -221,8 +223,11 @@ def tile_semanticgraph_pb_v_kernel(tc, q, k, h, cooccur, wv, bv, p, y, grad_out,
         def quantize_dk(hf, n):
             quantize(dk_q[hf], E5M2, dk_g[hf], Q * n, Q * (n + 1))
 
-        def quantize_dv(hf, s0):
-            quantize(dv_q[hf], E5M2, dv_g[hf], P * s0, P * (s0 + 2))
+        def quantize_dk_tile(t):
+            quantize(dk_q[1], E5M2, dk_g[1], P * t, P * (t + 1))
+
+        def quantize_dv(hf, s0, s1):
+            quantize(dv_q[hf], E5M2, dv_g[hf], P * s0, P * s1)
 
         def product0(hf, t, bank):
             bank0[hf, t] = psum.tile([P, D], F32, name=bank)
@@ -285,23 +290,23 @@ def tile_semanticgraph_pb_v_kernel(tc, q, k, h, cooccur, wv, bv, p, y, grad_out,
         product0(0, 2, "ob0")
         product0(0, 3, "ob1")
         stage1_quarter(0, 0, 0)
-        group_dv(0, 0)
-        group_dv(0, 2)
-        interleave(scopy, h_g[0], h_raw[0], 0, Q)
+        group_dv(0, 0, 2)
+        group_dv(0, 2, 4)
+        interleave(scopy, h_g[0], h_raw[0], 0, H0_FIRST)
         add_att(1, 1, 0, Q, 0)
         residual(0, 2)
         quantize_att(1, 1, 0, Q)
         stage1_quarter(0, 1)
-        quantize_dv(0, 0)
+        quantize_dv(0, 0, 2)
         add_att(0, 1, Q, G, Q)
         round_quarter(scopy, 0, 0)
         round_quarter(scopy, 0, 1)
-        interleave(scopy, h_g[0], h_raw[0], Q, D)
+        interleave(scopy, h_g[0], h_raw[0], H0_FIRST, D)
+        group_dk_quarter(scopy, 0, 0, 2)
         quantize_dk(0, 0)
         product0(0, 0, "turn1")
         product0(0, 1, "turn0")
         add_att(1, 1, Q, G, Q)
-        group_dk_quarter(scopy, 0, 0, 2)
         quantize_att(0, 1, Q, G)
         stage1_quarter(1, 0, 0)
         quantize_att(1, 1, Q, G)
@@ -309,44 +314,47 @@ def tile_semanticgraph_pb_v_kernel(tc, q, k, h, cooccur, wv, bv, p, y, grad_out,
         store0(0, 2)
 
         quantize(h_q[0], E4M3, h_g[0], 0, D)
-        interleave_h1_gpsimd(h_g[0], Q, D)
         open1(0, "ob0")
+        quantize_dk(1, 0)
+        interleave_h1_gpsimd(dk_g[1], Q, D)
         interleave_h1(scopy, 0, P)
         finish0(0, 3)
+        product0(1, 0, "acc3")
         finish0(0, 0)
         finish0(0, 1)
         round_quarter(scopy, 1, 0)
-        open1(1, "acc2")
         round_quarter(scopy, 1, 1)
         interleave_h1(scopy, P, Q)
         turn(1, 0, "ob1")
-        turn(1, 2, "acc3")
-        quantize_dk(1, 0)
-        product0(1, 0, "acc0")
-        product0(1, 1, "turn1")
-        quantize(h_q[1], E4M3, h_g[0], Q, D)
-        quantize_dv(0, 2)
-        open1(2, "turn0")
-        group_dv(1, 0)
-        quantize(h_q[1], E4M3, h_g[1], 0, Q)
-        quantize_dv(1, 0)
-        close1(0)
-        close1(1)
-        open1(3, "acc1")
+        turn(1, 2, "acc0")
         finish0(1, 0)
-        group_dv(1, 2)
-        group_dk_quarter(scopy, 1, 0, 1)
+        product0(1, 1, "turn1")
+        open1(1, "acc2")
+        quantize(h_q[1], E4M3, dk_g[1], Q, D, 0)
+        group_dv(1, 0, 1)
+        group_dv(1, 1, 2)
+        quantize(h_q[1], E4M3, h_g[1], 0, Q)
+        group_dv(1, 2, 4)
+        quantize_dv(1, 0, 1)
+        close1(0)
         finish0(1, 1)
+        quantize_dv(1, 1, 2)
+        close1(1)
+        quantize_dv(0, 2, 4)
+        open1(2, "turn0")
+        group_dk_quarter(scopy, 1, 0, 1)
         finish1(0, nc.sync)
-        quantize_dv(1, 2)
+        quantize_dv(1, 2, 4)
         close1(2)
+        open1(3, "acc1")
         close1(3)
         group_dk_quarter(vcopy, 1, 1, 2)
+        quantize_dk_tile(2)
+        product0(1, 2, "acc3")
         finish1(1, nc.sync)
-        quantize_dk(1, 1)
-        product0(1, 2, "ob1")
-        product0(1, 3, "acc3")
+        quantize_dk_tile(3)
+        product0(1, 3, "acc0")
         finish1(2, nc.sync)
-        finish1(3, nc.sync)
         finish0(1, 2)
+        finish1(3, nc.scalar)
         finish0(1, 3)

@@ -10,7 +10,8 @@ J = 4
 G = P * J
 Q = G // 2
 WV_SCALAR = 320
-H0_FIRST = 352
+H0_FIRST = 416
+H1_FIRST = 192
 
 F32 = mybir.dt.float32
 BF16 = mybir.dt.bfloat16
@@ -294,10 +295,10 @@ def tile_semanticgraph_pb_v_kernel(tc, q, k, h, cooccur, wv, bv, p, y, grad_out,
         group_dv(0, 2, 4)
         interleave(scopy, h_g[0], h_raw[0], 0, H0_FIRST)
         add_att(1, 1, 0, Q, 0)
-        residual(0, 2)
+        quantize_dv(0, 0, 2)
         quantize_att(1, 1, 0, Q)
         stage1_quarter(0, 1)
-        quantize_dv(0, 0, 2)
+        residual(0, 2)
         add_att(0, 1, Q, G, Q)
         round_quarter(scopy, 0, 0)
         round_quarter(scopy, 0, 1)
@@ -317,23 +318,23 @@ def tile_semanticgraph_pb_v_kernel(tc, q, k, h, cooccur, wv, bv, p, y, grad_out,
         open1(0, "ob0")
         quantize_dk(1, 0)
         interleave_h1_gpsimd(dk_g[1], Q, D)
-        interleave_h1(scopy, 0, P)
+        interleave_h1(scopy, 0, H1_FIRST)
         finish0(0, 3)
         product0(1, 0, "acc3")
         finish0(0, 0)
         finish0(0, 1)
         round_quarter(scopy, 1, 0)
         round_quarter(scopy, 1, 1)
-        interleave_h1(scopy, P, Q)
+        interleave_h1(scopy, H1_FIRST, Q)
         turn(1, 0, "ob1")
         turn(1, 2, "acc0")
         finish0(1, 0)
         product0(1, 1, "turn1")
         open1(1, "acc2")
-        quantize(h_q[1], E4M3, dk_g[1], Q, D, 0)
+        quantize(h_q[1], E4M3, h_g[1], 0, Q)
         group_dv(1, 0, 1)
         group_dv(1, 1, 2)
-        quantize(h_q[1], E4M3, h_g[1], 0, Q)
+        quantize(h_q[1], E4M3, dk_g[1], Q, D, 0)
         group_dv(1, 2, 4)
         quantize_dv(1, 0, 1)
         close1(0)

@@ -10,8 +10,8 @@ J = 4
 G = P * J
 Q = G // 2
 WV_SCALAR = 320
-H0_FIRST = 416
-H1_FIRST = 192
+ADD_VECTOR = 208
+H0_FIRST = 288
 
 F32 = mybir.dt.float32
 BF16 = mybir.dt.bfloat16
@@ -82,6 +82,8 @@ def tile_semanticgraph_pb_v_kernel(tc, q, k, h, cooccur, wv, bv, p, y, grad_out,
 
         ident = sb([P, P], F32, "ident")
         make_identity(nc, ident[:])
+        ident_bf = sb([P, P], BF16, "ident_bf")
+        make_identity(nc, ident_bf[:])
 
         def operand(width, name):
             return (sb([P, width], U32, name + "_codes"), sb([P, width], U8, name + "_scales"))
@@ -109,6 +111,7 @@ def tile_semanticgraph_pb_v_kernel(tc, q, k, h, cooccur, wv, bv, p, y, grad_out,
         dv_q = [operand(D, f"dv_q{hf}") for hf in range(2)]
         o0 = [sb([P, J, D], F32, f"o0_{hf}") for hf in range(2)]
         o1 = sb([P, J, D], F32, "o1")
+        c_bank = {}
         vcopy, scopy = nc.vector.tensor_copy, nc.scalar.copy
 
         def mask_and_sort(i, c0, c1):
@@ -133,6 +136,23 @@ def tile_semanticgraph_pb_v_kernel(tc, q, k, h, cooccur, wv, bv, p, y, grad_out,
                 op=ALU.add,
             )
 
+        def stage_c(i, k0, bank):
+            c_bank[i, k0] = psum.tile([P, J, ADD_VECTOR], BF16, name=bank)
+            for j in range(0, J, 2):
+                src = c_raw[i, 1][:, j : j + 2, k0 : k0 + ADD_VECTOR]
+                nc.tensor.matmul(c_bank[i, k0][:, j : j + 2, :], ident_bf[:], src, start=True, stop=True)
+
+        def add_att_shared(i, k0):
+            k1 = k0 + ADD_VECTOR
+            shares = ((nc.vector, k0, k1, c_bank[i, k0][:]), (nc.gpsimd, k1, k0 + Q, c_raw[i, 1][:, :, k1 : k0 + Q]))
+            for engine, a, b, c in shares:
+                engine.tensor_tensor(
+                    out=att_g[i, 1][:, J * a : J * b].rearrange("p (c a j) -> p c j a", a=2, j=J),
+                    in0=p_raw[i, 1, k0][:, :, a - k0 : b - k0].rearrange("p j (c a) -> p c j a", a=2),
+                    in1=c.rearrange("p j (c a) -> p c j a", a=2),
+                    op=ALU.add,
+                )
+
         def interleave(copy, dst, src, c0, c1):
             copy(
                 out=dst[:, J * c0 : J * c1].rearrange("p (c a j) -> p c j a", a=2, j=J),
@@ -145,10 +165,11 @@ def tile_semanticgraph_pb_v_kernel(tc, q, k, h, cooccur, wv, bv, p, y, grad_out,
                 in_=h_raw[1][:, :, c0:c1].rearrange("p (e u) (c a) -> p c u e a", a=2, u=2),
             )
 
-        def interleave_h1_gpsimd(dst, c0, c1):
+        def interleave_gpsimd(dst, hf, c0, c1):
+            rows_of_word = "p (u e) c -> p c u e" if hf == 0 else "p (e u) c -> p c u e"
             nc.gpsimd.tensor_scalar(
                 out=dst[:, : J * (c1 - c0)].rearrange("p (c u e) -> p c u e", u=2, e=2),
-                in0=h_raw[1][:, :, c0:c1].rearrange("p (e u) c -> p c u e", u=2),
+                in0=h_raw[hf][:, :, c0:c1].rearrange(rows_of_word, u=2),
                 scalar1=1.0,
                 scalar2=0.0,
                 op0=ALU.mult,
@@ -196,17 +217,18 @@ def tile_semanticgraph_pb_v_kernel(tc, q, k, h, cooccur, wv, bv, p, y, grad_out,
                 in_=acc_q[x, n][:].rearrange("p s (m u) -> p s u m", u=2),
             )
 
-        def turn(hf, s0, bank):
-            turned[hf, s0] = psum.tile([P, 2, 2, P], F32, name=bank)
-            for a in range(2):
-                words = dz1[hf][:, s0 + a, :].bitcast(F32)
+        def turn(hf, s0, s1, bank):
+            t = psum.tile([P, s1 - s0, 2, P], F32, name=bank)
+            for s in range(s0, s1):
+                turned[hf, s] = t[:, s - s0 :]
+                words = dz1[hf][:, s, :].bitcast(F32)
                 for u in range(2):
-                    nc.tensor.transpose(turned[hf, s0][:, a, u, :], words[:, P * u : P * (u + 1)], ident[:])
+                    nc.tensor.transpose(t[:, s - s0, u, :], words[:, P * u : P * (u + 1)], ident[:])
 
         def group_dv(hf, s0, s1):
             scopy(
                 out=dv_g[hf][:, G * s0 : G * s1].bitcast(F32).rearrange("p (s m u) -> p s m u", m=P, u=2),
-                in_=turned[hf, s0 - s0 % 2][:, s0 % 2 : s0 % 2 + s1 - s0].rearrange("p s u m -> p s m u"),
+                in_=turned[hf, s0][:, : s1 - s0].rearrange("p s u m -> p s m u"),
             )
 
         def group_dk(copy, u):
@@ -282,8 +304,10 @@ def tile_semanticgraph_pb_v_kernel(tc, q, k, h, cooccur, wv, bv, p, y, grad_out,
         for s, copy in enumerate((scopy, vcopy, scopy, scopy)):
             round_dz1(copy, s)
         add_att(0, 1, 0, Q, 0)
-        turn(0, 0, "turn1")
-        turn(0, 2, "turn0")
+        turn(0, 0, 2, "turn1")
+        turn(0, 2, 4, "turn0")
+        stage_c(1, 0, "acc2")
+        stage_c(0, Q, "acc3")
         group_dk(scopy, 0)
         group_dk(vcopy, 1)
         quantize_att(0, 1, 0, Q)
@@ -294,47 +318,52 @@ def tile_semanticgraph_pb_v_kernel(tc, q, k, h, cooccur, wv, bv, p, y, grad_out,
         group_dv(0, 0, 2)
         group_dv(0, 2, 4)
         interleave(scopy, h_g[0], h_raw[0], 0, H0_FIRST)
-        add_att(1, 1, 0, Q, 0)
+        add_att_shared(1, 0)
         quantize_dv(0, 0, 2)
         quantize_att(1, 1, 0, Q)
         stage1_quarter(0, 1)
+        stage_c(1, Q, "acc2")
+        interleave_gpsimd(att_g[1, 1], 0, D - P, D)
         residual(0, 2)
-        add_att(0, 1, Q, G, Q)
+        residual(0, 3)
+        add_att_shared(0, Q)
         round_quarter(scopy, 0, 0)
         round_quarter(scopy, 0, 1)
-        interleave(scopy, h_g[0], h_raw[0], H0_FIRST, D)
+        interleave(scopy, h_g[0], h_raw[0], H0_FIRST, D - P)
         group_dk_quarter(scopy, 0, 0, 2)
         quantize_dk(0, 0)
         product0(0, 0, "turn1")
         product0(0, 1, "turn0")
-        add_att(1, 1, Q, G, Q)
+        add_att_shared(1, Q)
         quantize_att(0, 1, Q, G)
         stage1_quarter(1, 0, 0)
         quantize_att(1, 1, Q, G)
         stage1_quarter(1, 1)
         store0(0, 2)
+        store0(0, 3)
 
-        quantize(h_q[0], E4M3, h_g[0], 0, D)
+        quantize(h_q[0], E4M3, att_g[1, 1], D - P, D, 0)
+        quantize(h_q[0], E4M3, h_g[0], 0, D - P)
         open1(0, "ob0")
         quantize_dk(1, 0)
-        interleave_h1_gpsimd(dk_g[1], Q, D)
-        interleave_h1(scopy, 0, H1_FIRST)
-        finish0(0, 3)
+        interleave_gpsimd(dk_g[1], 1, Q, D)
+        interleave_h1(scopy, 0, Q)
         product0(1, 0, "acc3")
         finish0(0, 0)
         finish0(0, 1)
         round_quarter(scopy, 1, 0)
         round_quarter(scopy, 1, 1)
-        interleave_h1(scopy, H1_FIRST, Q)
-        turn(1, 0, "ob1")
-        turn(1, 2, "acc0")
+        turn(1, 0, 1, "acc2")
+        turn(1, 1, 2, "turn1")
+        product0(1, 1, "ob1")
+        turn(1, 2, 4, "acc0")
         finish0(1, 0)
-        product0(1, 1, "turn1")
-        open1(1, "acc2")
+        open1(1, "turn0")
         quantize(h_q[1], E4M3, h_g[1], 0, Q)
         group_dv(1, 0, 1)
         group_dv(1, 1, 2)
         quantize(h_q[1], E4M3, dk_g[1], Q, D, 0)
+        group_dk_quarter(scopy, 1, 0, 1)
         group_dv(1, 2, 4)
         quantize_dv(1, 0, 1)
         close1(0)
@@ -342,20 +371,19 @@ def tile_semanticgraph_pb_v_kernel(tc, q, k, h, cooccur, wv, bv, p, y, grad_out,
         quantize_dv(1, 1, 2)
         close1(1)
         quantize_dv(0, 2, 4)
-        open1(2, "turn0")
-        group_dk_quarter(scopy, 1, 0, 1)
+        open1(2, "acc1")
         finish1(0, nc.sync)
-        quantize_dv(1, 2, 4)
-        close1(2)
-        open1(3, "acc1")
-        close1(3)
-        group_dk_quarter(vcopy, 1, 1, 2)
         quantize_dk_tile(2)
         product0(1, 2, "acc3")
+        quantize_dv(1, 2, 4)
+        close1(2)
+        open1(3, "acc2")
+        close1(3)
+        group_dk_quarter(vcopy, 1, 1, 2)
         finish1(1, nc.sync)
         quantize_dk_tile(3)
         product0(1, 3, "acc0")
-        finish1(2, nc.sync)
         finish0(1, 2)
+        finish1(2, nc.sync)
         finish1(3, nc.scalar)
         finish0(1, 3)

@@ -10,7 +10,7 @@ J = 4
 G = P * J
 Q = G // 2
 WV_SCALAR = 320
-ADD_VECTOR = 208
+ADD_VECTOR = {(1, 0): 216, (0, Q): 192, (1, Q): 216}
 H0_FIRST = 288
 
 F32 = mybir.dt.float32
@@ -98,14 +98,17 @@ def tile_semanticgraph_pb_v_kernel(tc, q, k, h, cooccur, wv, bv, p, y, grad_out,
         dz2 = [sb([P, J, D], BF16, f"dz2_{i}") for i in range(2)]
         dz2_g = [sb([P, D * J], BF16, f"dz2_g{i}") for i in range(2)]
         dz2_q = [operand(D, f"dz2_q{i}") for i in range(2)]
-        att_g = {(i, hf): sb([P, G * J], BF16, f"att_g{i}{hf}") for i in range(2) for hf in range(2)}
+        att_g = {(i, hf): sb([P, G * J], BF16, f"att_g{i}{hf}") for i, hf in ((0, 0), (1, 0), (0, 1))}
         att_q = {(i, hf): operand(G, f"att_q{i}{hf}") for i in range(2) for hf in range(2)}
         wv_g = sb([P, D * J], BF16, "wv_g")
         wv_q = operand(D, "wv_q")
         h_g = [sb([P, D * J], BF16, f"h_g{hf}") for hf in range(2)]
         h_q = [operand(D, f"h_q{hf}") for hf in range(2)]
         dz1 = [sb([P, J, G], BF16, f"dz1_{hf}") for hf in range(2)]
-        dk_g = [sb([P, G * J], BF16, f"dk_g{hf}") for hf in range(2)]
+        dk_g = sb([P, G * J], BF16, "dk_g")
+        shared = [sb([P, J * (ADD_VECTOR[1, Q * x] + Q)], BF16, f"shared{x}") for x in range(2)]
+        att_quarter = {(0, Q): att_g[0, 1][:, J * Q :], (1, 0): shared[0][:, : J * Q], (1, Q): shared[1][:, : J * Q]}
+        dk_first = [shared[1 - u][:, J * ADD_VECTOR[1, Q * (1 - u)] :] for u in range(2)]
         dk_q = [operand(G, f"dk_q{hf}") for hf in range(2)]
         dv_g = [sb([P, D * J], BF16, f"dv_g{hf}") for hf in range(2)]
         dv_q = [operand(D, f"dv_q{hf}") for hf in range(2)]
@@ -137,17 +140,17 @@ def tile_semanticgraph_pb_v_kernel(tc, q, k, h, cooccur, wv, bv, p, y, grad_out,
             )
 
         def stage_c(i, k0, bank):
-            c_bank[i, k0] = psum.tile([P, J, ADD_VECTOR], BF16, name=bank)
+            c_bank[i, k0] = psum.tile([P, J, ADD_VECTOR[i, k0]], BF16, name=bank)
             for j in range(0, J, 2):
-                src = c_raw[i, 1][:, j : j + 2, k0 : k0 + ADD_VECTOR]
+                src = c_raw[i, 1][:, j : j + 2, k0 : k0 + ADD_VECTOR[i, k0]]
                 nc.tensor.matmul(c_bank[i, k0][:, j : j + 2, :], ident_bf[:], src, start=True, stop=True)
 
         def add_att_shared(i, k0):
-            k1 = k0 + ADD_VECTOR
+            k1 = k0 + ADD_VECTOR[i, k0]
             shares = ((nc.vector, k0, k1, c_bank[i, k0][:]), (nc.gpsimd, k1, k0 + Q, c_raw[i, 1][:, :, k1 : k0 + Q]))
             for engine, a, b, c in shares:
                 engine.tensor_tensor(
-                    out=att_g[i, 1][:, J * a : J * b].rearrange("p (c a j) -> p c j a", a=2, j=J),
+                    out=att_quarter[i, k0][:, J * (a - k0) : J * (b - k0)].rearrange("p (c a j) -> p c j a", a=2, j=J),
                     in0=p_raw[i, 1, k0][:, :, a - k0 : b - k0].rearrange("p j (c a) -> p c j a", a=2),
                     in1=c.rearrange("p j (c a) -> p c j a", a=2),
                     op=ALU.add,
@@ -233,21 +236,21 @@ def tile_semanticgraph_pb_v_kernel(tc, q, k, h, cooccur, wv, bv, p, y, grad_out,
 
         def group_dk(copy, u):
             copy(
-                out=dk_g[0][:, 2 * G * u : 2 * G * (u + 1)].rearrange("p (e a b s) -> p e a s b", e=2, b=2, s=J),
+                out=dk_first[u].rearrange("p (e a b s) -> p e a s b", e=2, b=2, s=J),
                 in_=dz1[0][:, :, 2 * P * u : 2 * P * (u + 1)].rearrange("p s (a b e) -> p e a s b", b=2, e=2),
             )
 
         def group_dk_quarter(copy, x, u0, u1):
             copy(
-                out=dk_g[1][:, G * (2 * x + u0) : G * (2 * x + u1)].rearrange("p (u a b s) -> p u a s b", a=P // 2, b=2, s=J),
+                out=dk_g[:, G * (2 * x + u0) : G * (2 * x + u1)].rearrange("p (u a b s) -> p u a s b", a=P // 2, b=2, s=J),
                 in_=dz1[1][:].rearrange("p s (u x a b) -> p x u a s b", u=2, x=2, b=2)[:, x, u0:u1],
             )
 
-        def quantize_dk(hf, n):
-            quantize(dk_q[hf], E5M2, dk_g[hf], Q * n, Q * (n + 1))
+        def quantize_dk_first(u):
+            quantize(dk_q[0], E5M2, dk_first[u], Q * u, Q * (u + 1), 0)
 
         def quantize_dk_tile(t):
-            quantize(dk_q[1], E5M2, dk_g[1], P * t, P * (t + 1))
+            quantize(dk_q[1], E5M2, dk_g, P * t, P * (t + 1))
 
         def quantize_dv(hf, s0, s1):
             quantize(dv_q[hf], E5M2, dv_g[hf], P * s0, P * s1)
@@ -311,7 +314,7 @@ def tile_semanticgraph_pb_v_kernel(tc, q, k, h, cooccur, wv, bv, p, y, grad_out,
         group_dk(scopy, 0)
         group_dk(vcopy, 1)
         quantize_att(0, 1, 0, Q)
-        quantize_dk(0, 1)
+        quantize_dk_first(1)
         product0(0, 2, "ob0")
         product0(0, 3, "ob1")
         stage1_quarter(0, 0, 0)
@@ -320,10 +323,10 @@ def tile_semanticgraph_pb_v_kernel(tc, q, k, h, cooccur, wv, bv, p, y, grad_out,
         interleave(scopy, h_g[0], h_raw[0], 0, H0_FIRST)
         add_att_shared(1, 0)
         quantize_dv(0, 0, 2)
-        quantize_att(1, 1, 0, Q)
+        quantize(att_q[1, 1], E4M3, att_quarter[1, 0], 0, Q)
         stage1_quarter(0, 1)
         stage_c(1, Q, "acc2")
-        interleave_gpsimd(att_g[1, 1], 0, D - P, D)
+        interleave_gpsimd(shared[0], 0, D - P, D)
         residual(0, 2)
         residual(0, 3)
         add_att_shared(0, Q)
@@ -331,22 +334,22 @@ def tile_semanticgraph_pb_v_kernel(tc, q, k, h, cooccur, wv, bv, p, y, grad_out,
         round_quarter(scopy, 0, 1)
         interleave(scopy, h_g[0], h_raw[0], H0_FIRST, D - P)
         group_dk_quarter(scopy, 0, 0, 2)
-        quantize_dk(0, 0)
+        quantize_dk_first(0)
         product0(0, 0, "turn1")
         product0(0, 1, "turn0")
         add_att_shared(1, Q)
         quantize_att(0, 1, Q, G)
         stage1_quarter(1, 0, 0)
-        quantize_att(1, 1, Q, G)
+        quantize(att_q[1, 1], E4M3, att_quarter[1, Q], Q, G, 0)
         stage1_quarter(1, 1)
         store0(0, 2)
         store0(0, 3)
 
-        quantize(h_q[0], E4M3, att_g[1, 1], D - P, D, 0)
+        quantize(h_q[0], E4M3, shared[0], D - P, D, 0)
         quantize(h_q[0], E4M3, h_g[0], 0, D - P)
         open1(0, "ob0")
-        quantize_dk(1, 0)
-        interleave_gpsimd(dk_g[1], 1, Q, D)
+        quantize(dk_q[1], E5M2, dk_g, 0, Q)
+        interleave_gpsimd(dk_g, 1, Q, D)
         interleave_h1(scopy, 0, Q)
         product0(1, 0, "acc3")
         finish0(0, 0)
@@ -362,7 +365,7 @@ def tile_semanticgraph_pb_v_kernel(tc, q, k, h, cooccur, wv, bv, p, y, grad_out,
         quantize(h_q[1], E4M3, h_g[1], 0, Q)
         group_dv(1, 0, 1)
         group_dv(1, 1, 2)
-        quantize(h_q[1], E4M3, dk_g[1], Q, D, 0)
+        quantize(h_q[1], E4M3, dk_g, Q, D, 0)
         group_dk_quarter(scopy, 1, 0, 1)
         group_dv(1, 2, 4)
         quantize_dv(1, 0, 1)

@@ -32,7 +32,7 @@ def tile_semanticgraph_pb_v_kernel(tc, q, k, h, cooccur, wv, bv, p, y, grad_out,
         psum = ctx.enter_context(tc.psum_pool(name="psum", bufs=1))
 
         def sb(shape, dtype, name):
-            return keep.tile(shape, dtype, name=name, align_bytes=64)
+            return keep.tile(shape, dtype, name=name, align_bytes=256)
 
         ctx.enter_context(tc.manual_schedule())
 

@@ -9,9 +9,8 @@ P = 128
 J = 4
 G = P * J
 Q = G // 2
-WV_SCALAR = 320
-ADD_VECTOR = {(1, 0): 216, (0, Q): 192, (1, Q): 216}
-H0_FIRST = 288
+ADD_VECTOR = {(1, 0): 216, (1, 1): 216, (0, 2): 216, (1, 2): 216, (0, 3): 216}
+TIED = ((0, 0), (1, 0), (1, 1), (0, 2), (1, 2))
 
 F32 = mybir.dt.float32
 BF16 = mybir.dt.bfloat16
@@ -44,8 +43,8 @@ def tile_semanticgraph_pb_v_kernel(tc, q, k, h, cooccur, wv, bv, p, y, grad_out,
         def rows(ap, i, c0, c1):
             return ap[G * i : G * (i + 1), c0:c1].rearrange("(p j) w -> p j w", j=J)
 
-        def pairs(ap, x):
-            return ap[G + Q * x : G + Q * (x + 1), :].rearrange("(p u) w -> p u w", u=2)
+        def tiles(ap, t0, t1):
+            return ap[G + P * t0 : G + P * t1, :].rearrange("(t p) w -> p t w", p=P)
 
         g_raw, y_raw, p_raw, c_raw, h_raw = {}, {}, {}, {}, {}
 
@@ -56,29 +55,32 @@ def tile_semanticgraph_pb_v_kernel(tc, q, k, h, cooccur, wv, bv, p, y, grad_out,
         def load_c(i, hf):
             c_raw[i, hf] = load(rows(cooccur, i, G * hf, G * (hf + 1)), [P, J, G], BF16, f"c_{i}{hf}")
 
-        def load_p(i, hf, k0, k1):
-            p_raw[i, hf, k0] = load(rows(p, i, G * hf + k0, G * hf + k1), [P, J, k1 - k0], F32, f"p_{i}{hf}_{k0}")
+        def load_p(i, k0, k1):
+            t = load(rows(p, i, k0, k1), [P, J, k1 - k0], F32, f"p_{i}_{k0}")
+            for a in range(k0, k1, P):
+                p_raw[i, a] = t[:, :, a - k0 :]
 
         def load_h(hf):
             h_raw[hf] = load(rows(h, hf, 0, D), [P, J, D], BF16, f"h_raw{hf}")
 
         load_yg(0)
-        load_c(0, 0)
-        load_p(0, 0, 0, G)
         load_yg(1)
+        load_c(0, 0)
+        load_p(0, 0, G)
         load_c(1, 0)
-        load_p(1, 0, 0, Q)
-        load_p(1, 0, Q, G)
+        load_p(1, 0, Q)
+        load_p(1, Q, G)
         wv_raw = load(rows(wv, 0, 0, D), [P, J, D], BF16, "wv_raw")
         load_c(0, 1)
-        load_p(0, 1, 0, Q)
+        load_p(0, G, G + Q)
         load_c(1, 1)
-        load_p(1, 1, 0, Q)
+        load_p(1, G, G + Q)
         load_h(0)
-        load_p(0, 1, Q, G)
-        load_p(1, 1, Q, G)
+        load_p(0, G + Q, N)
+        load_p(1, G + Q, N - P)
+        load_p(1, N - P, N)
         load_h(1)
-        g_pairs = [load(pairs(grad_out, x), [P, 2, D], BF16, f"g_pairs{x}") for x in range(2)]
+        g_tiles = [load(tiles(grad_out, 2 * x, 2 * x + 2), [P, 2, D], BF16, f"g_tiles{x}") for x in range(2)]
 
         ident = sb([P, P], F32, "ident")
         make_identity(nc, ident[:])
@@ -95,92 +97,96 @@ def tile_semanticgraph_pb_v_kernel(tc, q, k, h, cooccur, wv, bv, p, y, grad_out,
                 out=codes[:, c0:c1].bitcast(fmt), scales=scales[:, c0:c1], in_=grouped[:, J * g0 : J * (g0 + c1 - c0)]
             )
 
+        step = [sb([P, J, D], BF16, f"step_{i}") for i in range(2)]
         dz2 = [sb([P, J, D], BF16, f"dz2_{i}") for i in range(2)]
         dz2_g = [sb([P, D * J], BF16, f"dz2_g{i}") for i in range(2)]
         dz2_q = [operand(D, f"dz2_q{i}") for i in range(2)]
-        att_g = {(i, hf): sb([P, G * J], BF16, f"att_g{i}{hf}") for i, hf in ((0, 0), (1, 0), (0, 1))}
-        att_q = {(i, hf): operand(G, f"att_q{i}{hf}") for i in range(2) for hf in range(2)}
-        wv_g = sb([P, D * J], BF16, "wv_g")
+        att_q = {(i, x): operand(Q, f"att_q{i}{x}") for i in range(2) for x in range(4)}
         wv_q = operand(D, "wv_q")
         h_g = [sb([P, D * J], BF16, f"h_g{hf}") for hf in range(2)]
         h_q = [operand(D, f"h_q{hf}") for hf in range(2)]
         dz1 = [sb([P, J, G], BF16, f"dz1_{hf}") for hf in range(2)]
-        dk_g = sb([P, G * J], BF16, "dk_g")
-        shared = [sb([P, J * (ADD_VECTOR[1, Q * x] + Q)], BF16, f"shared{x}") for x in range(2)]
-        att_quarter = {(0, Q): att_g[0, 1][:, J * Q :], (1, 0): shared[0][:, : J * Q], (1, Q): shared[1][:, : J * Q]}
-        dk_first = [shared[1 - u][:, J * ADD_VECTOR[1, Q * (1 - u)] :] for u in range(2)]
         dk_q = [operand(G, f"dk_q{hf}") for hf in range(2)]
         dv_g = [sb([P, D * J], BF16, f"dv_g{hf}") for hf in range(2)]
         dv_q = [operand(D, f"dv_q{hf}") for hf in range(2)]
         o0 = [sb([P, J, D], F32, f"o0_{hf}") for hf in range(2)]
         o1 = sb([P, J, D], F32, "o1")
+        att_g = {(i, x): sb([P, Q * J], BF16, f"att_g{i}{x}")[:] for i in range(2) for x in range(4) if (i, x) not in TIED}
+        share_att = sb([P, J * (ADD_VECTOR[1, 1] + ADD_VECTOR[1, 0] + Q)], BF16, "share_att")
+        for n, block in enumerate(((1, 1), (1, 0), (0, 0))):
+            at = J * ADD_VECTOR[1, 0] * n
+            att_g[block] = share_att[:, at : at + J * Q]
+
+        share_wv = sb([P, J * (ADD_VECTOR[0, 2] + D)], BF16, "share_wv")
+        att_g[0, 2], wv_g = share_wv[:, : J * Q], share_wv[:, J * ADD_VECTOR[0, 2] :]
+        share_dk = sb([P, J * (ADD_VECTOR[1, 2] + Q)], BF16, "share_dk")
+        att_g[1, 2] = share_dk[:, : J * Q]
+        dk_first = [sb([P, J * Q], BF16, "dk_first0")[:], share_dk[:, J * ADD_VECTOR[1, 2] :]]
+        dk_g = sb([P, G * J], BF16, "dk_g")
         c_bank = {}
         vcopy, scopy = nc.vector.tensor_copy, nc.scalar.copy
 
-        def mask_and_sort(i, c0, c1):
-            nc.vector.scalar_tensor_tensor(
-                out=dz2[i][:, :, c0:c1],
-                in0=y_raw[i][:, :, c0:c1],
-                scalar=0.0,
-                in1=g_raw[i][:, :, c0:c1],
-                op0=ALU.is_gt,
-                op1=ALU.mult,
+        def positive(i):
+            nc.vector.tensor_scalar(out=step[i][:], in0=y_raw[i][:], scalar1=0.0, scalar2=None, op0=ALU.is_gt)
+
+        def mask(i, c0, c1):
+            nc.vector.tensor_tensor(
+                out=dz2[i][:, :, c0:c1], in0=step[i][:, :, c0:c1], in1=g_raw[i][:, :, c0:c1], op=ALU.mult
             )
-            scopy(
+
+        def sort(copy, i, c0, c1):
+            copy(
                 out=dz2_g[i][:].rearrange("p (s m j) -> p m j s", s=J, j=J)[:, c0 // J : c1 // J],
                 in_=dz2[i][:, :, c0:c1].rearrange("p j (m s) -> p m j s", s=J),
             )
 
-        def add_att(i, hf, k0, k1, piece):
+        def walk(ap):
+            return ap.rearrange("p j (c a) -> p c j a", a=2)
+
+        def grouped(ap):
+            return ap.rearrange("p (c a j) -> p c j a", a=2, j=J)
+
+        def c_cols(i, k0, k1):
+            return c_raw[i, k0 // G][:, :, k0 % G : k0 % G + k1 - k0]
+
+        def add_att(i, k0, k1):
+            out = att_g[i, k0 // Q][:, J * (k0 % Q) : J * (k0 % Q + k1 - k0)]
             nc.vector.tensor_tensor(
-                out=att_g[i, hf][:, J * k0 : J * k1].rearrange("p (c a j) -> p c j a", a=2, j=J),
-                in0=p_raw[i, hf, piece][:, :, k0 - piece : k1 - piece].rearrange("p j (c a) -> p c j a", a=2),
-                in1=c_raw[i, hf][:, :, k0:k1].rearrange("p j (c a) -> p c j a", a=2),
-                op=ALU.add,
+                out=grouped(out), in0=walk(p_raw[i, k0][:, :, : k1 - k0]), in1=walk(c_cols(i, k0, k1)), op=ALU.add
             )
 
-        def stage_c(i, k0, bank):
-            c_bank[i, k0] = psum.tile([P, J, ADD_VECTOR[i, k0]], BF16, name=bank)
+        def stage_c(i, x, bank):
+            c_bank[i, x] = psum.tile([P, J, ADD_VECTOR[i, x]], BF16, name=bank)
+            src = c_cols(i, Q * x, Q * x + ADD_VECTOR[i, x])
             for j in range(0, J, 2):
-                src = c_raw[i, 1][:, j : j + 2, k0 : k0 + ADD_VECTOR[i, k0]]
-                nc.tensor.matmul(c_bank[i, k0][:, j : j + 2, :], ident_bf[:], src, start=True, stop=True)
+                nc.tensor.matmul(c_bank[i, x][:, j : j + 2, :], ident_bf[:], src[:, j : j + 2, :], start=True, stop=True)
 
-        def add_att_shared(i, k0):
-            k1 = k0 + ADD_VECTOR[i, k0]
-            shares = ((nc.vector, k0, k1, c_bank[i, k0][:]), (nc.gpsimd, k1, k0 + Q, c_raw[i, 1][:, :, k1 : k0 + Q]))
+        def add_att_shared(i, x):
+            n = ADD_VECTOR[i, x]
+            shares = ((nc.vector, 0, n, c_bank[i, x][:]), (nc.gpsimd, n, Q, c_cols(i, Q * x + n, Q * (x + 1))))
             for engine, a, b, c in shares:
                 engine.tensor_tensor(
-                    out=att_quarter[i, k0][:, J * (a - k0) : J * (b - k0)].rearrange("p (c a j) -> p c j a", a=2, j=J),
-                    in0=p_raw[i, 1, k0][:, :, a - k0 : b - k0].rearrange("p j (c a) -> p c j a", a=2),
-                    in1=c.rearrange("p j (c a) -> p c j a", a=2),
+                    out=grouped(att_g[i, x][:, J * a : J * b]),
+                    in0=walk(p_raw[i, Q * x][:, :, a:b]),
+                    in1=walk(c),
                     op=ALU.add,
                 )
 
         def interleave(copy, dst, src, c0, c1):
-            copy(
-                out=dst[:, J * c0 : J * c1].rearrange("p (c a j) -> p c j a", a=2, j=J),
-                in_=src[:, :, c0:c1].rearrange("p j (c a) -> p c j a", a=2),
-            )
+            copy(out=grouped(dst[:, J * c0 : J * c1]), in_=walk(src[:, :, c0:c1]))
 
-        def interleave_h1(copy, c0, c1):
-            copy(
-                out=h_g[1][:, J * c0 : J * c1].rearrange("p (c a u e) -> p c u e a", a=2, u=2, e=2),
-                in_=h_raw[1][:, :, c0:c1].rearrange("p (e u) (c a) -> p c u e a", a=2, u=2),
-            )
-
-        def interleave_gpsimd(dst, hf, c0, c1):
-            rows_of_word = "p (u e) c -> p c u e" if hf == 0 else "p (e u) c -> p c u e"
+        def interleave_gpsimd(dst, src, c0, c1):
             nc.gpsimd.tensor_scalar(
-                out=dst[:, : J * (c1 - c0)].rearrange("p (c u e) -> p c u e", u=2, e=2),
-                in0=h_raw[hf][:, :, c0:c1].rearrange(rows_of_word, u=2),
+                out=dst[:, : J * (c1 - c0)].rearrange("p (c j) -> p c j", j=J),
+                in0=src[:, :, c0:c1].rearrange("p j c -> p c j"),
                 scalar1=1.0,
                 scalar2=0.0,
                 op0=ALU.mult,
                 op1=ALU.add,
             )
 
-        def quantize_att(i, hf, k0, k1):
-            quantize(att_q[i, hf], E4M3, att_g[i, hf], k0, k1)
+        def quantize_att(i, k0, k1):
+            quantize(att_q[i, k0 // Q], E4M3, att_g[i, k0 // Q], k0 % Q, k0 % Q + k1 - k0)
 
         def mm(out, stationary, tile, moving, c0, c1, start, stop):
             nc.tensor.matmul_mx(
@@ -193,31 +199,23 @@ def tile_semanticgraph_pb_v_kernel(tc, q, k, h, cooccur, wv, bv, p, y, grad_out,
                 stop=stop,
             )
 
-        acc, acc_q, turned, bank0, bank1 = {}, {}, {}, {}, {}
+        acc, turned, bank0, bank1 = {}, {}, {}, {}
 
-        def stage1(i):
+        def stage1(i, k0, k1, banks=None):
+            if i == 0:
+                acc[k0] = [psum.tile([P, J // len(banks), k1 - k0], F32, name=b) for b in banks]
+            per = J // len(acc[k0])
             for s in range(J):
-                if i == 0:
-                    acc[s] = psum.tile([P, G], F32, name=f"acc{s}")
-                mm(acc[s][:], dz2_q[i], s, att_q[i, 0], 0, G, i == 0, i == 1)
+                n, a = divmod(s, per)
+                c0 = k0 % Q
+                mm(acc[k0][n][:, a, :], dz2_q[i], s, att_q[i, k0 // Q], c0, c0 + k1 - k0, i + a == 0, i + a == per)
 
-        def stage1_quarter(x, i, first=None):
-            for s in range(J):
-                n, a = divmod(s, 2)
-                if i == 0 and a == 0:
-                    acc_q[x, n] = psum.tile([P, 2, Q], F32, name=f"acc{first + n}")
-                mm(acc_q[x, n][:, a, :], dz2_q[i], s, att_q[i, 1], Q * x, Q * (x + 1), i + a == 0, i + a == 2)
-
-        def round_dz1(copy, s):
+        def round_dz1(copy, k0, k1, n):
+            per = J // len(acc[k0])
+            dst = dz1[k0 // G][:, per * n : per * (n + 1), :].rearrange("p s (u w e) -> p s u w e", u=2, e=2)
             copy(
-                out=dz1[0][:, s, :].rearrange("p (u w e) -> p u w e", u=2, e=2),
-                in_=acc[s][:].rearrange("p (w u e) -> p u w e", u=2, e=2),
-            )
-
-        def round_quarter(copy, x, n):
-            copy(
-                out=dz1[1][:, 2 * n : 2 * n + 2, :].rearrange("p s (u x m) -> p x s u m", u=2, x=2)[:, x],
-                in_=acc_q[x, n][:].rearrange("p s (m u) -> p s u m", u=2),
+                out=dst[:, :, :, k0 % G // J : (k0 % G + k1 - k0) // J],
+                in_=acc[k0][n][:].rearrange("p s (w u e) -> p s u w e", u=2, e=2),
             )
 
         def turn(hf, s0, s1, bank):
@@ -228,29 +226,30 @@ def tile_semanticgraph_pb_v_kernel(tc, q, k, h, cooccur, wv, bv, p, y, grad_out,
                 for u in range(2):
                     nc.tensor.transpose(t[:, s - s0, u, :], words[:, P * u : P * (u + 1)], ident[:])
 
-        def group_dv(hf, s0, s1):
-            scopy(
+        def group_dv(copy, hf, s0, s1):
+            copy(
                 out=dv_g[hf][:, G * s0 : G * s1].bitcast(F32).rearrange("p (s m u) -> p s m u", m=P, u=2),
                 in_=turned[hf, s0][:, : s1 - s0].rearrange("p s u m -> p s m u"),
             )
 
-        def group_dk(copy, u):
+        def group_dk(copy, x, u):
             copy(
-                out=dk_first[u].rearrange("p (e a b s) -> p e a s b", e=2, b=2, s=J),
-                in_=dz1[0][:, :, 2 * P * u : 2 * P * (u + 1)].rearrange("p s (a b e) -> p e a s b", b=2, e=2),
+                out=dk_first[u].rearrange("p (e x a b s) -> p x e a s b", e=2, x=2, b=2, s=J)[:, x],
+                in_=dz1[0][:, :, Q * u : Q * (u + 1)].rearrange("p s (x a b e) -> p x e a s b", x=2, b=2, e=2)[:, x],
             )
 
-        def group_dk_quarter(copy, x, u0, u1):
+        def group_dk_tiles(copy, t0, t1):
+            w0, w1 = P * t0 // J, P * t1 // J
             copy(
-                out=dk_g[:, G * (2 * x + u0) : G * (2 * x + u1)].rearrange("p (u a b s) -> p u a s b", a=P // 2, b=2, s=J),
-                in_=dz1[1][:].rearrange("p s (u x a b) -> p x u a s b", u=2, x=2, b=2)[:, x, u0:u1],
+                out=dk_g[:, G * t0 : G * t1].rearrange("p (w u e s) -> p u w s e", u=2, e=2, s=J),
+                in_=dz1[1][:].rearrange("p s (u w e) -> p u w s e", u=2, e=2)[:, :, w0:w1],
             )
 
         def quantize_dk_first(u):
             quantize(dk_q[0], E5M2, dk_first[u], Q * u, Q * (u + 1), 0)
 
-        def quantize_dk_tile(t):
-            quantize(dk_q[1], E5M2, dk_g, P * t, P * (t + 1))
+        def quantize_dk(t0, t1):
+            quantize(dk_q[1], E5M2, dk_g, P * t0, P * t1)
 
         def quantize_dv(hf, s0, s1):
             quantize(dv_q[hf], E5M2, dv_g[hf], P * s0, P * s1)
@@ -260,16 +259,16 @@ def tile_semanticgraph_pb_v_kernel(tc, q, k, h, cooccur, wv, bv, p, y, grad_out,
             mm(bank0[hf, t][:], dk_q[hf], t, wv_q, 0, D, True, True)
 
         def residual(hf, t):
-            g_tile = g_raw[0][:, t, :] if hf == 0 else g_pairs[t // 2][:, t % 2, :]
+            g_tile = g_raw[0][:, t, :] if hf == 0 else g_tiles[t // 2][:, t % 2, :]
             nc.vector.tensor_tensor(out=o0[hf][:, t, :], in0=bank0[hf, t][:], in1=g_tile, op=ALU.add)
 
-        def store0(hf, t):
-            dst = rows(out_0, 0, 0, D)[:, t : t + 1, :] if hf == 0 else pairs(out_0, t // 2)[:, t % 2 : t % 2 + 1, :]
-            nc.sync.dma_start(out=dst, in_=o0[hf][:, t : t + 1, :])
+        def store0(hf, t0, t1):
+            dst = rows(out_0, 0, 0, D)[:, t0:t1, :] if hf == 0 else tiles(out_0, t0, t1)
+            nc.sync.dma_start(out=dst, in_=o0[hf][:, t0:t1, :])
 
         def finish0(hf, t):
             residual(hf, t)
-            store0(hf, t)
+            store0(hf, t, t + 1)
 
         def open1(s, bank):
             bank1[s] = psum.tile([P, D], F32, name=bank)
@@ -278,115 +277,129 @@ def tile_semanticgraph_pb_v_kernel(tc, q, k, h, cooccur, wv, bv, p, y, grad_out,
         def close1(s):
             mm(bank1[s][:], dv_q[1], s, h_q[1], 0, D, False, True)
 
-        def finish1(s, queue):
-            scopy(out=o1[:, s, :], in_=bank1[s][:])
+        def finish1(copy, s, queue):
+            copy(out=o1[:, s, :], in_=bank1[s][:])
             queue.dma_start(out=rows(out_1, 0, 0, D)[:, s : s + 1, :], in_=o1[:, s : s + 1, :])
 
-        for c0 in range(0, D, 2 * P):
-            mask_and_sort(0, c0, c0 + 2 * P)
-        add_att(0, 0, 0, Q, 0)
-        add_att(0, 0, Q, G, 0)
-        quantize_att(0, 0, 0, Q)
+        positive(0)
+        for c0 in range(0, D, Q):
+            mask(0, c0, c0 + Q)
+            sort(scopy, 0, c0, c0 + Q)
+        positive(1)
+        mask(1, 0, Q)
+        sort(scopy, 1, 0, Q)
+        mask(1, Q, D)
         quantize(dz2_q[0], E5M2, dz2_g[0], 0, D)
-        for c0 in range(0, D, P):
-            mask_and_sort(1, c0, c0 + P)
-        quantize_att(0, 0, Q, G)
-        stage1(0)
-        add_att(1, 0, 0, Q, 0)
+        sort(vcopy, 1, Q, D)
         quantize(dz2_q[1], E5M2, dz2_g[1], 0, D)
-        add_att(1, 0, Q, G, Q)
-        quantize_att(1, 0, 0, Q)
-        quantize_att(1, 0, Q, G)
-        stage1(1)
-
-        interleave(scopy, wv_g, wv_raw, 0, D // 2)
-        interleave(scopy, wv_g, wv_raw, D // 2, WV_SCALAR)
-        interleave(vcopy, wv_g, wv_raw, WV_SCALAR, D)
-        quantize(wv_q, E4M3, wv_g, 0, D // 2)
-        quantize(wv_q, E4M3, wv_g, D // 2, D)
-        for s, copy in enumerate((scopy, vcopy, scopy, scopy)):
-            round_dz1(copy, s)
-        add_att(0, 1, 0, Q, 0)
-        turn(0, 0, 2, "turn1")
-        turn(0, 2, 4, "turn0")
-        stage_c(1, 0, "acc2")
-        stage_c(0, Q, "acc3")
-        group_dk(scopy, 0)
-        group_dk(vcopy, 1)
-        quantize_att(0, 1, 0, Q)
-        quantize_dk_first(1)
-        product0(0, 2, "ob0")
-        product0(0, 3, "ob1")
-        stage1_quarter(0, 0, 0)
-        group_dv(0, 0, 2)
-        group_dv(0, 2, 4)
-        interleave(scopy, h_g[0], h_raw[0], 0, H0_FIRST)
+        stage_c(1, 0, "b4")
+        stage_c(1, 1, "b5")
+        add_att(0, 0, Q)
+        add_att(0, Q, G)
+        quantize_att(0, 0, Q)
         add_att_shared(1, 0)
-        quantize_dv(0, 0, 2)
-        quantize(att_q[1, 1], E4M3, att_quarter[1, 0], 0, Q)
-        stage1_quarter(0, 1)
-        stage_c(1, Q, "acc2")
-        interleave_gpsimd(shared[0], 0, D - P, D)
-        residual(0, 2)
-        residual(0, 3)
-        add_att_shared(0, Q)
-        round_quarter(scopy, 0, 0)
-        round_quarter(scopy, 0, 1)
-        interleave(scopy, h_g[0], h_raw[0], H0_FIRST, D - P)
-        group_dk_quarter(scopy, 0, 0, 2)
+        quantize_att(0, Q, G)
+        stage1(0, 0, Q, ("b0", "b1"))
+        stage1(0, Q, G, ("b2", "b3"))
+        quantize_att(1, 0, Q)
+        stage1(1, 0, Q)
+        add_att_shared(1, 1)
+        round_dz1(scopy, 0, Q, 0)
+        round_dz1(scopy, 0, Q, 1)
+        interleave(vcopy, wv_g, wv_raw, 0, P)
+        quantize_att(1, Q, G)
+        stage1(1, Q, G)
+        stage_c(0, 2, "b4")
+        stage_c(0, 3, "b0")
+        interleave(vcopy, wv_g, wv_raw, P, D)
+        group_dk(scopy, 0, 0)
+        group_dk(vcopy, 0, 1)
+        quantize(wv_q, E4M3, wv_g, 0, Q)
+        add_att_shared(0, 2)
+        round_dz1(scopy, Q, G, 0)
+        round_dz1(scopy, Q, G, 1)
+        turn(0, 0, 2, "b5")
+        stage_c(1, 2, "b7")
+        turn(0, 2, 4, "b6")
+        quantize(wv_q, E4M3, wv_g, Q, D)
+        group_dk(vcopy, 1, 1)
+        group_dk(scopy, 1, 0)
+        quantize_att(0, G, G + Q)
+        stage1(0, G, G + Q, ("b2", "b3"))
+        quantize_dk_first(1)
+        product0(0, 2, "b4")
+        product0(0, 3, "b1")
+        group_dv(scopy, 0, 0, 2)
+        group_dv(scopy, 0, 2, 4)
+        add_att_shared(1, 2)
         quantize_dk_first(0)
-        product0(0, 0, "turn1")
-        product0(0, 1, "turn0")
-        add_att_shared(1, Q)
-        quantize_att(0, 1, Q, G)
-        stage1_quarter(1, 0, 0)
-        quantize(att_q[1, 1], E4M3, att_quarter[1, Q], Q, G, 0)
-        stage1_quarter(1, 1)
-        store0(0, 2)
-        store0(0, 3)
-
-        quantize(h_q[0], E4M3, shared[0], D - P, D, 0)
+        quantize_att(1, G, G + Q)
+        stage1(1, G, G + Q)
+        interleave(scopy, h_g[0], h_raw[0], 0, D - P)
+        interleave_gpsimd(att_g[1, 2], h_raw[0], D - P, D)
+        residual(0, 2)
+        add_att_shared(0, 3)
+        round_dz1(scopy, G, G + Q, 0)
+        round_dz1(scopy, G, G + Q, 1)
+        product0(0, 0, "b2")
+        product0(0, 1, "b0")
+        group_dk_tiles(scopy, 0, 2)
+        add_att(1, G + Q, N - P)
+        quantize_att(0, G + Q, N)
+        stage1(0, G + Q, N - P, ("b7",))
+        stage1(0, N - P, N, ("b4", "b5"))
+        add_att(1, N - P, N)
+        quantize_att(1, G + Q, N - P)
+        stage1(1, G + Q, N - P)
+        quantize(h_q[0], E4M3, att_g[1, 2], D - P, D, 0)
+        quantize_att(1, N - P, N)
+        stage1(1, N - P, N)
+        interleave(scopy, h_g[1], h_raw[1], 0, P)
+        quantize_dv(0, 0, 2)
         quantize(h_q[0], E4M3, h_g[0], 0, D - P)
-        open1(0, "ob0")
-        quantize(dk_q[1], E5M2, dk_g, 0, Q)
-        interleave_gpsimd(dk_g, 1, Q, D)
-        interleave_h1(scopy, 0, Q)
-        product0(1, 0, "acc3")
+        quantize_dk(0, 2)
+        interleave_gpsimd(dk_g, h_raw[1], Q, D)
+        open1(0, "b3")
+        product0(1, 0, "b6")
+        round_dz1(scopy, G + Q, N - P, 0)
+        round_dz1(scopy, N - P, N, 0)
+        round_dz1(scopy, N - P, N, 1)
+        interleave(scopy, h_g[1], h_raw[1], P, Q)
+        residual(0, 3)
+        store0(0, 2, 4)
         finish0(0, 0)
         finish0(0, 1)
-        round_quarter(scopy, 1, 0)
-        round_quarter(scopy, 1, 1)
-        turn(1, 0, 1, "acc2")
-        turn(1, 1, 2, "turn1")
-        product0(1, 1, "ob1")
-        turn(1, 2, 4, "acc0")
+        product0(1, 1, "b1")
+        turn(1, 0, 1, "b7")
+        turn(1, 1, 2, "b4")
+        turn(1, 2, 4, "b5")
+        open1(1, "b2")
+        group_dv(scopy, 1, 0, 1)
+        group_dv(scopy, 1, 1, 2)
         finish0(1, 0)
-        open1(1, "turn0")
-        quantize(h_q[1], E4M3, h_g[1], 0, Q)
-        group_dv(1, 0, 1)
-        group_dv(1, 1, 2)
         quantize(h_q[1], E4M3, dk_g, Q, D, 0)
-        group_dk_quarter(scopy, 1, 0, 1)
-        group_dv(1, 2, 4)
+        quantize(h_q[1], E4M3, h_g[1], 0, Q)
         quantize_dv(1, 0, 1)
         close1(0)
-        finish0(1, 1)
+        group_dv(scopy, 1, 2, 4)
+        group_dk_tiles(scopy, 2, 3)
+        group_dk_tiles(scopy, 3, 4)
         quantize_dv(1, 1, 2)
         close1(1)
+        finish0(1, 1)
+        quantize_dk(2, 3)
+        product0(1, 2, "b0")
         quantize_dv(0, 2, 4)
-        open1(2, "acc1")
-        finish1(0, nc.sync)
-        quantize_dk_tile(2)
-        product0(1, 2, "acc3")
+        open1(2, "b6")
+        open1(3, "b7")
         quantize_dv(1, 2, 4)
+        finish1(scopy, 0, nc.sync)
         close1(2)
-        open1(3, "acc2")
+        quantize_dk(3, 4)
+        product0(1, 3, "b4")
         close1(3)
-        group_dk_quarter(vcopy, 1, 1, 2)
-        finish1(1, nc.sync)
-        quantize_dk_tile(3)
-        product0(1, 3, "acc0")
+        finish1(scopy, 1, nc.sync)
         finish0(1, 2)
-        finish1(2, nc.sync)
-        finish1(3, nc.scalar)
+        finish1(scopy, 2, nc.sync)
         finish0(1, 3)
+        finish1(scopy, 3, nc.scalar)

@@ -9,8 +9,7 @@ P = 128
 J = 4
 G = P * J
 Q = G // 2
-ADD_VECTOR = {(1, 0): 216, (1, 1): 216, (0, 2): 216, (1, 2): 216, (0, 3): 216}
-TIED = ((0, 0), (1, 0), (1, 1), (0, 2), (1, 2))
+ADD_VECTOR = 216
 
 F32 = mybir.dt.float32
 BF16 = mybir.dt.bfloat16
@@ -111,18 +110,17 @@ def tile_semanticgraph_pb_v_kernel(tc, q, k, h, cooccur, wv, bv, p, y, grad_out,
         dv_q = [operand(D, f"dv_q{hf}") for hf in range(2)]
         o0 = [sb([P, J, D], F32, f"o0_{hf}") for hf in range(2)]
         o1 = sb([P, J, D], F32, "o1")
-        att_g = {(i, x): sb([P, Q * J], BF16, f"att_g{i}{x}")[:] for i in range(2) for x in range(4) if (i, x) not in TIED}
-        share_att = sb([P, J * (ADD_VECTOR[1, 1] + ADD_VECTOR[1, 0] + Q)], BF16, "share_att")
-        for n, block in enumerate(((1, 1), (1, 0), (0, 0))):
-            at = J * ADD_VECTOR[1, 0] * n
-            att_g[block] = share_att[:, at : at + J * Q]
-
-        share_wv = sb([P, J * (ADD_VECTOR[0, 2] + D)], BF16, "share_wv")
-        att_g[0, 2], wv_g = share_wv[:, : J * Q], share_wv[:, J * ADD_VECTOR[0, 2] :]
-        share_dk = sb([P, J * (ADD_VECTOR[1, 2] + Q)], BF16, "share_dk")
-        att_g[1, 2] = share_dk[:, : J * Q]
-        dk_first = [sb([P, J * Q], BF16, "dk_first0")[:], share_dk[:, J * ADD_VECTOR[1, 2] :]]
         dk_g = sb([P, G * J], BF16, "dk_g")
+        att_g = {block: sb([P, Q * J], BF16, f"att_g{block[0]}{block[1]}")[:] for block in ((0, 1), (0, 3), (1, 3))}
+        lead = J * ADD_VECTOR
+        share_att = sb([P, 2 * lead + J * Q], BF16, "share_att")
+        for n, block in enumerate(((1, 1), (1, 0), (0, 0))):
+            att_g[block] = share_att[:, lead * n : lead * n + J * Q]
+        share_wv = sb([P, lead + J * D], BF16, "share_wv")
+        att_g[0, 2], wv_g = share_wv[:, : J * Q], share_wv[:, lead:]
+        share_dk = sb([P, lead + J * Q], BF16, "share_dk")
+        att_g[1, 2] = share_dk[:, : J * Q]
+        dk_first = [sb([P, J * Q], BF16, "dk_first0")[:], share_dk[:, lead:]]
         c_bank = {}
         vcopy, scopy = nc.vector.tensor_copy, nc.scalar.copy
 
@@ -156,13 +154,13 @@ def tile_semanticgraph_pb_v_kernel(tc, q, k, h, cooccur, wv, bv, p, y, grad_out,
             )
 
         def stage_c(i, x, bank):
-            c_bank[i, x] = psum.tile([P, J, ADD_VECTOR[i, x]], BF16, name=bank)
-            src = c_cols(i, Q * x, Q * x + ADD_VECTOR[i, x])
+            c_bank[i, x] = psum.tile([P, J, ADD_VECTOR], BF16, name=bank)
+            src = c_cols(i, Q * x, Q * x + ADD_VECTOR)
             for j in range(0, J, 2):
                 nc.tensor.matmul(c_bank[i, x][:, j : j + 2, :], ident_bf[:], src[:, j : j + 2, :], start=True, stop=True)
 
         def add_att_shared(i, x):
-            n = ADD_VECTOR[i, x]
+            n = ADD_VECTOR
             shares = ((nc.vector, 0, n, c_bank[i, x][:]), (nc.gpsimd, n, Q, c_cols(i, Q * x + n, Q * (x + 1))))
             for engine, a, b, c in shares:
                 engine.tensor_tensor(
@@ -201,22 +199,21 @@ def tile_semanticgraph_pb_v_kernel(tc, q, k, h, cooccur, wv, bv, p, y, grad_out,
 
         acc, turned, bank0, bank1 = {}, {}, {}, {}
 
-        def stage1(i, k0, k1, banks=None):
+        def stage1(i, x, banks=None):
             if i == 0:
-                acc[k0] = [psum.tile([P, J // len(banks), k1 - k0], F32, name=b) for b in banks]
-            per = J // len(acc[k0])
+                acc[x] = [psum.tile([P, 2, Q], F32, name=bank) for bank in banks]
             for s in range(J):
-                n, a = divmod(s, per)
-                c0 = k0 % Q
-                mm(acc[k0][n][:, a, :], dz2_q[i], s, att_q[i, k0 // Q], c0, c0 + k1 - k0, i + a == 0, i + a == per)
+                n, a = divmod(s, 2)
+                mm(acc[x][n][:, a, :], dz2_q[i], s, att_q[i, x], 0, Q, i + a == 0, i + a == 2)
 
-        def round_dz1(copy, k0, k1, n):
-            per = J // len(acc[k0])
-            dst = dz1[k0 // G][:, per * n : per * (n + 1), :].rearrange("p s (u w e) -> p s u w e", u=2, e=2)
-            copy(
-                out=dst[:, :, :, k0 % G // J : (k0 % G + k1 - k0) // J],
-                in_=acc[k0][n][:].rearrange("p s (w u e) -> p s u w e", u=2, e=2),
-            )
+        def stage1_last(z):
+            for s in range(J):
+                n, a = divmod(s, 2)
+                mm(acc[3][n][:, a, P * z : P * (z + 1)], dz2_q[1], s, att_q[1, 3], P * z, P * (z + 1), False, z + a == 2)
+
+        def round_dz1(copy, x, n):
+            dst = dz1[x // 2][:, 2 * n : 2 * n + 2, :].rearrange("p s (u x w e) -> p x s u w e", u=2, x=2, e=2)
+            copy(out=dst[:, x % 2], in_=acc[x][n][:].rearrange("p s (w u e) -> p s u w e", u=2, e=2))
 
         def turn(hf, s0, s1, bank):
             t = psum.tile([P, s1 - s0, 2, P], F32, name=bank)
@@ -277,9 +274,9 @@ def tile_semanticgraph_pb_v_kernel(tc, q, k, h, cooccur, wv, bv, p, y, grad_out,
         def close1(s):
             mm(bank1[s][:], dv_q[1], s, h_q[1], 0, D, False, True)
 
-        def finish1(copy, s, queue):
+        def finish1(copy, s):
             copy(out=o1[:, s, :], in_=bank1[s][:])
-            queue.dma_start(out=rows(out_1, 0, 0, D)[:, s : s + 1, :], in_=o1[:, s : s + 1, :])
+            nc.sync.dma_start(out=rows(out_1, 0, 0, D)[:, s : s + 1, :], in_=o1[:, s : s + 1, :])
 
         positive(0)
         for c0 in range(0, D, Q):
@@ -292,6 +289,7 @@ def tile_semanticgraph_pb_v_kernel(tc, q, k, h, cooccur, wv, bv, p, y, grad_out,
         quantize(dz2_q[0], E5M2, dz2_g[0], 0, D)
         sort(vcopy, 1, Q, D)
         quantize(dz2_q[1], E5M2, dz2_g[1], 0, D)
+
         stage_c(1, 0, "b4")
         stage_c(1, 1, "b5")
         add_att(0, 0, Q)
@@ -299,16 +297,17 @@ def tile_semanticgraph_pb_v_kernel(tc, q, k, h, cooccur, wv, bv, p, y, grad_out,
         quantize_att(0, 0, Q)
         add_att_shared(1, 0)
         quantize_att(0, Q, G)
-        stage1(0, 0, Q, ("b0", "b1"))
-        stage1(0, Q, G, ("b2", "b3"))
+        stage1(0, 0, ("b0", "b1"))
+        stage1(0, 1, ("b2", "b3"))
         quantize_att(1, 0, Q)
-        stage1(1, 0, Q)
+        stage1(1, 0)
         add_att_shared(1, 1)
-        round_dz1(scopy, 0, Q, 0)
-        round_dz1(scopy, 0, Q, 1)
+        round_dz1(scopy, 0, 0)
+        round_dz1(scopy, 0, 1)
         interleave(vcopy, wv_g, wv_raw, 0, P)
         quantize_att(1, Q, G)
-        stage1(1, Q, G)
+        stage1(1, 1)
+
         stage_c(0, 2, "b4")
         stage_c(0, 3, "b0")
         interleave(vcopy, wv_g, wv_raw, P, D)
@@ -316,8 +315,8 @@ def tile_semanticgraph_pb_v_kernel(tc, q, k, h, cooccur, wv, bv, p, y, grad_out,
         group_dk(vcopy, 0, 1)
         quantize(wv_q, E4M3, wv_g, 0, Q)
         add_att_shared(0, 2)
-        round_dz1(scopy, Q, G, 0)
-        round_dz1(scopy, Q, G, 1)
+        round_dz1(scopy, 1, 0)
+        round_dz1(scopy, 1, 1)
         turn(0, 0, 2, "b5")
         stage_c(1, 2, "b7")
         turn(0, 2, 4, "b6")
@@ -325,65 +324,64 @@ def tile_semanticgraph_pb_v_kernel(tc, q, k, h, cooccur, wv, bv, p, y, grad_out,
         group_dk(vcopy, 1, 1)
         group_dk(scopy, 1, 0)
         quantize_att(0, G, G + Q)
-        stage1(0, G, G + Q, ("b2", "b3"))
+        stage1(0, 2, ("b2", "b3"))
         quantize_dk_first(1)
         product0(0, 2, "b4")
         product0(0, 3, "b1")
         group_dv(scopy, 0, 0, 2)
         group_dv(scopy, 0, 2, 4)
         add_att_shared(1, 2)
-        quantize_dk_first(0)
+        quantize_dv(0, 0, 2)
         quantize_att(1, G, G + Q)
-        stage1(1, G, G + Q)
+        stage1(1, 2)
         interleave(scopy, h_g[0], h_raw[0], 0, D - P)
         interleave_gpsimd(att_g[1, 2], h_raw[0], D - P, D)
+        quantize_dk_first(0)
         residual(0, 2)
         add_att_shared(0, 3)
-        round_dz1(scopy, G, G + Q, 0)
-        round_dz1(scopy, G, G + Q, 1)
+        round_dz1(scopy, 2, 0)
+        round_dz1(scopy, 2, 1)
         product0(0, 0, "b2")
         product0(0, 1, "b0")
         group_dk_tiles(scopy, 0, 2)
+
         add_att(1, G + Q, N - P)
         quantize_att(0, G + Q, N)
-        stage1(0, G + Q, N - P, ("b7",))
-        stage1(0, N - P, N, ("b4", "b5"))
-        add_att(1, N - P, N)
+        stage1(0, 3, ("b7", "b4"))
         quantize_att(1, G + Q, N - P)
-        stage1(1, G + Q, N - P)
-        quantize(h_q[0], E4M3, att_g[1, 2], D - P, D, 0)
-        quantize_att(1, N - P, N)
-        stage1(1, N - P, N)
-        interleave(scopy, h_g[1], h_raw[1], 0, P)
-        quantize_dv(0, 0, 2)
+        stage1_last(0)
+        add_att(1, N - P, N)
         quantize(h_q[0], E4M3, h_g[0], 0, D - P)
-        quantize_dk(0, 2)
-        interleave_gpsimd(dk_g, h_raw[1], Q, D)
-        open1(0, "b3")
-        product0(1, 0, "b6")
-        round_dz1(scopy, G + Q, N - P, 0)
-        round_dz1(scopy, N - P, N, 0)
-        round_dz1(scopy, N - P, N, 1)
-        interleave(scopy, h_g[1], h_raw[1], P, Q)
+        quantize_att(1, N - P, N)
+        stage1_last(1)
+
         residual(0, 3)
         store0(0, 2, 4)
+        quantize_dk(0, 2)
+        interleave_gpsimd(dk_g, h_raw[1], Q, D)
+        quantize(h_q[0], E4M3, att_g[1, 2], D - P, D, 0)
+        product0(1, 0, "b6")
+        open1(0, "b3")
+        interleave(scopy, h_g[1], h_raw[1], 0, P)
+        round_dz1(scopy, 3, 0)
+        interleave(scopy, h_g[1], h_raw[1], P, Q)
+        round_dz1(scopy, 3, 1)
         finish0(0, 0)
         finish0(0, 1)
+        turn(1, 0, 1, "b5")
+        turn(1, 1, 2, "b7")
         product0(1, 1, "b1")
-        turn(1, 0, 1, "b7")
-        turn(1, 1, 2, "b4")
-        turn(1, 2, 4, "b5")
+        turn(1, 2, 4, "b4")
         open1(1, "b2")
         group_dv(scopy, 1, 0, 1)
         group_dv(scopy, 1, 1, 2)
         finish0(1, 0)
-        quantize(h_q[1], E4M3, dk_g, Q, D, 0)
         quantize(h_q[1], E4M3, h_g[1], 0, Q)
+        quantize(h_q[1], E4M3, dk_g, Q, D, 0)
         quantize_dv(1, 0, 1)
         close1(0)
-        group_dv(scopy, 1, 2, 4)
         group_dk_tiles(scopy, 2, 3)
-        group_dk_tiles(scopy, 3, 4)
+        group_dv(scopy, 1, 2, 4)
         quantize_dv(1, 1, 2)
         close1(1)
         finish0(1, 1)
@@ -392,14 +390,15 @@ def tile_semanticgraph_pb_v_kernel(tc, q, k, h, cooccur, wv, bv, p, y, grad_out,
         quantize_dv(0, 2, 4)
         open1(2, "b6")
         open1(3, "b7")
+        finish1(scopy, 0)
         quantize_dv(1, 2, 4)
-        finish1(scopy, 0, nc.sync)
         close1(2)
-        quantize_dk(3, 4)
-        product0(1, 3, "b4")
         close1(3)
-        finish1(scopy, 1, nc.sync)
+        group_dk_tiles(vcopy, 3, 4)
+        finish1(scopy, 1)
         finish0(1, 2)
-        finish1(scopy, 2, nc.sync)
+        quantize_dk(3, 4)
+        product0(1, 3, "b5")
+        finish1(scopy, 2)
+        finish1(vcopy, 3)
         finish0(1, 3)
-        finish1(scopy, 3, nc.scalar)

from contextlib import ExitStack

import concourse.mybir as mybir
from concourse.masks import make_identity

N = 1024
D = 512
P = 128
J = 4
G = P * J
Q = G // 2
ADD_VECTOR = 216

F32 = mybir.dt.float32
BF16 = mybir.dt.bfloat16
U32 = mybir.dt.uint32
U8 = mybir.dt.uint8
E4M3 = mybir.dt.float8_e4m3fn_x4
E5M2 = mybir.dt.float8_e5m2_x4
ALU = mybir.AluOpType

FLOPS = 2 * N * N * D + 2 * 2 * N * D * D
BYTES = N * D * 2 * 2 + N * N * 2 + D * D * 2 + N * N * 4 + N * D * 4 + N * D * 4 + D * D * 4


def tile_semanticgraph_pb_v_kernel(tc, q, k, h, cooccur, wv, bv, p, y, grad_out, out_0, out_1):
    nc = tc.nc
    with ExitStack() as ctx:
        keep = ctx.enter_context(tc.tile_pool(name="keep", bufs=1))
        psum = ctx.enter_context(tc.psum_pool(name="psum", bufs=1))

        def sb(shape, dtype, name):
            return keep.tile(shape, dtype, name=name, align_bytes=256)

        ctx.enter_context(tc.manual_schedule())

        def load(ap, shape, dtype, name):
            t = sb(shape, dtype, name)
            nc.sync.dma_start(out=t[:], in_=ap)
            return t

        def rows(ap, i, c0, c1):
            return ap[G * i : G * (i + 1), c0:c1].rearrange("(p j) w -> p j w", j=J)

        def tiles(ap, t0, t1):
            return ap[G + P * t0 : G + P * t1, :].rearrange("(t p) w -> p t w", p=P)

        g_raw, y_raw, p_raw, c_raw, h_raw = {}, {}, {}, {}, {}

        def load_yg(i):
            y_raw[i] = load(rows(y, i, 0, D), [P, J, D], F32, f"y_{i}")
            g_raw[i] = load(rows(grad_out, i, 0, D), [P, J, D], BF16, f"g_{i}")

        def load_c(i, hf):
            c_raw[i, hf] = load(rows(cooccur, i, G * hf, G * (hf + 1)), [P, J, G], BF16, f"c_{i}{hf}")

        def load_p(i, k0, k1):
            t = load(rows(p, i, k0, k1), [P, J, k1 - k0], F32, f"p_{i}_{k0}")
            for a in range(k0, k1, P):
                p_raw[i, a] = t[:, :, a - k0 :]

        def load_h(hf):
            h_raw[hf] = load(rows(h, hf, 0, D), [P, J, D], BF16, f"h_raw{hf}")

        load_yg(0)
        load_yg(1)
        load_c(0, 0)
        load_p(0, 0, G)
        load_c(1, 0)
        load_p(1, 0, Q)
        load_p(1, Q, G)
        wv_raw = load(rows(wv, 0, 0, D), [P, J, D], BF16, "wv_raw")
        load_c(0, 1)
        load_p(0, G, G + Q)
        load_c(1, 1)
        load_p(1, G, G + Q)
        load_h(0)
        load_p(0, G + Q, N)
        load_p(1, G + Q, N - P)
        load_p(1, N - P, N)
        load_h(1)
        g_tiles = [load(tiles(grad_out, 2 * x, 2 * x + 2), [P, 2, D], BF16, f"g_tiles{x}") for x in range(2)]

        ident = sb([P, P], F32, "ident")
        make_identity(nc, ident[:])
        ident_bf = sb([P, P], BF16, "ident_bf")
        make_identity(nc, ident_bf[:])

        def operand(width, name):
            return (sb([P, width], U32, name + "_codes"), sb([P, width], U8, name + "_scales"))

        def quantize(op, fmt, grouped, c0, c1, at=None):
            codes, scales = op
            g0 = c0 if at is None else at
            nc.vector.quantize_mx(
                out=codes[:, c0:c1].bitcast(fmt), scales=scales[:, c0:c1], in_=grouped[:, J * g0 : J * (g0 + c1 - c0)]
            )

        step = [sb([P, J, D], BF16, f"step_{i}") for i in range(2)]
        dz2 = [sb([P, J, D], BF16, f"dz2_{i}") for i in range(2)]
        dz2_g = [sb([P, D * J], BF16, f"dz2_g{i}") for i in range(2)]
        dz2_q = [operand(D, f"dz2_q{i}") for i in range(2)]
        att_q = {(i, x): operand(Q, f"att_q{i}{x}") for i in range(2) for x in range(4)}
        wv_q = operand(D, "wv_q")
        h_g = [sb([P, D * J], BF16, f"h_g{hf}") for hf in range(2)]
        h_q = [operand(D, f"h_q{hf}") for hf in range(2)]
        dz1 = [sb([P, J, G], BF16, f"dz1_{hf}") for hf in range(2)]
        dk_q = [operand(G, f"dk_q{hf}") for hf in range(2)]
        dv_g = [sb([P, D * J], BF16, f"dv_g{hf}") for hf in range(2)]
        dv_q = [operand(D, f"dv_q{hf}") for hf in range(2)]
        o0 = [sb([P, J, D], F32, f"o0_{hf}") for hf in range(2)]
        o1 = sb([P, J, D], F32, "o1")
        dk_g = sb([P, G * J], BF16, "dk_g")
        att_g = {block: sb([P, Q * J], BF16, f"att_g{block[0]}{block[1]}")[:] for block in ((0, 1), (0, 3), (1, 3))}
        lead = J * ADD_VECTOR
        share_att = sb([P, 2 * lead + J * Q], BF16, "share_att")
        for n, block in enumerate(((1, 1), (1, 0), (0, 0))):
            att_g[block] = share_att[:, lead * n : lead * n + J * Q]
        share_wv = sb([P, lead + J * D], BF16, "share_wv")
        att_g[0, 2], wv_g = share_wv[:, : J * Q], share_wv[:, lead:]
        share_dk = sb([P, lead + J * Q], BF16, "share_dk")
        att_g[1, 2] = share_dk[:, : J * Q]
        dk_first = [sb([P, J * Q], BF16, "dk_first0")[:], share_dk[:, lead:]]
        c_bank = {}
        vcopy, scopy = nc.vector.tensor_copy, nc.scalar.copy

        def positive(i):
            nc.vector.tensor_scalar(out=step[i][:], in0=y_raw[i][:], scalar1=0.0, scalar2=None, op0=ALU.is_gt)

        def mask(i, c0, c1):
            nc.vector.tensor_tensor(
                out=dz2[i][:, :, c0:c1], in0=step[i][:, :, c0:c1], in1=g_raw[i][:, :, c0:c1], op=ALU.mult
            )

        def sort(copy, i, c0, c1):
            copy(
                out=dz2_g[i][:].rearrange("p (s m j) -> p m j s", s=J, j=J)[:, c0 // J : c1 // J],
                in_=dz2[i][:, :, c0:c1].rearrange("p j (m s) -> p m j s", s=J),
            )

        def walk(ap):
            return ap.rearrange("p j (c a) -> p c j a", a=2)

        def grouped(ap):
            return ap.rearrange("p (c a j) -> p c j a", a=2, j=J)

        def c_cols(i, k0, k1):
            return c_raw[i, k0 // G][:, :, k0 % G : k0 % G + k1 - k0]

        def add_att(i, k0, k1):
            out = att_g[i, k0 // Q][:, J * (k0 % Q) : J * (k0 % Q + k1 - k0)]
            nc.vector.tensor_tensor(
                out=grouped(out), in0=walk(p_raw[i, k0][:, :, : k1 - k0]), in1=walk(c_cols(i, k0, k1)), op=ALU.add
            )

        def stage_c(i, x, bank):
            c_bank[i, x] = psum.tile([P, J, ADD_VECTOR], BF16, name=bank)
            src = c_cols(i, Q * x, Q * x + ADD_VECTOR)
            for j in range(0, J, 2):
                nc.tensor.matmul(c_bank[i, x][:, j : j + 2, :], ident_bf[:], src[:, j : j + 2, :], start=True, stop=True)

        def add_att_shared(i, x):
            n = ADD_VECTOR
            shares = ((nc.vector, 0, n, c_bank[i, x][:]), (nc.gpsimd, n, Q, c_cols(i, Q * x + n, Q * (x + 1))))
            for engine, a, b, c in shares:
                engine.tensor_tensor(
                    out=grouped(att_g[i, x][:, J * a : J * b]),
                    in0=walk(p_raw[i, Q * x][:, :, a:b]),
                    in1=walk(c),
                    op=ALU.add,
                )

        def interleave(copy, dst, src, c0, c1):
            copy(out=grouped(dst[:, J * c0 : J * c1]), in_=walk(src[:, :, c0:c1]))

        def interleave_gpsimd(dst, src, c0, c1):
            nc.gpsimd.tensor_scalar(
                out=dst[:, : J * (c1 - c0)].rearrange("p (c j) -> p c j", j=J),
                in0=src[:, :, c0:c1].rearrange("p j c -> p c j"),
                scalar1=1.0,
                scalar2=0.0,
                op0=ALU.mult,
                op1=ALU.add,
            )

        def quantize_att(i, k0, k1):
            quantize(att_q[i, k0 // Q], E4M3, att_g[i, k0 // Q], k0 % Q, k0 % Q + k1 - k0)

        def mm(out, stationary, tile, moving, c0, c1, start, stop):
            nc.tensor.matmul_mx(
                out=out,
                lhsT=stationary[0][:, P * tile : P * (tile + 1)].bitcast(E5M2),
                lhsT_scale=stationary[1][:, P * tile : P * (tile + 1)],
                rhs=moving[0][:, c0:c1].bitcast(E4M3),
                rhs_scale=moving[1][:, c0:c1],
                start=start,
                stop=stop,
            )

        acc, turned, bank0, bank1 = {}, {}, {}, {}

        def stage1(i, x, banks=None):
            if i == 0:
                acc[x] = [psum.tile([P, 2, Q], F32, name=bank) for bank in banks]
            for s in range(J):
                n, a = divmod(s, 2)
                mm(acc[x][n][:, a, :], dz2_q[i], s, att_q[i, x], 0, Q, i + a == 0, i + a == 2)

        def stage1_last(z):
            for s in range(J):
                n, a = divmod(s, 2)
                mm(acc[3][n][:, a, P * z : P * (z + 1)], dz2_q[1], s, att_q[1, 3], P * z, P * (z + 1), False, z + a == 2)

        def round_dz1(copy, x, n):
            dst = dz1[x // 2][:, 2 * n : 2 * n + 2, :].rearrange("p s (u x w e) -> p x s u w e", u=2, x=2, e=2)
            copy(out=dst[:, x % 2], in_=acc[x][n][:].rearrange("p s (w u e) -> p s u w e", u=2, e=2))

        def turn(hf, s0, s1, bank):
            t = psum.tile([P, s1 - s0, 2, P], F32, name=bank)
            for s in range(s0, s1):
                turned[hf, s] = t[:, s - s0 :]
                words = dz1[hf][:, s, :].bitcast(F32)
                for u in range(2):
                    nc.tensor.transpose(t[:, s - s0, u, :], words[:, P * u : P * (u + 1)], ident[:])

        def group_dv(copy, hf, s0, s1):
            copy(
                out=dv_g[hf][:, G * s0 : G * s1].bitcast(F32).rearrange("p (s m u) -> p s m u", m=P, u=2),
                in_=turned[hf, s0][:, : s1 - s0].rearrange("p s u m -> p s m u"),
            )

        def group_dk(copy, x, u):
            copy(
                out=dk_first[u].rearrange("p (e x a b s) -> p x e a s b", e=2, x=2, b=2, s=J)[:, x],
                in_=dz1[0][:, :, Q * u : Q * (u + 1)].rearrange("p s (x a b e) -> p x e a s b", x=2, b=2, e=2)[:, x],
            )

        def group_dk_tiles(copy, t0, t1):
            w0, w1 = P * t0 // J, P * t1 // J
            copy(
                out=dk_g[:, G * t0 : G * t1].rearrange("p (w u e s) -> p u w s e", u=2, e=2, s=J),
                in_=dz1[1][:].rearrange("p s (u w e) -> p u w s e", u=2, e=2)[:, :, w0:w1],
            )

        def quantize_dk_first(u):
            quantize(dk_q[0], E5M2, dk_first[u], Q * u, Q * (u + 1), 0)

        def quantize_dk(t0, t1):
            quantize(dk_q[1], E5M2, dk_g, P * t0, P * t1)

        def quantize_dv(hf, s0, s1):
            quantize(dv_q[hf], E5M2, dv_g[hf], P * s0, P * s1)

        def product0(hf, t, bank):
            bank0[hf, t] = psum.tile([P, D], F32, name=bank)
            mm(bank0[hf, t][:], dk_q[hf], t, wv_q, 0, D, True, True)

        def residual(hf, t):
            g_tile = g_raw[0][:, t, :] if hf == 0 else g_tiles[t // 2][:, t % 2, :]
            nc.vector.tensor_tensor(out=o0[hf][:, t, :], in0=bank0[hf, t][:], in1=g_tile, op=ALU.add)

        def store0(hf, t0, t1):
            dst = rows(out_0, 0, 0, D)[:, t0:t1, :] if hf == 0 else tiles(out_0, t0, t1)
            nc.sync.dma_start(out=dst, in_=o0[hf][:, t0:t1, :])

        def finish0(hf, t):
            residual(hf, t)
            store0(hf, t, t + 1)

        def open1(s, bank):
            bank1[s] = psum.tile([P, D], F32, name=bank)
            mm(bank1[s][:], dv_q[0], s, h_q[0], 0, D, True, False)

        def close1(s):
            mm(bank1[s][:], dv_q[1], s, h_q[1], 0, D, False, True)

        def finish1(copy, s):
            copy(out=o1[:, s, :], in_=bank1[s][:])
            nc.sync.dma_start(out=rows(out_1, 0, 0, D)[:, s : s + 1, :], in_=o1[:, s : s + 1, :])

        positive(0)
        for c0 in range(0, D, Q):
            mask(0, c0, c0 + Q)
            sort(scopy, 0, c0, c0 + Q)
        positive(1)
        mask(1, 0, Q)
        sort(scopy, 1, 0, Q)
        mask(1, Q, D)
        quantize(dz2_q[0], E5M2, dz2_g[0], 0, D)
        sort(vcopy, 1, Q, D)
        quantize(dz2_q[1], E5M2, dz2_g[1], 0, D)

        stage_c(1, 0, "b4")
        stage_c(1, 1, "b5")
        add_att(0, 0, Q)
        add_att(0, Q, G)
        quantize_att(0, 0, Q)
        add_att_shared(1, 0)
        quantize_att(0, Q, G)
        stage1(0, 0, ("b0", "b1"))
        stage1(0, 1, ("b2", "b3"))
        quantize_att(1, 0, Q)
        stage1(1, 0)
        add_att_shared(1, 1)
        round_dz1(scopy, 0, 0)
        round_dz1(scopy, 0, 1)
        interleave(vcopy, wv_g, wv_raw, 0, P)
        quantize_att(1, Q, G)
        stage1(1, 1)

        stage_c(0, 2, "b4")
        stage_c(0, 3, "b0")
        interleave(vcopy, wv_g, wv_raw, P, D)
        group_dk(scopy, 0, 0)
        group_dk(vcopy, 0, 1)
        quantize(wv_q, E4M3, wv_g, 0, Q)
        add_att_shared(0, 2)
        round_dz1(scopy, 1, 0)
        round_dz1(scopy, 1, 1)
        turn(0, 0, 2, "b5")
        stage_c(1, 2, "b7")
        turn(0, 2, 4, "b6")
        quantize(wv_q, E4M3, wv_g, Q, D)
        group_dk(vcopy, 1, 1)
        group_dk(scopy, 1, 0)
        quantize_att(0, G, G + Q)
        stage1(0, 2, ("b2", "b3"))
        quantize_dk_first(1)
        product0(0, 2, "b4")
        product0(0, 3, "b1")
        group_dv(scopy, 0, 0, 2)
        group_dv(scopy, 0, 2, 4)
        add_att_shared(1, 2)
        quantize_dv(0, 0, 2)
        quantize_att(1, G, G + Q)
        stage1(1, 2)
        interleave(scopy, h_g[0], h_raw[0], 0, D - P)
        interleave_gpsimd(att_g[1, 2], h_raw[0], D - P, D)
        quantize_dk_first(0)
        residual(0, 2)
        add_att_shared(0, 3)
        round_dz1(scopy, 2, 0)
        round_dz1(scopy, 2, 1)
        product0(0, 0, "b2")
        product0(0, 1, "b0")
        group_dk_tiles(scopy, 0, 2)

        add_att(1, G + Q, N - P)
        quantize_att(0, G + Q, N)
        stage1(0, 3, ("b7", "b4"))
        quantize_att(1, G + Q, N - P)
        stage1_last(0)
        add_att(1, N - P, N)
        quantize(h_q[0], E4M3, h_g[0], 0, D - P)
        quantize_att(1, N - P, N)
        stage1_last(1)

        residual(0, 3)
        store0(0, 2, 4)
        quantize_dk(0, 2)
        interleave_gpsimd(dk_g, h_raw[1], Q, D)
        quantize(h_q[0], E4M3, att_g[1, 2], D - P, D, 0)
        product0(1, 0, "b6")
        open1(0, "b3")
        interleave(scopy, h_g[1], h_raw[1], 0, P)
        round_dz1(scopy, 3, 0)
        interleave(scopy, h_g[1], h_raw[1], P, Q)
        round_dz1(scopy, 3, 1)
        finish0(0, 0)
        finish0(0, 1)
        turn(1, 0, 1, "b5")
        turn(1, 1, 2, "b7")
        product0(1, 1, "b1")
        turn(1, 2, 4, "b4")
        open1(1, "b2")
        group_dv(scopy, 1, 0, 1)
        group_dv(scopy, 1, 1, 2)
        finish0(1, 0)
        quantize(h_q[1], E4M3, h_g[1], 0, Q)
        quantize(h_q[1], E4M3, dk_g, Q, D, 0)
        quantize_dv(1, 0, 1)
        close1(0)
        group_dk_tiles(scopy, 2, 3)
        group_dv(scopy, 1, 2, 4)
        quantize_dv(1, 1, 2)
        close1(1)
        finish0(1, 1)
        quantize_dk(2, 3)
        product0(1, 2, "b0")
        quantize_dv(0, 2, 4)
        open1(2, "b6")
        open1(3, "b7")
        finish1(scopy, 0)
        quantize_dv(1, 2, 4)
        close1(2)
        close1(3)
        group_dk_tiles(vcopy, 3, 4)
        finish1(scopy, 1)
        finish0(1, 2)
        quantize_dk(3, 4)
        product0(1, 3, "b5")
        finish1(scopy, 2)
        finish1(vcopy, 3)
        finish0(1, 3)
